import numpy as np
import ml_dtypes


def mxq(x, axis, fmt="e4m3"):
    dtype, down = {"e4m3": (ml_dtypes.float8_e4m3fn, 7), "e5m2": (ml_dtypes.float8_e5m2, 14)}[fmt]
    v = np.moveaxis(np.asarray(x, np.float32).astype(ml_dtypes.bfloat16).astype(np.float64), axis, -1)
    blocks = v.reshape(v.shape[:-1] + (-1, 32))
    amax = np.abs(blocks).max(-1, keepdims=True)
    byte = np.maximum(np.where(amax > 0, np.frexp(amax)[1] - 1 + 127, 0) - down, 1)
    scale = np.exp2(byte - 127.0)
    codes = (blocks / scale).astype(np.float32).astype(dtype).astype(np.float64)
    return np.moveaxis((codes * scale).reshape(v.shape), -1, axis)


WIDE = False


def mx_kscale(k):
    if not WIDE:
        return np.ones(k)
    levels = np.array([10, -10, 5, -5, 0])
    a = np.random.permutation(np.resize(levels, k // 512 * 4)).reshape(k // 512, 4)
    idx = np.arange(k)
    return np.exp2(a[idx // 512, idx % 128 // 32])


BF16 = ml_dtypes.bfloat16


def bf(x):
    return np.asarray(x, np.float32).astype(BF16)


def f64(x):
    return np.asarray(x).astype(np.float64)


E2M1 = np.array([0.0, 0.5, 1.0, 1.5, 2.0, 3.0, 4.0, 6.0, -0.0, -0.5, -1.0, -1.5, -2.0, -3.0, -4.0, -6.0])


def pack_weight(w, fmt):
    k, n = w.shape
    w = f64(bf(w)).reshape(k // 32, 32, n)
    amax = np.abs(w).max(1)
    if fmt == "e4m3":
        byte = np.frexp(amax)[1] - 1 + 127 - 7
    else:
        mant, ex = np.frexp(amax / 6.0)
        byte = np.where(mant > 0.5, ex, ex - 1) + 127
    byte = np.clip(np.where(amax > 0, byte, 1), 1, 254)
    scaled = (w * np.exp2(127.0 - byte)[:, None, :]).reshape(k, n).astype(np.float32)
    by_word = np.ascontiguousarray(scaled.reshape(k // 512, 128, 4, n).transpose(0, 1, 3, 2))
    if fmt == "e4m3":
        words = by_word.astype(ml_dtypes.float8_e4m3fn).view(np.uint8)
    else:
        c = by_word.astype(ml_dtypes.float4_e2m1fn).view(np.uint8) & 0xF
        words = c[..., 0::2] | (c[..., 1::2] << 4)
    return np.ascontiguousarray(words), np.ascontiguousarray(byte.astype(np.uint8).reshape(k // 512, 16, n))


def unpack_weight(words, scales, fmt):
    g, p, n, _ = words.shape
    if fmt == "e4m3":
        vals = np.ascontiguousarray(words).view(ml_dtypes.float8_e4m3fn).astype(np.float64)
    else:
        nib = np.empty((g, p, n, 4), np.uint8)
        nib[..., 0::2] = words & 0xF
        nib[..., 1::2] = words >> 4
        vals = E2M1[nib]
    vals = vals * np.repeat(np.exp2(scales.astype(np.float64) - 127.0), 8, axis=1)[..., None]
    return vals.transpose(0, 1, 3, 2).reshape(g * 512, n)


N, M, C, C0, C1 = 128, 2, 128, 2048, 4096
EPS = 1e-3


def bn_relu(y, gamma, beta):
    mean = y.mean(axis=(0, 1))
    var = y.var(axis=(0, 1))
    return np.maximum((y - mean) * (1.0 / np.sqrt(var + EPS)) * gamma + beta, 0.0)


def setup_inputs():
    t = mx_kscale(C0)
    r0 = 0.05 * 4.0 ** np.random.random(C0)
    voxel_feats = bf(np.random.standard_normal((N, M, C)) + 0.5 * np.random.standard_normal(C))
    W0 = bf(np.random.standard_normal((C0, C)) / np.sqrt(C) * r0[:, None])
    gamma0 = bf((1.0 + 0.1 * np.random.standard_normal(C0)) * t)
    beta0 = bf(0.2 * np.random.standard_normal(C0) * t)
    W1 = np.random.standard_normal((C1, 2 * C0)) * 0.2 / np.sqrt(2 * C0) / np.concatenate([t, t])[None, :]
    W1_words, W1_scales = pack_weight(np.ascontiguousarray(W1.T), "e4m3")
    gamma1 = bf(1.0 + 0.1 * np.random.standard_normal(C1))
    beta1 = bf(0.3 * np.random.standard_normal(C1) - 0.5)
    return {"voxel_feats": voxel_feats,
            "W0": W0,
            "gamma0": gamma0,
            "beta0": beta0,
            "W1_words": W1_words,
            "W1_scales": W1_scales,
            "gamma1": gamma1,
            "beta1": beta1}


def reference(voxel_feats, W0, gamma0, beta0, W1_words, W1_scales, gamma1, beta1):
    y0 = f64(voxel_feats) @ f64(W0).T
    p = bn_relu(y0, f64(gamma0), f64(beta0))
    a = p.max(axis=1, keepdims=True)
    x1 = np.concatenate([mxq(p, 2, "e4m3"), np.broadcast_to(mxq(a, 2, "e4m3"), (N, M, C0))], axis=2)
    y1 = x1 @ unpack_weight(W1_words, W1_scales, "e4m3")
    return bn_relu(y1, f64(gamma1), f64(beta1)).max(axis=1)

@@ -1,0 +1,374 @@
+from contextlib import ExitStack
+
+import concourse.mybir as mybir
+from concourse.masks import make_identity
+
+F32 = mybir.dt.float32
+BF16 = mybir.dt.bfloat16
+I32 = mybir.dt.int32
+U32 = mybir.dt.uint32
+U8 = mybir.dt.uint8
+FP8X4 = mybir.dt.float8_e4m3fn_x4
+ACT = mybir.ActivationFunctionType
+ALU = mybir.AluOpType
+
+P = 128
+NV = 128
+NM = 2
+ROWS = NV * NM
+C0 = 2048
+C1 = 4096
+G0 = C0 // 512
+EPS = 1e-3
+QUAD = 4
+NQ = C1 // (QUAD * P)
+
+PIN = True
+TAILSTEP = 2
+REGROUP_ON_G = ()
+RANGES = (1024, 1024, 1024, 512, 512)
+
+FLOPS = 2 * ROWS * 128 * C0 + 2 * ROWS * 2 * C0 * C1
+
+
+def tile_vfe_w_kernel(tc, voxel_feats, W0, gamma0, beta0, W1_words, W1_scales, gamma1, beta1, out):
+    nc = tc.nc
+    with ExitStack() as ctx:
+        if PIN:
+            ctx.enter_context(tc.manual_schedule())
+        keep = ctx.enter_context(tc.tile_pool(name="keep", bufs=1))
+        work = ctx.enter_context(tc.tile_pool(name="work", bufs=3))
+        psum = ctx.enter_context(tc.psum_pool(name="psum", bufs=1))
+
+        def bank(b, shape, dtype, name):
+            return psum.tile(shape, dtype, name=name, tag="b%d" % b)
+
+        gb = keep.tile([P, P], BF16)
+        nc.vector.memset(gb[:], 0.0)
+        planes = keep.tile([P, 2, C1], U8, align_bytes=64)
+        nc.vector.memset(planes[:].bitcast(I32), 0)
+        ident_bf = keep.tile([P, P], BF16)
+        make_identity(nc, ident_bf[:])
+        ident_f = keep.tile([P, P], F32)
+        make_identity(nc, ident_f[:])
+        zero_t = keep.tile([P, 1], F32)
+        nc.vector.memset(zero_t[:], 0.0)
+        eps_t = keep.tile([P, 1], F32)
+        nc.vector.tensor_scalar(out=eps_t[:], in0=zero_t[:], scalar1=EPS, scalar2=None, op0=ALU.add)
+
+        vox_sb = keep.tile([P, NM, 128], BF16)
+        nc.sync.dma_start(out=vox_sb[:], in_=voxel_feats)
+        w0_sb = keep.tile([P, G0, 4, 128], BF16)
+        w0_view = W0.rearrange("(g p t) c -> p g t c", g=G0, p=P, t=4)
+        for g in range(G0):
+            nc.sync.dma_start(out=w0_sb[:, g], in_=w0_view[:, g])
+        g0_sb = keep.tile([P, G0, 4], BF16)
+        nc.scalar.dma_start(out=g0_sb[:], in_=gamma0.rearrange("(g p t) -> p g t", g=G0, p=P, t=4))
+        b0_sb = keep.tile([P, G0, 4], BF16)
+        nc.scalar.dma_start(out=b0_sb[:], in_=beta0.rearrange("(g p t) -> p g t", g=G0, p=P, t=4))
+        nc.scalar.dma_start(out=gb[0:32, :], in_=gamma1.rearrange("(t p) -> t p", p=P))
+        nc.scalar.dma_start(out=gb[32:64, :], in_=beta1.rearrange("(t p) -> t p", p=P))
+        for h in range(2):
+            for quadrant in range(4):
+                nc.sync.dma_start(
+                    out=planes[32 * quadrant : 32 * quadrant + 16, h, :].bitcast(I32),
+                    in_=W1_scales[4 * h : 4 * h + 4, 4 * quadrant : 4 * quadrant + 4, :].bitcast(I32),
+                )
+        words = {}
+        n_lo = 0
+        for r, width in enumerate(RANGES):
+            order = (0, 1, 2, 3, 4, 5, 6, 7) if r == 0 else (4, 5, 6, 7, 0, 1, 2, 3)
+            for g in order:
+                wt = keep.tile([P, width], I32, name="w_%d_%d" % (r, g), align_bytes=64)
+                nc.sync.dma_start(
+                    out=wt[:],
+                    in_=W1_words[g].rearrange("p n t -> p (n t)")[:, 4 * n_lo : 4 * (n_lo + width)].bitcast(I32),
+                )
+                for c in range(0, width, P):
+                    words[(g, n_lo + c)] = (wt, c)
+            n_lo += width
+
+        xT = keep.tile([P, ROWS], BF16)
+        w0T = keep.tile([P, G0, 4, P], BF16)
+        gb1 = keep.tile([P, 64], F32)
+        st0 = keep.tile([P, G0, 4, 6], F32)
+        mv0 = keep.tile([P, G0, 4, 2], F32)
+        rstd0 = keep.tile([P, G0, 4], F32)
+        s0 = keep.tile([P, G0, 4], F32)
+        ms0 = keep.tile([P, G0, 4], F32)
+        sh0 = keep.tile([P, G0, 4], F32)
+        p_bf = keep.tile([P, G0, 4, ROWS], BF16)
+        grp = keep.tile([P, G0, ROWS, 4], BF16, align_bytes=64)
+        agr = keep.tile([P, G0, NV, 4], BF16, align_bytes=64)
+        p_codes = keep.tile([P, G0, ROWS], U32, align_bytes=64)
+        p_scales = keep.tile([P, G0, ROWS], U8, align_bytes=64)
+        a_codes = keep.tile([P, G0, NV], U32, align_bytes=64)
+        a_scales = keep.tile([P, G0, NV], U8, align_bytes=64)
+
+        xT_ps = bank(6, [P, NM, NV], BF16, "xT_ps")
+        for m in range(NM):
+            nc.tensor.transpose(xT_ps[:, m, :], vox_sb[:, m, :], ident_bf[:])
+        nc.vector.tensor_copy(out=xT[:], in_=xT_ps[:].rearrange("c m v -> c (m v)"))
+
+        wT_bank = (7, 6, 7, 6)
+        y0_bank = ((0, 1), (2, 3), (4, 5), (7, 6))
+        y0 = {}
+
+        def w0_transposes(g):
+            blocks = 5 if g == G0 - 1 else 4
+            wT_ps = bank(wT_bank[g], [P, blocks, P], BF16, "wT_ps")
+            for t in range(4):
+                nc.tensor.transpose(wT_ps[:, t, :], w0_sb[:, g, t, :], ident_bf[:])
+            if g == G0 - 1:
+                nc.tensor.transpose(wT_ps[:, 4, :], gb[:], ident_bf[:])
+            nc.scalar.copy(out=w0T[:, g], in_=wT_ps[:, 0:4, :])
+            if g == G0 - 1:
+                nc.scalar.copy(out=gb1[:], in_=wT_ps[:, 4, 0:64])
+
+        def l0_matmuls(g):
+            for half in range(2):
+                yt = bank(y0_bank[g][half], [P, 2, ROWS], F32, "y0")
+                y0[(g, half)] = yt
+                for u in range(2):
+                    nc.tensor.matmul(out=yt[:, u, :], lhsT=w0T[:, g, 2 * half + u, :], rhs=xT[:], start=True, stop=True)
+
+        def l0_stat(g, t):
+            nc.vector.bn_stats(out=st0[:, g, t, :], in_=y0[(g, t // 2)][:, t % 2, :])
+
+        def l0_aggr(g):
+            for t in range(4):
+                nc.vector.bn_aggr(out=mv0[:, g, t, :], in_=st0[:, g, t, :])
+
+        def l0_rstd(g):
+            nc.scalar.activation(out=rstd0[:, g, :], in_=mv0[:, g, :, 1], func=ACT.Abs_reciprocal_sqrt, bias=eps_t[:])
+
+        def l0_small(g):
+            nc.gpsimd.tensor_tensor(out=s0[:, g, :], in0=rstd0[:, g, :], in1=g0_sb[:, g, :], op=ALU.mult)
+            nc.gpsimd.tensor_tensor(out=ms0[:, g, :], in0=mv0[:, g, :, 0], in1=s0[:, g, :], op=ALU.mult)
+            nc.gpsimd.tensor_tensor(out=sh0[:, g, :], in0=b0_sb[:, g, :], in1=ms0[:, g, :], op=ALU.subtract)
+
+        def l0_act(g, ts):
+            for t in ts:
+                nc.scalar.activation(
+                    out=p_bf[:, g, t, :], in_=y0[(g, t // 2)][:, t % 2, :], func=ACT.Relu,
+                    bias=sh0[:, g, t : t + 1], scale=s0[:, g, t : t + 1],
+                )
+
+        def l0_regroup(g):
+            if g in REGROUP_ON_G:
+                nc.gpsimd.tensor_scalar(
+                    out=grp[:, g], in0=p_bf[:, g].rearrange("p t r -> p r t"),
+                    scalar1=1.0, scalar2=0.0, op0=ALU.mult, op1=ALU.add,
+                )
+            else:
+                nc.vector.tensor_copy(
+                    out=grp[:, g].rearrange("p (c i) t -> p c t i", i=4),
+                    in_=p_bf[:, g].rearrange("p t (c i) -> p c t i", i=4),
+                )
+
+        def l0_quant_p(g):
+            nc.vector.quantize_mx(
+                out=p_codes[:, g, :].bitcast(FP8X4), scales=p_scales[:, g, :],
+                in_=grp[:, g].rearrange("p r t -> p (r t)"),
+            )
+
+        def l0_max(g):
+            nc.vector.tensor_tensor(out=agr[:, g], in0=grp[:, g, 0:NV, :], in1=grp[:, g, NV:ROWS, :], op=ALU.max)
+
+        def l0_quant_a(g):
+            nc.vector.quantize_mx(
+                out=a_codes[:, g, :].bitcast(FP8X4), scales=a_scales[:, g, :],
+                in_=agr[:, g].rearrange("p r t -> p (r t)"),
+            )
+
+        w0_transposes(0)
+        w0_transposes(1)
+        l0_matmuls(0)
+        w0_transposes(2)
+        l0_matmuls(1)
+        for t in range(4):
+            l0_stat(0, t)
+        l0_aggr(0)
+        l0_rstd(0)
+        l0_small(0)
+        w0_transposes(3)
+        l0_matmuls(2)
+        l0_matmuls(3)
+        for g in range(1, G0):
+            for t in range(4):
+                l0_stat(g, t)
+            l0_aggr(g)
+            l0_act(g - 1, (0, 1))
+            l0_rstd(g)
+            l0_small(g)
+            l0_act(g - 1, (2, 3))
+        l0_act(G0 - 1, (0, 1, 2, 3))
+        l0_regroup(0)
+        l0_regroup(1)
+        l0_quant_p(0)
+        l0_regroup(2)
+        l0_quant_p(1)
+        l0_max(0)
+        l0_quant_p(2)
+        l0_regroup(3)
+        l0_max(1)
+        l0_quant_p(3)
+        l0_quant_a(0)
+        l0_max(2)
+        l0_quant_a(1)
+        l0_max(3)
+        l0_quant_a(2)
+        l0_quant_a(3)
+
+        st = {}
+        o_sb = keep.tile([P, C1], F32)
+
+        def mx_pass(acc, g, n0, first, last):
+            j = g % G0
+            top = g < G0
+            wt, c = words[(g, n0)]
+            nc.tensor.matmul_mx(
+                out=acc,
+                lhsT=wt[:, c : c + P].bitcast(FP8X4),
+                lhsT_scale=planes[4 * j : P, 0 if top else 1, n0 : n0 + P],
+                rhs=(p_codes if top else a_codes)[:, j, :].bitcast(FP8X4),
+                rhs_scale=(p_scales if top else a_scales)[:, j, :],
+                start=first, stop=last,
+            )
+
+        def mx_ya(q):
+            ya_ps = bank(q % 2, [P, QUAD, NV], F32, "ya_ps")
+            for i in range(QUAD):
+                for j in range(G0):
+                    mx_pass(ya_ps[:, i, :], G0 + j, (QUAD * q + i) * P, j == 0, j == G0 - 1)
+            st[("ya_ps", q)] = ya_ps
+
+        def s_yacopy(q):
+            ya_sb = work.tile([P, QUAD, NV], F32, name="ya_sb")
+            st[("ya_sb", q)] = ya_sb
+            nc.scalar.copy(out=ya_sb[:], in_=st[("ya_ps", q)][:])
+            st[("y", q)] = work.tile([P, QUAD, NM, NV], F32, name="y")
+            st[("st1", q)] = work.tile([P, QUAD, 6], F32, name="st1")
+            st[("mv1", q)] = work.tile([P, QUAD, 2], F32, name="mv1")
+            st[("rstd1", q)] = work.tile([P, QUAD], F32, name="rstd1")
+            st[("s1", q)] = work.tile([P, QUAD], F32, name="s1")
+            st[("ms1", q)] = work.tile([P, QUAD], F32, name="ms1")
+            st[("sh1", q)] = work.tile([P, QUAD], F32, name="sh1")
+            st[("z", q)] = work.tile([P, QUAD, NM, NV], F32, name="z")
+            st[("zmax", q)] = work.tile([P, QUAD, NV], F32, name="zmax")
+
+        def mx_yp(q, half):
+            yp_ps = bank(2 + 2 * (q % 2) + half, [P, 2, NM, NV], F32, "yp_ps")
+            st[("yp_ps", q, half)] = yp_ps
+            for u in range(2):
+                for j in range(G0):
+                    mx_pass(yp_ps[:, u].rearrange("p m v -> p (m v)"), j, (QUAD * q + 2 * half + u) * P, j == 0, j == G0 - 1)
+
+        def v_add(q, i0, i1, src):
+            nc.vector.tensor_tensor(
+                out=st[("y", q)][:, i0:i1],
+                in0=src,
+                in1=st[("ya_sb", q)][:, i0:i1].unsqueeze(2).to_broadcast([P, i1 - i0, NM, NV]),
+                op=ALU.add,
+            )
+
+        def v_stats(q, i0, i1):
+            for i in range(i0, i1):
+                nc.vector.bn_stats(out=st[("st1", q)][:, i, :], in_=st[("y", q)][:, i].rearrange("p m v -> p (m v)"))
+            for i in range(i0, i1):
+                nc.vector.bn_aggr(out=st[("mv1", q)][:, i, :], in_=st[("st1", q)][:, i, :])
+
+        def small(q, i0, i1):
+            mv1 = st[("mv1", q)]
+            rstd1, s1, ms1, sh1 = st[("rstd1", q)], st[("s1", q)], st[("ms1", q)], st[("sh1", q)]
+            nc.scalar.activation(out=rstd1[:, i0:i1], in_=mv1[:, i0:i1, 1], func=ACT.Abs_reciprocal_sqrt, bias=eps_t[:])
+            t0 = QUAD * q
+            nc.gpsimd.tensor_tensor(out=s1[:, i0:i1], in0=rstd1[:, i0:i1], in1=gb1[:, t0 + i0 : t0 + i1], op=ALU.mult)
+            nc.gpsimd.tensor_tensor(out=ms1[:, i0:i1], in0=mv1[:, i0:i1, 0], in1=s1[:, i0:i1], op=ALU.mult)
+            nc.gpsimd.tensor_tensor(out=sh1[:, i0:i1], in0=gb1[:, 32 + t0 + i0 : 32 + t0 + i1], in1=ms1[:, i0:i1], op=ALU.subtract)
+
+        def s_act(q, i0, i1):
+            for i in range(i0, i1):
+                nc.scalar.activation(
+                    out=st[("z", q)][:, i], in_=st[("y", q)][:, i], func=ACT.Relu,
+                    bias=st[("sh1", q)][:, i : i + 1], scale=st[("s1", q)][:, i : i + 1],
+                )
+
+        def v_max(q, i0, i1):
+            z = st[("z", q)]
+            nc.vector.tensor_tensor(out=st[("zmax", q)][:, i0:i1], in0=z[:, i0:i1, 0, :], in1=z[:, i0:i1, 1, :], op=ALU.max)
+
+        def pe_tr(q, i0, i1):
+            if i0 == 0:
+                st[("tr_ps", q)] = bank(6 + q % 2, [P, QUAD, P], F32, "tr_ps")
+            for i in range(i0, i1):
+                nc.tensor.transpose(st[("tr_ps", q)][:, i, :], st[("zmax", q)][:, i, :], ident_f[:])
+
+        def s_out(q, i0, i1):
+            cols = slice((QUAD * q + i0) * P, (QUAD * q + i1) * P)
+            nc.scalar.copy(out=o_sb[:, cols], in_=st[("tr_ps", q)][:, i0:i1, :].rearrange("v i n -> v (i n)"))
+            nc.sync.dma_start(out=out[:, cols], in_=o_sb[:, cols])
+
+        first_quad = []
+        n_lo = 0
+        for width in RANGES:
+            first_quad.append((n_lo // (QUAD * P), (n_lo + width) // (QUAD * P)))
+            n_lo += width
+        starts = dict(first_quad)
+
+        def add_stats(q, half):
+            v_add(q, 2 * half, 2 * half + 2, st[("yp_ps", q, half)][:])
+            v_stats(q, 2 * half, 2 * half + 2)
+
+        def finish(q):
+            if q >= 0:
+                pe_tr(q, 0, QUAD)
+                s_out(q, 0, QUAD)
+
+        LAST = NQ - 1
+        for q in range(LAST):
+            if q == 0:
+                mx_yp(0, 0)
+                mx_yp(0, 1)
+            if q in starts:
+                for q2 in range(q, starts[q]):
+                    mx_ya(q2)
+            s_yacopy(q)
+            if q >= 1:
+                s_act(q - 1, 0, QUAD)
+                mx_yp(q, 0)
+            add_stats(q, 0)
+            if q >= 1:
+                mx_yp(q, 1)
+            finish(q - 2)
+            add_stats(q, 1)
+            small(q, 0, QUAD)
+            if q >= 1:
+                v_max(q - 1, 0, QUAD)
+
+        q = LAST
+        mx_ya(q)
+        s_yacopy(q)
+        s_act(q - 1, 0, QUAD)
+        accs = [bank(2 + i, [P, NM, NV], F32, "yl_ps") for i in (2, 3, 0, 1)]
+        for j in range(G0):
+            for i in range(QUAD):
+                mx_pass(accs[i][:].rearrange("p m v -> p (m v)"), j, (QUAD * q + i) * P, j == 0, j == G0 - 1)
+            if j == 0:
+                finish(q - 2)
+        v_max(q - 1, 0, QUAD)
+        finish(q - 1)
+        step = TAILSTEP
+        for i0 in range(0, QUAD, step):
+            for i in range(i0, i0 + step):
+                v_add(q, i, i + 1, accs[i][:].unsqueeze(1))
+                v_stats(q, i, i + 1)
+            small(q, i0, i0 + step)
+            s_act(q, i0, i0 + step)
+            if i0 > 0:
+                v_max(q, i0 - step, i0)
+                pe_tr(q, i0 - step, i0)
+                s_out(q, i0 - step, i0)
+        v_max(q, QUAD - step, QUAD)
+        pe_tr(q, QUAD - step, QUAD)
+        s_out(q, QUAD - step, QUAD)

@@ -23,10 +23,11 @@ EPS = 1e-3
 QUAD = 4
 NQ = C1 // (QUAD * P)
 
-PIN = True
-TAILSTEP = 2
 REGROUP_ON_G = ()
 RANGES = (1024, 1024, 1024, 512, 512)
+TR_LAG = 3
+EARLY = True
+WORK_BUFS = 4
 
 FLOPS = 2 * ROWS * 128 * C0 + 2 * ROWS * 2 * C0 * C1
 
@@ -34,15 +35,18 @@ FLOPS = 2 * ROWS * 128 * C0 + 2 * ROWS * 2 * C0 * C1
 def tile_vfe_w_kernel(tc, voxel_feats, W0, gamma0, beta0, W1_words, W1_scales, gamma1, beta1, out):
     nc = tc.nc
     with ExitStack() as ctx:
-        if PIN:
-            ctx.enter_context(tc.manual_schedule())
+        ctx.enter_context(tc.manual_schedule())
         keep = ctx.enter_context(tc.tile_pool(name="keep", bufs=1))
-        work = ctx.enter_context(tc.tile_pool(name="work", bufs=3))
+        work = ctx.enter_context(tc.tile_pool(name="work", bufs=WORK_BUFS))
         psum = ctx.enter_context(tc.psum_pool(name="psum", bufs=1))
 
         def bank(b, shape, dtype, name):
             return psum.tile(shape, dtype, name=name, tag="b%d" % b)
 
+        zero_t = keep.tile([P, 1], F32)
+        nc.vector.memset(zero_t[:], 0.0)
+        eps_t = keep.tile([P, 1], F32)
+        nc.vector.tensor_scalar(out=eps_t[:], in0=zero_t[:], scalar1=EPS, scalar2=None, op0=ALU.add)
         gb = keep.tile([P, P], BF16)
         nc.vector.memset(gb[:], 0.0)
         planes = keep.tile([P, 2, C1], U8, align_bytes=64)
@@ -51,10 +55,6 @@ def tile_vfe_w_kernel(tc, voxel_feats, W0, gamma0, beta0, W1_words, W1_scales, g
         make_identity(nc, ident_bf[:])
         ident_f = keep.tile([P, P], F32)
         make_identity(nc, ident_f[:])
-        zero_t = keep.tile([P, 1], F32)
-        nc.vector.memset(zero_t[:], 0.0)
-        eps_t = keep.tile([P, 1], F32)
-        nc.vector.tensor_scalar(out=eps_t[:], in0=zero_t[:], scalar1=EPS, scalar2=None, op0=ALU.add)
 
         vox_sb = keep.tile([P, NM, 128], BF16)
         nc.sync.dma_start(out=vox_sb[:], in_=voxel_feats)
@@ -62,12 +62,14 @@ def tile_vfe_w_kernel(tc, voxel_feats, W0, gamma0, beta0, W1_words, W1_scales, g
         w0_view = W0.rearrange("(g p t) c -> p g t c", g=G0, p=P, t=4)
         for g in range(G0):
             nc.sync.dma_start(out=w0_sb[:, g], in_=w0_view[:, g])
+        nc.scalar.dma_start(out=gb[0:32, :], in_=gamma1.rearrange("(t p) -> t p", p=P))
+        nc.scalar.dma_start(out=gb[32:64, :], in_=beta1.rearrange("(t p) -> t p", p=P))
         g0_sb = keep.tile([P, G0, 4], BF16)
         nc.scalar.dma_start(out=g0_sb[:], in_=gamma0.rearrange("(g p t) -> p g t", g=G0, p=P, t=4))
         b0_sb = keep.tile([P, G0, 4], BF16)
         nc.scalar.dma_start(out=b0_sb[:], in_=beta0.rearrange("(g p t) -> p g t", g=G0, p=P, t=4))
-        nc.scalar.dma_start(out=gb[0:32, :], in_=gamma1.rearrange("(t p) -> t p", p=P))
-        nc.scalar.dma_start(out=gb[32:64, :], in_=beta1.rearrange("(t p) -> t p", p=P))
+        warm = keep.tile([P, 1], F32)
+        nc.scalar.activation(out=warm[:], in_=eps_t[:], func=ACT.Abs_reciprocal_sqrt)
         for h in range(2):
             for quadrant in range(4):
                 nc.sync.dma_start(
@@ -102,30 +104,30 @@ def tile_vfe_w_kernel(tc, voxel_feats, W0, gamma0, beta0, W1_words, W1_scales, g
         agr = keep.tile([P, G0, NV, 4], BF16, align_bytes=64)
         p_codes = keep.tile([P, G0, ROWS], U32, align_bytes=64)
         p_scales = keep.tile([P, G0, ROWS], U8, align_bytes=64)
-        a_codes = keep.tile([P, G0, NV], U32, align_bytes=64)
-        a_scales = keep.tile([P, G0, NV], U8, align_bytes=64)
+        a_codes = keep.tile([P, G0, NM, NV], U32, align_bytes=64)
+        a_scales = keep.tile([P, G0, NM, NV], U8, align_bytes=64)
 
-        xT_ps = bank(6, [P, NM, NV], BF16, "xT_ps")
+        xT_ps = bank(0, [P, NM, NV], BF16, "xT_ps")
         for m in range(NM):
             nc.tensor.transpose(xT_ps[:, m, :], vox_sb[:, m, :], ident_bf[:])
         nc.vector.tensor_copy(out=xT[:], in_=xT_ps[:].rearrange("c m v -> c (m v)"))
 
-        wT_bank = (7, 6, 7, 6)
-        y0_bank = ((0, 1), (2, 3), (4, 5), (7, 6))
+        y0_bank = ((2, 3), (4, 5), (6, 7), (1, 0))
         y0 = {}
-
-        def w0_transposes(g):
+        for g in range(G0):
             blocks = 5 if g == G0 - 1 else 4
-            wT_ps = bank(wT_bank[g], [P, blocks, P], BF16, "wT_ps")
+            wT_ps = bank(4 + g, [P, blocks, P], BF16, "wT_ps")
             for t in range(4):
                 nc.tensor.transpose(wT_ps[:, t, :], w0_sb[:, g, t, :], ident_bf[:])
             if g == G0 - 1:
                 nc.tensor.transpose(wT_ps[:, 4, :], gb[:], ident_bf[:])
-            nc.scalar.copy(out=w0T[:, g], in_=wT_ps[:, 0:4, :])
+            if g % 2 == 0:
+                nc.scalar.copy(out=w0T[:, g], in_=wT_ps[:, 0:4, :])
+            else:
+                nc.vector.tensor_copy(out=w0T[:, g], in_=wT_ps[:, 0:4, :])
             if g == G0 - 1:
                 nc.scalar.copy(out=gb1[:], in_=wT_ps[:, 4, 0:64])
-
-        def l0_matmuls(g):
+        for g in range(G0):
             for half in range(2):
                 yt = bank(y0_bank[g][half], [P, 2, ROWS], F32, "y0")
                 y0[(g, half)] = yt
@@ -138,17 +140,18 @@ def tile_vfe_w_kernel(tc, voxel_feats, W0, gamma0, beta0, W1_words, W1_scales, g
         def l0_aggr(g):
             for t in range(4):
                 nc.vector.bn_aggr(out=mv0[:, g, t, :], in_=st0[:, g, t, :])
-
-        def l0_rstd(g):
             nc.scalar.activation(out=rstd0[:, g, :], in_=mv0[:, g, :, 1], func=ACT.Abs_reciprocal_sqrt, bias=eps_t[:])
 
-        def l0_small(g):
-            nc.gpsimd.tensor_tensor(out=s0[:, g, :], in0=rstd0[:, g, :], in1=g0_sb[:, g, :], op=ALU.mult)
-            nc.gpsimd.tensor_tensor(out=ms0[:, g, :], in0=mv0[:, g, :, 0], in1=s0[:, g, :], op=ALU.mult)
-            nc.gpsimd.tensor_tensor(out=sh0[:, g, :], in0=b0_sb[:, g, :], in1=ms0[:, g, :], op=ALU.subtract)
+        def l0_small(g, step):
+            if step == 0:
+                nc.vector.tensor_tensor(out=s0[:, g, :], in0=rstd0[:, g, :], in1=g0_sb[:, g, :], op=ALU.mult)
+            elif step == 1:
+                nc.vector.tensor_tensor(out=ms0[:, g, :], in0=mv0[:, g, :, 0], in1=s0[:, g, :], op=ALU.mult)
+            else:
+                nc.vector.tensor_tensor(out=sh0[:, g, :], in0=b0_sb[:, g, :], in1=ms0[:, g, :], op=ALU.subtract)
 
-        def l0_act(g, ts):
-            for t in ts:
+        def l0_act(g):
+            for t in range(4):
                 nc.scalar.activation(
                     out=p_bf[:, g, t, :], in_=y0[(g, t // 2)][:, t % 2, :], func=ACT.Relu,
                     bias=sh0[:, g, t : t + 1], scale=s0[:, g, t : t + 1],
@@ -175,66 +178,44 @@ def tile_vfe_w_kernel(tc, voxel_feats, W0, gamma0, beta0, W1_words, W1_scales, g
         def l0_max(g):
             nc.vector.tensor_tensor(out=agr[:, g], in0=grp[:, g, 0:NV, :], in1=grp[:, g, NV:ROWS, :], op=ALU.max)
 
-        def l0_quant_a(g):
+        def l0_quant_a(g, m):
             nc.vector.quantize_mx(
-                out=a_codes[:, g, :].bitcast(FP8X4), scales=a_scales[:, g, :],
+                out=a_codes[:, g, m, :].bitcast(FP8X4), scales=a_scales[:, g, m, :],
                 in_=agr[:, g].rearrange("p r t -> p (r t)"),
             )
-
-        w0_transposes(0)
-        w0_transposes(1)
-        l0_matmuls(0)
-        w0_transposes(2)
-        l0_matmuls(1)
-        for t in range(4):
-            l0_stat(0, t)
-        l0_aggr(0)
-        l0_rstd(0)
-        l0_small(0)
-        w0_transposes(3)
-        l0_matmuls(2)
-        l0_matmuls(3)
-        for g in range(1, G0):
-            for t in range(4):
-                l0_stat(g, t)
-            l0_aggr(g)
-            l0_act(g - 1, (0, 1))
-            l0_rstd(g)
-            l0_small(g)
-            l0_act(g - 1, (2, 3))
-        l0_act(G0 - 1, (0, 1, 2, 3))
-        l0_regroup(0)
-        l0_regroup(1)
-        l0_quant_p(0)
-        l0_regroup(2)
-        l0_quant_p(1)
-        l0_max(0)
-        l0_quant_p(2)
-        l0_regroup(3)
-        l0_max(1)
-        l0_quant_p(3)
-        l0_quant_a(0)
-        l0_max(2)
-        l0_quant_a(1)
-        l0_max(3)
-        l0_quant_a(2)
-        l0_quant_a(3)
 
         st = {}
         o_sb = keep.tile([P, C1], F32)
 
-        def mx_pass(acc, g, n0, first, last):
+        def mx_pass(acc, g, n0, first, last, both=False):
             j = g % G0
             top = g < G0
             wt, c = words[(g, n0)]
+            if top:
+                rhs, rhs_scale = p_codes[:, j, :], p_scales[:, j, :]
+            elif both:
+                rhs = a_codes[:, j].rearrange("p m v -> p (m v)")
+                rhs_scale = a_scales[:, j].rearrange("p m v -> p (m v)")
+            else:
+                rhs, rhs_scale = a_codes[:, j, 0, :], a_scales[:, j, 0, :]
             nc.tensor.matmul_mx(
                 out=acc,
                 lhsT=wt[:, c : c + P].bitcast(FP8X4),
                 lhsT_scale=planes[4 * j : P, 0 if top else 1, n0 : n0 + P],
-                rhs=(p_codes if top else a_codes)[:, j, :].bitcast(FP8X4),
-                rhs_scale=(p_scales if top else a_scales)[:, j, :],
+                rhs=rhs.bitcast(FP8X4),
+                rhs_scale=rhs_scale,
                 start=first, stop=last,
             )
+
+        def tiles_of(q):
+            st[("y", q)] = work.tile([P, QUAD, NM, NV], F32, name="y")
+            st[("st1", q)] = work.tile([P, QUAD, 6], F32, name="st1")
+            st[("mv1", q)] = work.tile([P, QUAD, 2], F32, name="mv1")
+            st[("rstd1", q)] = work.tile([P, QUAD], F32, name="rstd1")
+            st[("s1", q)] = work.tile([P, QUAD], F32, name="s1")
+            st[("ms1", q)] = work.tile([P, QUAD], F32, name="ms1")
+            st[("sh1", q)] = work.tile([P, QUAD], F32, name="sh1")
+            st[("zmax", q)] = work.tile([P, QUAD, NV], F32, name="zmax")
 
         def mx_ya(q):
             ya_ps = bank(q % 2, [P, QUAD, NV], F32, "ya_ps")
@@ -247,18 +228,10 @@ def tile_vfe_w_kernel(tc, voxel_feats, W0, gamma0, beta0, W1_words, W1_scales, g
             ya_sb = work.tile([P, QUAD, NV], F32, name="ya_sb")
             st[("ya_sb", q)] = ya_sb
             nc.scalar.copy(out=ya_sb[:], in_=st[("ya_ps", q)][:])
-            st[("y", q)] = work.tile([P, QUAD, NM, NV], F32, name="y")
-            st[("st1", q)] = work.tile([P, QUAD, 6], F32, name="st1")
-            st[("mv1", q)] = work.tile([P, QUAD, 2], F32, name="mv1")
-            st[("rstd1", q)] = work.tile([P, QUAD], F32, name="rstd1")
-            st[("s1", q)] = work.tile([P, QUAD], F32, name="s1")
-            st[("ms1", q)] = work.tile([P, QUAD], F32, name="ms1")
-            st[("sh1", q)] = work.tile([P, QUAD], F32, name="sh1")
-            st[("z", q)] = work.tile([P, QUAD, NM, NV], F32, name="z")
-            st[("zmax", q)] = work.tile([P, QUAD, NV], F32, name="zmax")
+            tiles_of(q)
 
-        def mx_yp(q, half):
-            yp_ps = bank(2 + 2 * (q % 2) + half, [P, 2, NM, NV], F32, "yp_ps")
+        def mx_yp(q, half, b):
+            yp_ps = bank(b, [P, 2, NM, NV], F32, "yp_ps")
             st[("yp_ps", q, half)] = yp_ps
             for u in range(2):
                 for j in range(G0):
@@ -272,30 +245,35 @@ def tile_vfe_w_kernel(tc, voxel_feats, W0, gamma0, beta0, W1_words, W1_scales, g
                 op=ALU.add,
             )
 
-        def v_stats(q, i0, i1):
+        def v_stats(q, i0, i1, srcs=None):
             for i in range(i0, i1):
-                nc.vector.bn_stats(out=st[("st1", q)][:, i, :], in_=st[("y", q)][:, i].rearrange("p m v -> p (m v)"))
+                src = st[("y", q)][:, i] if srcs is None else srcs[i][:]
+                nc.vector.bn_stats(out=st[("st1", q)][:, i, :], in_=src.rearrange("p m v -> p (m v)"))
             for i in range(i0, i1):
                 nc.vector.bn_aggr(out=st[("mv1", q)][:, i, :], in_=st[("st1", q)][:, i, :])
 
-        def small(q, i0, i1):
+        def s_rstd(q, i0, i1):
+            nc.scalar.activation(
+                out=st[("rstd1", q)][:, i0:i1], in_=st[("mv1", q)][:, i0:i1, 1], func=ACT.Abs_reciprocal_sqrt, bias=eps_t[:]
+            )
+
+        def small(eng, q, i0, i1):
             mv1 = st[("mv1", q)]
             rstd1, s1, ms1, sh1 = st[("rstd1", q)], st[("s1", q)], st[("ms1", q)], st[("sh1", q)]
-            nc.scalar.activation(out=rstd1[:, i0:i1], in_=mv1[:, i0:i1, 1], func=ACT.Abs_reciprocal_sqrt, bias=eps_t[:])
             t0 = QUAD * q
-            nc.gpsimd.tensor_tensor(out=s1[:, i0:i1], in0=rstd1[:, i0:i1], in1=gb1[:, t0 + i0 : t0 + i1], op=ALU.mult)
-            nc.gpsimd.tensor_tensor(out=ms1[:, i0:i1], in0=mv1[:, i0:i1, 0], in1=s1[:, i0:i1], op=ALU.mult)
-            nc.gpsimd.tensor_tensor(out=sh1[:, i0:i1], in0=gb1[:, 32 + t0 + i0 : 32 + t0 + i1], in1=ms1[:, i0:i1], op=ALU.subtract)
+            eng.tensor_tensor(out=s1[:, i0:i1], in0=rstd1[:, i0:i1], in1=gb1[:, t0 + i0 : t0 + i1], op=ALU.mult)
+            eng.tensor_tensor(out=ms1[:, i0:i1], in0=mv1[:, i0:i1, 0], in1=s1[:, i0:i1], op=ALU.mult)
+            eng.tensor_tensor(out=sh1[:, i0:i1], in0=gb1[:, 32 + t0 + i0 : 32 + t0 + i1], in1=ms1[:, i0:i1], op=ALU.subtract)
 
-        def s_act(q, i0, i1):
+        def s_act(q, i0, i1, srcs=None):
             for i in range(i0, i1):
                 nc.scalar.activation(
-                    out=st[("z", q)][:, i], in_=st[("y", q)][:, i], func=ACT.Relu,
+                    out=st[("y", q)][:, i], in_=(st[("y", q)][:, i] if srcs is None else srcs[i][:]), func=ACT.Relu,
                     bias=st[("sh1", q)][:, i : i + 1], scale=st[("s1", q)][:, i : i + 1],
                 )
 
         def v_max(q, i0, i1):
-            z = st[("z", q)]
+            z = st[("y", q)]
             nc.vector.tensor_tensor(out=st[("zmax", q)][:, i0:i1], in0=z[:, i0:i1, 0, :], in1=z[:, i0:i1, 1, :], op=ALU.max)
 
         def pe_tr(q, i0, i1):
@@ -309,66 +287,144 @@ def tile_vfe_w_kernel(tc, voxel_feats, W0, gamma0, beta0, W1_words, W1_scales, g
             nc.scalar.copy(out=o_sb[:, cols], in_=st[("tr_ps", q)][:, i0:i1, :].rearrange("v i n -> v (i n)"))
             nc.sync.dma_start(out=out[:, cols], in_=o_sb[:, cols])
 
-        first_quad = []
+        def finish(q):
+            if 0 <= q:
+                pe_tr(q, 0, QUAD)
+                s_out(q, 0, QUAD)
+
+        early = {}
+
+        def early_passes(i, js):
+            if i not in early:
+                early[i] = bank(2 + i, [P, NM, NV], F32, "ye_ps")
+            for j in js:
+                mx_pass(early[i][:].rearrange("p m v -> p (m v)"), j, i * P, j == 0, j == G0 - 1)
+
+        for t in range(4):
+            l0_stat(0, t)
+        l0_aggr(0)
+        for g in range(1, G0):
+            l0_stat(g, 0)
+            l0_stat(g, 1)
+            l0_stat(g, 2)
+            l0_small(g - 1, 0)
+            l0_stat(g, 3)
+            l0_small(g - 1, 1)
+            l0_aggr(g)
+            l0_small(g - 1, 2)
+            l0_act(g - 1)
+            if g >= 2:
+                l0_regroup(g - 2)
+                l0_quant_p(g - 2)
+        l0_small(G0 - 1, 0)
+        l0_regroup(G0 - 2)
+        l0_small(G0 - 1, 1)
+        l0_quant_p(G0 - 2)
+        l0_small(G0 - 1, 2)
+        l0_act(G0 - 1)
+        if EARLY:
+            early_passes(0, (0,))
+            early_passes(1, (0,))
+            early_passes(0, (1,))
+            early_passes(1, (1,))
+            early_passes(2, (0, 1))
+            early_passes(3, (0, 1))
+            for i in range(4):
+                early_passes(i, (2,))
+            early_passes(4, (0, 1, 2))
+            early_passes(5, (0, 1, 2))
+        l0_max(0)
+        l0_max(1)
+        l0_quant_a(0, 0)
+        l0_quant_a(1, 0)
+        l0_max(2)
+        l0_quant_a(2, 0)
+        l0_regroup(G0 - 1)
+        l0_quant_p(G0 - 1)
+        l0_max(3)
+        l0_quant_a(3, 0)
+        for g in range(G0):
+            l0_quant_a(g, 1)
+
+        first_quad = {}
         n_lo = 0
         for width in RANGES:
-            first_quad.append((n_lo // (QUAD * P), (n_lo + width) // (QUAD * P)))
+            first_quad[n_lo // (QUAD * P)] = (n_lo + width) // (QUAD * P)
             n_lo += width
-        starts = dict(first_quad)
 
         def add_stats(q, half):
             v_add(q, 2 * half, 2 * half + 2, st[("yp_ps", q, half)][:])
             v_stats(q, 2 * half, 2 * half + 2)
 
-        def finish(q):
-            if q >= 0:
-                pe_tr(q, 0, QUAD)
-                s_out(q, 0, QUAD)
-
         LAST = NQ - 1
         for q in range(LAST):
             if q == 0:
-                mx_yp(0, 0)
-                mx_yp(0, 1)
-            if q in starts:
-                for q2 in range(q, starts[q]):
+                if EARLY:
+                    for i in range(6):
+                        early_passes(i, (3,))
+                else:
+                    mx_yp(0, 0, 2)
+                    mx_yp(0, 1, 3)
+            if q in first_quad:
+                for q2 in range(q, min(first_quad[q], LAST)):
                     mx_ya(q2)
-            s_yacopy(q)
+                    s_yacopy(q2)
             if q >= 1:
+                s_rstd(q - 1, 0, QUAD)
+                small(nc.gpsimd, q - 1, 0, QUAD)
                 s_act(q - 1, 0, QUAD)
-                mx_yp(q, 0)
-            add_stats(q, 0)
-            if q >= 1:
-                mx_yp(q, 1)
-            finish(q - 2)
-            add_stats(q, 1)
-            small(q, 0, QUAD)
+            if EARLY and q == 0:
+                for i in range(4):
+                    v_add(0, i, i + 1, early[i][:].unsqueeze(1))
+                v_stats(0, 0, 4)
+            elif EARLY and q == 1:
+                for i in range(2):
+                    v_add(1, i, i + 1, early[4 + i][:].unsqueeze(1))
+                v_stats(1, 0, 2)
+                mx_yp(1, 1, 3)
+                add_stats(1, 1)
+            else:
+                if q >= 1:
+                    mx_yp(q, 0, 2 + 2 * (q % 2))
+                add_stats(q, 0)
+                if q >= 1:
+                    mx_yp(q, 1, 3 + 2 * (q % 2))
+            finish(q - TR_LAG)
+            if not (EARLY and q <= 1):
+                add_stats(q, 1)
             if q >= 1:
                 v_max(q - 1, 0, QUAD)
 
         q = LAST
-        mx_ya(q)
-        s_yacopy(q)
+        tiles_of(q)
+        s_rstd(q - 1, 0, QUAD)
+        small(nc.gpsimd, q - 1, 0, QUAD)
         s_act(q - 1, 0, QUAD)
-        accs = [bank(2 + i, [P, NM, NV], F32, "yl_ps") for i in (2, 3, 0, 1)]
+        accs = [bank(b, [P, NM, NV], F32, "yl_ps") for b in (4, 5, 2, 3)]
+        for pair in range(2):
+            for i in (2 * pair, 2 * pair + 1):
+                for j in range(G0):
+                    mx_pass(accs[i][:].rearrange("p m v -> p (m v)"), G0 + j, (QUAD * q + i) * P, j == 0, False, both=True)
+            finish(q - TR_LAG + pair)
         for j in range(G0):
             for i in range(QUAD):
-                mx_pass(accs[i][:].rearrange("p m v -> p (m v)"), j, (QUAD * q + i) * P, j == 0, j == G0 - 1)
-            if j == 0:
-                finish(q - 2)
+                mx_pass(accs[i][:].rearrange("p m v -> p (m v)"), j, (QUAD * q + i) * P, False, j == G0 - 1)
+            if j == 0 and TR_LAG == 3:
+                pass
         v_max(q - 1, 0, QUAD)
-        finish(q - 1)
-        step = TAILSTEP
-        for i0 in range(0, QUAD, step):
-            for i in range(i0, i0 + step):
-                v_add(q, i, i + 1, accs[i][:].unsqueeze(1))
-                v_stats(q, i, i + 1)
-            small(q, i0, i0 + step)
-            s_act(q, i0, i0 + step)
-            if i0 > 0:
-                v_max(q, i0 - step, i0)
-                pe_tr(q, i0 - step, i0)
-                s_out(q, i0 - step, i0)
-        v_max(q, QUAD - step, QUAD)
-        pe_tr(q, QUAD - step, QUAD)
-        s_out(q, QUAD - step, QUAD)
+        v_stats(q, 0, 2, accs)
+        s_rstd(q, 0, 2)
+        v_stats(q, 2, 4, accs)
+        s_rstd(q, 2, 4)
+        small(nc.vector, q, 0, 2)
+        s_act(q, 0, 2, accs)
+        small(nc.vector, q, 2, 4)
+        s_act(q, 2, 4, accs)
+        if TR_LAG == 3:
+            finish(q - 1)
+        v_max(q, 0, 2)
+        pe_tr(q, 0, 2)
+        s_out(q, 0, 2)
+        v_max(q, 2, 4)
+        pe_tr(q, 2, 4)
+        s_out(q, 2, 4)

@@ -24,9 +24,8 @@ QUAD = 4
 NQ = C1 // (QUAD * P)
 
 REGROUP_ON_G = ()
-RANGES = (1024, 1024, 1024, 512, 512)
+LOADS = ((0, 1024, True), (0, 1024, False), (1024, 1024, False), (1024, 1024, True), (2048, 1024, False), (2048, 1024, True), (3072, 1024, False), (3072, 512, True), (3584, 512, True))
 TR_LAG = 3
-EARLY = True
 WORK_BUFS = 4
 
 FLOPS = 2 * ROWS * 128 * C0 + 2 * ROWS * 2 * C0 * C1
@@ -77,18 +76,16 @@ def tile_vfe_w_kernel(tc, voxel_feats, W0, gamma0, beta0, W1_words, W1_scales, g
                     in_=W1_scales[4 * h : 4 * h + 4, 4 * quadrant : 4 * quadrant + 4, :].bitcast(I32),
                 )
         words = {}
-        n_lo = 0
-        for r, width in enumerate(RANGES):
-            order = (0, 1, 2, 3, 4, 5, 6, 7) if r == 0 else (4, 5, 6, 7, 0, 1, 2, 3)
-            for g in order:
-                wt = keep.tile([P, width], I32, name="w_%d_%d" % (r, g), align_bytes=64)
+        for lo, width, top in LOADS:
+            for j in range(G0):
+                g = j if top else G0 + j
+                wt = keep.tile([P, width], I32, name="w_%d_%d" % (lo, g), align_bytes=64)
                 nc.sync.dma_start(
                     out=wt[:],
-                    in_=W1_words[g].rearrange("p n t -> p (n t)")[:, 4 * n_lo : 4 * (n_lo + width)].bitcast(I32),
+                    in_=W1_words[g].rearrange("p n t -> p (n t)")[:, 4 * lo : 4 * (lo + width)].bitcast(I32),
                 )
                 for c in range(0, width, P):
-                    words[(g, n_lo + c)] = (wt, c)
-            n_lo += width
+                    words[(g, lo + c)] = (wt, c)
 
         xT = keep.tile([P, ROWS], BF16)
         w0T = keep.tile([P, G0, 4, P], BF16)
@@ -104,8 +101,8 @@ def tile_vfe_w_kernel(tc, voxel_feats, W0, gamma0, beta0, W1_words, W1_scales, g
         agr = keep.tile([P, G0, NV, 4], BF16, align_bytes=64)
         p_codes = keep.tile([P, G0, ROWS], U32, align_bytes=64)
         p_scales = keep.tile([P, G0, ROWS], U8, align_bytes=64)
-        a_codes = keep.tile([P, G0, NM, NV], U32, align_bytes=64)
-        a_scales = keep.tile([P, G0, NM, NV], U8, align_bytes=64)
+        a_codes = keep.tile([P, G0, NV], U32, align_bytes=64)
+        a_scales = keep.tile([P, G0, NV], U8, align_bytes=64)
 
         xT_ps = bank(0, [P, NM, NV], BF16, "xT_ps")
         for m in range(NM):
@@ -178,26 +175,23 @@ def tile_vfe_w_kernel(tc, voxel_feats, W0, gamma0, beta0, W1_words, W1_scales, g
         def l0_max(g):
             nc.vector.tensor_tensor(out=agr[:, g], in0=grp[:, g, 0:NV, :], in1=grp[:, g, NV:ROWS, :], op=ALU.max)
 
-        def l0_quant_a(g, m):
+        def l0_quant_a(g):
             nc.vector.quantize_mx(
-                out=a_codes[:, g, m, :].bitcast(FP8X4), scales=a_scales[:, g, m, :],
+                out=a_codes[:, g, :].bitcast(FP8X4), scales=a_scales[:, g, :],
                 in_=agr[:, g].rearrange("p r t -> p (r t)"),
             )
 
         st = {}
         o_sb = keep.tile([P, C1], F32)
 
-        def mx_pass(acc, g, n0, first, last, both=False):
+        def mx_pass(acc, g, n0, first, last):
             j = g % G0
             top = g < G0
             wt, c = words[(g, n0)]
             if top:
                 rhs, rhs_scale = p_codes[:, j, :], p_scales[:, j, :]
-            elif both:
-                rhs = a_codes[:, j].rearrange("p m v -> p (m v)")
-                rhs_scale = a_scales[:, j].rearrange("p m v -> p (m v)")
             else:
-                rhs, rhs_scale = a_codes[:, j, 0, :], a_scales[:, j, 0, :]
+                rhs, rhs_scale = a_codes[:, j, :], a_scales[:, j, :]
             nc.tensor.matmul_mx(
                 out=acc,
                 lhsT=wt[:, c : c + P].bitcast(FP8X4),
@@ -282,23 +276,18 @@ def tile_vfe_w_kernel(tc, voxel_feats, W0, gamma0, beta0, W1_words, W1_scales, g
             for i in range(i0, i1):
                 nc.tensor.transpose(st[("tr_ps", q)][:, i, :], st[("zmax", q)][:, i, :], ident_f[:])
 
-        def s_out(q, i0, i1):
+        def s_out(q, i0, i1, on_vector=False):
             cols = slice((QUAD * q + i0) * P, (QUAD * q + i1) * P)
-            nc.scalar.copy(out=o_sb[:, cols], in_=st[("tr_ps", q)][:, i0:i1, :].rearrange("v i n -> v (i n)"))
+            if on_vector:
+                nc.vector.tensor_copy(out=o_sb[:, cols], in_=st[("tr_ps", q)][:, i0:i1, :].rearrange("v i n -> v (i n)"))
+            else:
+                nc.scalar.copy(out=o_sb[:, cols], in_=st[("tr_ps", q)][:, i0:i1, :].rearrange("v i n -> v (i n)"))
             nc.sync.dma_start(out=out[:, cols], in_=o_sb[:, cols])
 
         def finish(q):
             if 0 <= q:
                 pe_tr(q, 0, QUAD)
                 s_out(q, 0, QUAD)
-
-        early = {}
-
-        def early_passes(i, js):
-            if i not in early:
-                early[i] = bank(2 + i, [P, NM, NV], F32, "ye_ps")
-            for j in js:
-                mx_pass(early[i][:].rearrange("p m v -> p (m v)"), j, i * P, j == 0, j == G0 - 1)
 
         for t in range(4):
             l0_stat(0, t)
@@ -313,44 +302,56 @@ def tile_vfe_w_kernel(tc, voxel_feats, W0, gamma0, beta0, W1_words, W1_scales, g
             l0_aggr(g)
             l0_small(g - 1, 2)
             l0_act(g - 1)
-            if g >= 2:
-                l0_regroup(g - 2)
-                l0_quant_p(g - 2)
+            if g - 1 in REGROUP_ON_G:
+                l0_regroup(g - 1)
+        if 0 not in REGROUP_ON_G:
+            l0_regroup(0)
         l0_small(G0 - 1, 0)
-        l0_regroup(G0 - 2)
+        l0_quant_p(0)
         l0_small(G0 - 1, 1)
-        l0_quant_p(G0 - 2)
+        if 1 not in REGROUP_ON_G:
+            l0_regroup(1)
         l0_small(G0 - 1, 2)
         l0_act(G0 - 1)
-        if EARLY:
-            early_passes(0, (0,))
-            early_passes(1, (0,))
-            early_passes(0, (1,))
-            early_passes(1, (1,))
-            early_passes(2, (0, 1))
-            early_passes(3, (0, 1))
-            for i in range(4):
-                early_passes(i, (2,))
-            early_passes(4, (0, 1, 2))
-            early_passes(5, (0, 1, 2))
+        l0_quant_p(1)
+        l0_regroup(2)
         l0_max(0)
+        l0_quant_p(2)
         l0_max(1)
-        l0_quant_a(0, 0)
-        l0_quant_a(1, 0)
+        l0_quant_a(0)
+        l0_quant_a(1)
         l0_max(2)
-        l0_quant_a(2, 0)
         l0_regroup(G0 - 1)
+        l0_quant_a(2)
         l0_quant_p(G0 - 1)
         l0_max(3)
-        l0_quant_a(3, 0)
-        for g in range(G0):
-            l0_quant_a(g, 1)
+        l0_quant_a(3)
+
+        early = [bank(2 + i, [P, NM, NV], F32, "ye_ps") for i in range(4)]
+        pair_10 = bank(6, [P, 2, NM, NV], F32, "yp_ps")
+        st[("yp_ps", 1, 0)] = pair_10
+
+        def early_passes(i, js):
+            acc = early[i][:] if i < 4 else pair_10[:, i - 4]
+            for j in js:
+                mx_pass(acc.rearrange("p m v -> p (m v)"), j, i * P, j == 0, j == G0 - 1)
+
+        early_passes(0, (0,))
+        early_passes(1, (0,))
+        early_passes(0, (1,))
+        early_passes(1, (1,))
+        early_passes(2, (0, 1))
+        early_passes(3, (0, 1))
+        for i in range(4):
+            early_passes(i, (2,))
+        early_passes(4, (0, 1, 2))
+        for i in range(5):
+            early_passes(i, (3,))
 
         first_quad = {}
-        n_lo = 0
-        for width in RANGES:
-            first_quad[n_lo // (QUAD * P)] = (n_lo + width) // (QUAD * P)
-            n_lo += width
+        for lo, width, top in LOADS:
+            if not top:
+                first_quad[lo // (QUAD * P)] = (lo + width) // (QUAD * P)
 
         def add_stats(q, half):
             v_add(q, 2 * half, 2 * half + 2, st[("yp_ps", q, half)][:])
@@ -358,73 +359,60 @@ def tile_vfe_w_kernel(tc, voxel_feats, W0, gamma0, beta0, W1_words, W1_scales, g
 
         LAST = NQ - 1
         for q in range(LAST):
-            if q == 0:
-                if EARLY:
-                    for i in range(6):
-                        early_passes(i, (3,))
-                else:
-                    mx_yp(0, 0, 2)
-                    mx_yp(0, 1, 3)
-            if q in first_quad:
-                for q2 in range(q, min(first_quad[q], LAST)):
+            if q in first_quad and q < LAST:
+                for q2 in range(q, first_quad[q]):
                     mx_ya(q2)
                     s_yacopy(q2)
+                    if q2 == 0:
+                        early_passes(5, (0, 1, 2, 3))
             if q >= 1:
                 s_rstd(q - 1, 0, QUAD)
                 small(nc.gpsimd, q - 1, 0, QUAD)
                 s_act(q - 1, 0, QUAD)
-            if EARLY and q == 0:
+            if q == 0:
                 for i in range(4):
                     v_add(0, i, i + 1, early[i][:].unsqueeze(1))
                 v_stats(0, 0, 4)
-            elif EARLY and q == 1:
-                for i in range(2):
-                    v_add(1, i, i + 1, early[4 + i][:].unsqueeze(1))
-                v_stats(1, 0, 2)
-                mx_yp(1, 1, 3)
-                add_stats(1, 1)
             else:
-                if q >= 1:
+                if q >= 2:
                     mx_yp(q, 0, 2 + 2 * (q % 2))
                 add_stats(q, 0)
-                if q >= 1:
-                    mx_yp(q, 1, 3 + 2 * (q % 2))
-            finish(q - TR_LAG)
-            if not (EARLY and q <= 1):
+                mx_yp(q, 1, 7 if q == 1 else 3 + 2 * (q % 2))
+                finish(q - TR_LAG)
                 add_stats(q, 1)
-            if q >= 1:
                 v_max(q - 1, 0, QUAD)
 
         q = LAST
-        tiles_of(q)
+        accs = [bank(b, [P, NM, NV], F32, "yl_ps") for b in (4, 5, 2, 3)]
+        for i in range(QUAD):
+            for j in range(G0):
+                mx_pass(accs[i][:].rearrange("p m v -> p (m v)"), j, (QUAD * q + i) * P, j == 0, j == G0 - 1)
+        pe_tr(q - 3, 0, QUAD)
+        pe_tr(q - 2, 0, QUAD)
         s_rstd(q - 1, 0, QUAD)
         small(nc.gpsimd, q - 1, 0, QUAD)
-        s_act(q - 1, 0, QUAD)
-        accs = [bank(b, [P, NM, NV], F32, "yl_ps") for b in (4, 5, 2, 3)]
-        for pair in range(2):
-            for i in (2 * pair, 2 * pair + 1):
-                for j in range(G0):
-                    mx_pass(accs[i][:].rearrange("p m v -> p (m v)"), G0 + j, (QUAD * q + i) * P, j == 0, False, both=True)
-            finish(q - TR_LAG + pair)
-        for j in range(G0):
-            for i in range(QUAD):
-                mx_pass(accs[i][:].rearrange("p m v -> p (m v)"), j, (QUAD * q + i) * P, False, j == G0 - 1)
-            if j == 0 and TR_LAG == 3:
-                pass
-        v_max(q - 1, 0, QUAD)
-        v_stats(q, 0, 2, accs)
+        s_out(q - 3, 0, QUAD)
+        s_out(q - 2, 0, QUAD)
+        s_act(q - 1, 0, 2)
+        for i in (0, 1):
+            v_add(q, i, i + 1, accs[i][:].unsqueeze(1))
+        v_stats(q, 0, 2)
         s_rstd(q, 0, 2)
-        v_stats(q, 2, 4, accs)
+        s_act(q - 1, 2, 4)
+        for i in (2, 3):
+            v_add(q, i, i + 1, accs[i][:].unsqueeze(1))
+        v_stats(q, 2, 4)
         s_rstd(q, 2, 4)
         small(nc.vector, q, 0, 2)
-        s_act(q, 0, 2, accs)
+        s_act(q, 0, 2)
         small(nc.vector, q, 2, 4)
-        s_act(q, 2, 4, accs)
-        if TR_LAG == 3:
-            finish(q - 1)
+        s_act(q, 2, 4)
+        v_max(q - 1, 0, QUAD)
+        pe_tr(q - 1, 0, QUAD)
         v_max(q, 0, 2)
         pe_tr(q, 0, 2)
-        s_out(q, 0, 2)
         v_max(q, 2, 4)
         pe_tr(q, 2, 4)
+        s_out(q - 1, 0, QUAD)
+        s_out(q, 0, 2, True)
         s_out(q, 2, 4)

@@ -52,6 +52,12 @@ def tile_vfe_w_kernel(tc, voxel_feats, W0, gamma0, beta0, W1_words, W1_scales, g
         nc.vector.memset(planes[:].bitcast(I32), 0)
         ident_bf = keep.tile([P, P], BF16)
         make_identity(nc, ident_bf[:])
+        for h in range(2):
+            for quadrant in range(4):
+                nc.gpsimd.dma_start(
+                    out=planes[32 * quadrant : 32 * quadrant + 16, h, :].bitcast(F32),
+                    in_=W1_scales[4 * h : 4 * h + 4, 4 * quadrant : 4 * quadrant + 4, :].bitcast(F32),
+                )
         ident_f = keep.tile([P, P], F32)
         make_identity(nc, ident_f[:])
 
@@ -69,12 +75,6 @@ def tile_vfe_w_kernel(tc, voxel_feats, W0, gamma0, beta0, W1_words, W1_scales, g
         nc.scalar.dma_start(out=b0_sb[:], in_=beta0.rearrange("(g p t) -> p g t", g=G0, p=P, t=4))
         warm = keep.tile([P, 1], F32)
         nc.scalar.activation(out=warm[:], in_=eps_t[:], func=ACT.Abs_reciprocal_sqrt)
-        for h in range(2):
-            for quadrant in range(4):
-                nc.sync.dma_start(
-                    out=planes[32 * quadrant : 32 * quadrant + 16, h, :].bitcast(I32),
-                    in_=W1_scales[4 * h : 4 * h + 4, 4 * quadrant : 4 * quadrant + 4, :].bitcast(I32),
-                )
         words = {}
         for lo, width, top in LOADS:
             for j in range(G0):

@@ -26,6 +26,8 @@ NQ = C1 // (QUAD * P)
 REGROUP_ON_G = ()
 LOADS = ((0, 1024, True), (0, 1024, False), (1024, 1024, False), (1024, 1024, True), (2048, 1024, False), (2048, 1024, True), (3072, 1024, False), (3072, 512, True), (3584, 512, True))
 TR_LAG = 3
+L0_ORDER = (0, 1, 2, 3, 4, 5, 6, 7)
+S_CHAIN_FROM = 0
 WORK_BUFS = 4
 
 FLOPS = 2 * ROWS * 128 * C0 + 2 * ROWS * 2 * C0 * C1
@@ -90,6 +92,7 @@ def tile_vfe_w_kernel(tc, voxel_feats, W0, gamma0, beta0, W1_words, W1_scales, g
         xT = keep.tile([P, ROWS], BF16)
         w0T = keep.tile([P, G0, 4, P], BF16)
         gb1 = keep.tile([P, 64], F32)
+        ngam1 = keep.tile([P, 32], F32)
         st0 = keep.tile([P, G0, 4, 6], F32)
         mv0 = keep.tile([P, G0, 4, 2], F32)
         rstd0 = keep.tile([P, G0, 4], F32)
@@ -111,7 +114,7 @@ def tile_vfe_w_kernel(tc, voxel_feats, W0, gamma0, beta0, W1_words, W1_scales, g
 
         y0_bank = ((2, 3), (4, 5), (6, 7), (1, 0))
         y0 = {}
-        for g in range(G0):
+        def w0_transposes(g):
             blocks = 5 if g == G0 - 1 else 4
             wT_ps = bank(4 + g, [P, blocks, P], BF16, "wT_ps")
             for t in range(4):
@@ -124,12 +127,20 @@ def tile_vfe_w_kernel(tc, voxel_feats, W0, gamma0, beta0, W1_words, W1_scales, g
                 nc.vector.tensor_copy(out=w0T[:, g], in_=wT_ps[:, 0:4, :])
             if g == G0 - 1:
                 nc.scalar.copy(out=gb1[:], in_=wT_ps[:, 4, 0:64])
-        for g in range(G0):
+                nc.gpsimd.tensor_scalar(out=ngam1[:], in0=gb1[:, 0:32], scalar1=-1.0, scalar2=0.0, op0=ALU.mult, op1=ALU.add)
+
+        def l0_matmuls(g):
             for half in range(2):
                 yt = bank(y0_bank[g][half], [P, 2, ROWS], F32, "y0")
                 y0[(g, half)] = yt
                 for u in range(2):
                     nc.tensor.matmul(out=yt[:, u, :], lhsT=w0T[:, g, 2 * half + u, :], rhs=xT[:], start=True, stop=True)
+
+        for step in L0_ORDER:
+            if step < G0:
+                w0_transposes(step)
+            else:
+                l0_matmuls(step - G0)
 
         def l0_stat(g, t):
             nc.vector.bn_stats(out=st0[:, g, t, :], in_=y0[(g, t // 2)][:, t % 2, :])
@@ -259,6 +270,25 @@ def tile_vfe_w_kernel(tc, voxel_feats, W0, gamma0, beta0, W1_words, W1_scales, g
             eng.tensor_tensor(out=ms1[:, i0:i1], in0=mv1[:, i0:i1, 0], in1=s1[:, i0:i1], op=ALU.mult)
             eng.tensor_tensor(out=sh1[:, i0:i1], in0=gb1[:, 32 + t0 + i0 : 32 + t0 + i1], in1=ms1[:, i0:i1], op=ALU.subtract)
 
+        def v_negmean(q, i0, i1):
+            t0 = QUAD * q
+            nc.vector.tensor_tensor(
+                out=st[("ms1", q)][:, i0:i1], in0=st[("mv1", q)][:, i0:i1, 0], in1=ngam1[:, t0 + i0 : t0 + i1], op=ALU.mult
+            )
+
+        def s_chain(q, i0, i1):
+            rstd1, s1, ms1, sh1 = st[("rstd1", q)], st[("s1", q)], st[("ms1", q)], st[("sh1", q)]
+            nc.scalar.activation(
+                out=rstd1[:, i0:i1], in_=st[("mv1", q)][:, i0:i1, 1], func=ACT.Abs_reciprocal_sqrt, bias=eps_t[:]
+            )
+            for i in range(i0, i1):
+                t = QUAD * q + i
+                nc.scalar.activation(out=s1[:, i : i + 1], in_=rstd1[:, i : i + 1], func=ACT.Copy, scale=gb1[:, t : t + 1])
+                nc.scalar.activation(
+                    out=sh1[:, i : i + 1], in_=rstd1[:, i : i + 1], func=ACT.Identity,
+                    scale=ms1[:, i : i + 1], bias=gb1[:, 32 + t : 33 + t],
+                )
+
         def s_act(q, i0, i1, srcs=None):
             for i in range(i0, i1):
                 nc.scalar.activation(
@@ -366,13 +396,18 @@ def tile_vfe_w_kernel(tc, voxel_feats, W0, gamma0, beta0, W1_words, W1_scales, g
                     if q2 == 0:
                         early_passes(5, (0, 1, 2, 3))
             if q >= 1:
-                s_rstd(q - 1, 0, QUAD)
-                small(nc.gpsimd, q - 1, 0, QUAD)
+                if q - 1 >= S_CHAIN_FROM:
+                    s_chain(q - 1, 0, QUAD)
+                else:
+                    s_rstd(q - 1, 0, QUAD)
+                    small(nc.gpsimd, q - 1, 0, QUAD)
                 s_act(q - 1, 0, QUAD)
             if q == 0:
                 for i in range(4):
                     v_add(0, i, i + 1, early[i][:].unsqueeze(1))
                 v_stats(0, 0, 4)
+                if S_CHAIN_FROM == 0:
+                    v_negmean(0, 0, QUAD)
             else:
                 if q >= 2:
                     mx_yp(q, 0, 2 + 2 * (q % 2))
@@ -380,7 +415,10 @@ def tile_vfe_w_kernel(tc, voxel_feats, W0, gamma0, beta0, W1_words, W1_scales, g
                 mx_yp(q, 1, 7 if q == 1 else 3 + 2 * (q % 2))
                 finish(q - TR_LAG)
                 add_stats(q, 1)
-                v_max(q - 1, 0, QUAD)
+                if q >= S_CHAIN_FROM:
+                    v_negmean(q, 0, QUAD)
+                if q < LAST - 1:
+                    v_max(q - 1, 0, QUAD)
 
         q = LAST
         accs = [bank(b, [P, NM, NV], F32, "yl_ps") for b in (4, 5, 2, 3)]
@@ -388,31 +426,30 @@ def tile_vfe_w_kernel(tc, voxel_feats, W0, gamma0, beta0, W1_words, W1_scales, g
             for j in range(G0):
                 mx_pass(accs[i][:].rearrange("p m v -> p (m v)"), j, (QUAD * q + i) * P, j == 0, j == G0 - 1)
         pe_tr(q - 3, 0, QUAD)
-        pe_tr(q - 2, 0, QUAD)
-        s_rstd(q - 1, 0, QUAD)
-        small(nc.gpsimd, q - 1, 0, QUAD)
-        s_out(q - 3, 0, QUAD)
-        s_out(q - 2, 0, QUAD)
-        s_act(q - 1, 0, 2)
+        s_chain(q - 1, 0, QUAD)
+        s_act(q - 1, 0, QUAD)
         for i in (0, 1):
             v_add(q, i, i + 1, accs[i][:].unsqueeze(1))
         v_stats(q, 0, 2)
-        s_rstd(q, 0, 2)
-        s_act(q - 1, 2, 4)
+        v_negmean(q, 0, 2)
+        v_max(q - 2, 0, QUAD)
+        pe_tr(q - 2, 0, QUAD)
+        s_chain(q, 0, 2)
+        s_act(q, 0, 2)
         for i in (2, 3):
             v_add(q, i, i + 1, accs[i][:].unsqueeze(1))
         v_stats(q, 2, 4)
-        s_rstd(q, 2, 4)
-        small(nc.vector, q, 0, 2)
-        s_act(q, 0, 2)
-        small(nc.vector, q, 2, 4)
+        v_negmean(q, 2, 4)
+        s_out(q - 3, 0, QUAD)
+        s_chain(q, 2, 4)
         s_act(q, 2, 4)
         v_max(q - 1, 0, QUAD)
         pe_tr(q - 1, 0, QUAD)
+        s_out(q - 2, 0, QUAD, True)
         v_max(q, 0, 2)
         pe_tr(q, 0, 2)
         v_max(q, 2, 4)
         pe_tr(q, 2, 4)
-        s_out(q - 1, 0, QUAD)
-        s_out(q, 0, 2, True)
+        s_out(q - 1, 0, QUAD, True)
+        s_out(q, 0, 2)
         s_out(q, 2, 4)

@@ -23,10 +23,10 @@ EPS = 1e-3
 QUAD = 4
 NQ = C1 // (QUAD * P)
 
-REGROUP_ON_G = ()
-LOADS = ((0, 1024, True), (0, 1024, False), (1024, 1024, False), (1024, 1024, True), (2048, 1024, False), (2048, 1024, True), (3072, 1024, False), (3072, 512, True), (3584, 512, True))
+REGROUP_ON_G = (0, 1)
+LOADS = ((0, 1024, True), (0, 1024, False), (1024, 1024, False), (1024, 1024, True), (2048, 1024, False), (2048, 1024, True), (3072, 512, False), (3072, 512, True), (3584, 512, False), (3584, 512, True))
 TR_LAG = 3
-L0_ORDER = (0, 1, 2, 3, 4, 5, 6, 7)
+L0_ORDER = (0, 1, 4, 2, 5, 3, 6, 7)
 S_CHAIN_FROM = 0
 WORK_BUFS = 4
 
@@ -44,6 +44,8 @@ def tile_vfe_w_kernel(tc, voxel_feats, W0, gamma0, beta0, W1_words, W1_scales, g
         def bank(b, shape, dtype, name):
             return psum.tile(shape, dtype, name=name, tag="b%d" % b)
 
+        warm_bf = keep.tile([P, 512], BF16)
+        nc.vector.memset(warm_bf[:], 0.0)
         zero_t = keep.tile([P, 1], F32)
         nc.vector.memset(zero_t[:], 0.0)
         eps_t = keep.tile([P, 1], F32)
@@ -92,7 +94,8 @@ def tile_vfe_w_kernel(tc, voxel_feats, W0, gamma0, beta0, W1_words, W1_scales, g
         xT = keep.tile([P, ROWS], BF16)
         w0T = keep.tile([P, G0, 4, P], BF16)
         gb1 = keep.tile([P, 64], F32)
-        ngam1 = keep.tile([P, 32], F32)
+        sgn1 = keep.tile([P, 32], F32)
+        agam1 = keep.tile([P, 32], F32)
         st0 = keep.tile([P, G0, 4, 6], F32)
         mv0 = keep.tile([P, G0, 4, 2], F32)
         rstd0 = keep.tile([P, G0, 4], F32)
@@ -107,6 +110,9 @@ def tile_vfe_w_kernel(tc, voxel_feats, W0, gamma0, beta0, W1_words, W1_scales, g
         a_codes = keep.tile([P, G0, NV], U32, align_bytes=64)
         a_scales = keep.tile([P, G0, NV], U8, align_bytes=64)
 
+        warm_ps = bank(7, [P, 512], F32, "warm_ps")
+        for n in range(3):
+            nc.tensor.matmul(out=warm_ps[:], lhsT=warm_bf[:, 0:P], rhs=warm_bf[:], start=True, stop=True)
         xT_ps = bank(0, [P, NM, NV], BF16, "xT_ps")
         for m in range(NM):
             nc.tensor.transpose(xT_ps[:, m, :], vox_sb[:, m, :], ident_bf[:])
@@ -121,13 +127,11 @@ def tile_vfe_w_kernel(tc, voxel_feats, W0, gamma0, beta0, W1_words, W1_scales, g
                 nc.tensor.transpose(wT_ps[:, t, :], w0_sb[:, g, t, :], ident_bf[:])
             if g == G0 - 1:
                 nc.tensor.transpose(wT_ps[:, 4, :], gb[:], ident_bf[:])
-            if g % 2 == 0:
-                nc.scalar.copy(out=w0T[:, g], in_=wT_ps[:, 0:4, :])
-            else:
-                nc.vector.tensor_copy(out=w0T[:, g], in_=wT_ps[:, 0:4, :])
+            nc.scalar.copy(out=w0T[:, g], in_=wT_ps[:, 0:4, :])
             if g == G0 - 1:
                 nc.scalar.copy(out=gb1[:], in_=wT_ps[:, 4, 0:64])
-                nc.gpsimd.tensor_scalar(out=ngam1[:], in0=gb1[:, 0:32], scalar1=-1.0, scalar2=0.0, op0=ALU.mult, op1=ALU.add)
+                nc.scalar.activation(out=sgn1[:], in_=wT_ps[:, 4, 0:32], func=ACT.Sign)
+                nc.scalar.activation(out=agam1[:], in_=wT_ps[:, 4, 0:32], func=ACT.Abs)
 
         def l0_matmuls(g):
             for half in range(2):
@@ -192,8 +196,59 @@ def tile_vfe_w_kernel(tc, voxel_feats, W0, gamma0, beta0, W1_words, W1_scales, g
                 in_=agr[:, g].rearrange("p r t -> p (r t)"),
             )
 
-        st = {}
+        def l0_act2(g, t0):
+            for t in (t0, t0 + 1):
+                nc.scalar.activation(
+                    out=p_bf[:, g, t, :], in_=y0[(g, t // 2)][:, t % 2, :], func=ACT.Relu,
+                    bias=sh0[:, g, t : t + 1], scale=s0[:, g, t : t + 1],
+                )
+
+        def l0_ag(g):
+            for t in range(4):
+                nc.vector.bn_aggr(out=mv0[:, g, t, :], in_=st0[:, g, t, :])
+
+        def l0_rstd(g):
+            nc.scalar.activation(out=rstd0[:, g, :], in_=mv0[:, g, :, 1], func=ACT.Abs_reciprocal_sqrt, bias=eps_t[:])
+
+        for t in range(4):
+            l0_stat(0, t)
+        l0_ag(0)
+        l0_rstd(0)
+        for g in range(1, G0):
+            l0_stat(g, 0)
+            l0_stat(g, 1)
+            l0_small(g - 1, 0)
+            l0_stat(g, 2)
+            l0_small(g - 1, 1)
+            l0_stat(g, 3)
+            l0_small(g - 1, 2)
+            l0_ag(g)
+            l0_act2(g - 1, 0)
+            l0_rstd(g)
+            l0_act2(g - 1, 2)
+            if g - 1 in REGROUP_ON_G:
+                l0_regroup(g - 1)
+        l0_quant_p(0)
+        l0_small(G0 - 1, 0)
+        l0_max(0)
+        l0_small(G0 - 1, 1)
+        l0_quant_a(0)
+        l0_small(G0 - 1, 2)
+        l0_act(G0 - 1)
+        l0_quant_p(1)
+        l0_regroup(2)
+        l0_max(1)
+        l0_quant_p(2)
+        l0_max(2)
+        l0_quant_a(1)
+        l0_regroup(G0 - 1)
+        l0_quant_a(2)
+        l0_quant_p(G0 - 1)
+        l0_max(3)
+        l0_quant_a(3)
+
         o_sb = keep.tile([P, C1], F32)
+        st = {}
 
         def mx_pass(acc, g, n0, first, last):
             j = g % G0
@@ -212,244 +267,205 @@ def tile_vfe_w_kernel(tc, voxel_feats, W0, gamma0, beta0, W1_words, W1_scales, g
                 start=first, stop=last,
             )
 
-        def tiles_of(q):
-            st[("y", q)] = work.tile([P, QUAD, NM, NV], F32, name="y")
-            st[("st1", q)] = work.tile([P, QUAD, 6], F32, name="st1")
-            st[("mv1", q)] = work.tile([P, QUAD, 2], F32, name="mv1")
-            st[("rstd1", q)] = work.tile([P, QUAD], F32, name="rstd1")
-            st[("s1", q)] = work.tile([P, QUAD], F32, name="s1")
-            st[("ms1", q)] = work.tile([P, QUAD], F32, name="ms1")
-            st[("sh1", q)] = work.tile([P, QUAD], F32, name="sh1")
-            st[("zmax", q)] = work.tile([P, QUAD, NV], F32, name="zmax")
+        def open_tiles(q, i0, banks):
+            for k, b in enumerate(banks):
+                st[("acc", q, i0 + k)] = bank(b, [P, NM, NV], F32, "yp_ps")
 
-        def mx_ya(q):
-            ya_ps = bank(q % 2, [P, QUAD, NV], F32, "ya_ps")
+        def p_passes(q, i0, i1, js):
+            for j in js:
+                for i in range(i0, i1):
+                    mx_pass(st[("acc", q, i)][:].rearrange("p m v -> p (m v)"), j, (QUAD * q + i) * P, j == 0, j == G0 - 1)
+
+        def a_passes(q, b):
+            ya_ps = bank(b, [P, QUAD, NV], F32, "ya_ps")
+            st[("ya_ps", q)] = ya_ps
             for i in range(QUAD):
                 for j in range(G0):
                     mx_pass(ya_ps[:, i, :], G0 + j, (QUAD * q + i) * P, j == 0, j == G0 - 1)
-            st[("ya_ps", q)] = ya_ps
 
-        def s_yacopy(q):
-            ya_sb = work.tile([P, QUAD, NV], F32, name="ya_sb")
-            st[("ya_sb", q)] = ya_sb
-            nc.scalar.copy(out=ya_sb[:], in_=st[("ya_ps", q)][:])
-            tiles_of(q)
+        def s_yacopy(q, on_vector=False):
+            st[("ya", q)] = work.tile([P, QUAD, NV], F32, name="ya_sb")
+            st[("y", q)] = work.tile([P, QUAD, NM, NV], F32, name="y")
+            for n in ("sum1", "nm1", "var1", "rstd1", "s1", "sh1"):
+                st[(n, q)] = work.tile([P, QUAD], F32, name=n)
+            st[("zmax", q)] = work.tile([P, QUAD, NV], F32, name="zmax")
+            st[("z", q)] = work.tile([P, QUAD, NV], F32, name="z")
+            for i in range(QUAD):
+                t = QUAD * q + i
+                if on_vector:
+                    nc.vector.tensor_scalar(out=st[("ya", q)][:, i, :], in0=st[("ya_ps", q)][:, i, :], scalar1=sgn1[:, t : t + 1], scalar2=None, op0=ALU.mult)
+                else:
+                    nc.scalar.activation(out=st[("ya", q)][:, i, :], in_=st[("ya_ps", q)][:, i, :], func=ACT.Copy, scale=sgn1[:, t : t + 1])
 
-        def mx_yp(q, half, b):
-            yp_ps = bank(b, [P, 2, NM, NV], F32, "yp_ps")
-            st[("yp_ps", q, half)] = yp_ps
-            for u in range(2):
-                for j in range(G0):
-                    mx_pass(yp_ps[:, u].rearrange("p m v -> p (m v)"), j, (QUAD * q + 2 * half + u) * P, j == 0, j == G0 - 1)
-
-        def v_add(q, i0, i1, src):
-            nc.vector.tensor_tensor(
-                out=st[("y", q)][:, i0:i1],
-                in0=src,
-                in1=st[("ya_sb", q)][:, i0:i1].unsqueeze(2).to_broadcast([P, i1 - i0, NM, NV]),
-                op=ALU.add,
-            )
-
-        def v_stats(q, i0, i1, srcs=None):
-            for i in range(i0, i1):
-                src = st[("y", q)][:, i] if srcs is None else srcs[i][:]
-                nc.vector.bn_stats(out=st[("st1", q)][:, i, :], in_=src.rearrange("p m v -> p (m v)"))
-            for i in range(i0, i1):
-                nc.vector.bn_aggr(out=st[("mv1", q)][:, i, :], in_=st[("st1", q)][:, i, :])
-
-        def s_rstd(q, i0, i1):
-            nc.scalar.activation(
-                out=st[("rstd1", q)][:, i0:i1], in_=st[("mv1", q)][:, i0:i1, 1], func=ACT.Abs_reciprocal_sqrt, bias=eps_t[:]
-            )
-
-        def small(eng, q, i0, i1):
-            mv1 = st[("mv1", q)]
-            rstd1, s1, ms1, sh1 = st[("rstd1", q)], st[("s1", q)], st[("ms1", q)], st[("sh1", q)]
-            t0 = QUAD * q
-            eng.tensor_tensor(out=s1[:, i0:i1], in0=rstd1[:, i0:i1], in1=gb1[:, t0 + i0 : t0 + i1], op=ALU.mult)
-            eng.tensor_tensor(out=ms1[:, i0:i1], in0=mv1[:, i0:i1, 0], in1=s1[:, i0:i1], op=ALU.mult)
-            eng.tensor_tensor(out=sh1[:, i0:i1], in0=gb1[:, 32 + t0 + i0 : 32 + t0 + i1], in1=ms1[:, i0:i1], op=ALU.subtract)
-
-        def v_negmean(q, i0, i1):
-            t0 = QUAD * q
-            nc.vector.tensor_tensor(
-                out=st[("ms1", q)][:, i0:i1], in0=st[("mv1", q)][:, i0:i1, 0], in1=ngam1[:, t0 + i0 : t0 + i1], op=ALU.mult
-            )
-
-        def s_chain(q, i0, i1):
-            rstd1, s1, ms1, sh1 = st[("rstd1", q)], st[("s1", q)], st[("ms1", q)], st[("sh1", q)]
-            nc.scalar.activation(
-                out=rstd1[:, i0:i1], in_=st[("mv1", q)][:, i0:i1, 1], func=ACT.Abs_reciprocal_sqrt, bias=eps_t[:]
-            )
+        def v_add(q, i0, i1):
             for i in range(i0, i1):
                 t = QUAD * q + i
-                nc.scalar.activation(out=s1[:, i : i + 1], in_=rstd1[:, i : i + 1], func=ACT.Copy, scale=gb1[:, t : t + 1])
-                nc.scalar.activation(
-                    out=sh1[:, i : i + 1], in_=rstd1[:, i : i + 1], func=ACT.Identity,
-                    scale=ms1[:, i : i + 1], bias=gb1[:, 32 + t : 33 + t],
+                nc.vector.scalar_tensor_tensor(
+                    out=st[("y", q)][:, i], in0=st[("acc", q, i)][:], scalar=sgn1[:, t : t + 1],
+                    in1=st[("ya", q)][:, i : i + 1, :].to_broadcast([P, NM, NV]),
+                    op0=ALU.mult, op1=ALU.add, accum_out=st[("sum1", q)][:, i : i + 1],
                 )
 
-        def s_act(q, i0, i1, srcs=None):
-            for i in range(i0, i1):
-                nc.scalar.activation(
-                    out=st[("y", q)][:, i], in_=(st[("y", q)][:, i] if srcs is None else srcs[i][:]), func=ACT.Relu,
-                    bias=st[("sh1", q)][:, i : i + 1], scale=st[("s1", q)][:, i : i + 1],
-                )
+        def v_nm(q, i0, i1):
+            nc.vector.tensor_scalar(out=st[("nm1", q)][:, i0:i1], in0=st[("sum1", q)][:, i0:i1], scalar1=-1.0 / (16 * ROWS), scalar2=None, op0=ALU.mult)
 
         def v_max(q, i0, i1):
-            z = st[("y", q)]
-            nc.vector.tensor_tensor(out=st[("zmax", q)][:, i0:i1], in0=z[:, i0:i1, 0, :], in1=z[:, i0:i1, 1, :], op=ALU.max)
+            y = st[("y", q)]
+            nc.vector.tensor_tensor(out=st[("zmax", q)][:, i0:i1], in0=y[:, i0:i1, 0, :], in1=y[:, i0:i1, 1, :], op=ALU.max)
 
-        def pe_tr(q, i0, i1):
-            if i0 == 0:
-                st[("tr_ps", q)] = bank(6 + q % 2, [P, QUAD, P], F32, "tr_ps")
+        def s_var(q, i0, i1):
             for i in range(i0, i1):
-                nc.tensor.transpose(st[("tr_ps", q)][:, i, :], st[("zmax", q)][:, i, :], ident_f[:])
+                junk = work.tile([P, ROWS], BF16, name="junk")
+                nc.scalar.activation(
+                    out=junk[:], in_=st[("y", q)][:, i].rearrange("p m v -> p (m v)"), func=ACT.Square,
+                    scale=1.0 / 16, bias=st[("nm1", q)][:, i : i + 1], accum_out=st[("var1", q)][:, i : i + 1],
+                )
 
-        def s_out(q, i0, i1, on_vector=False):
+        def s_rstd(q, i0, i1):
+            nc.scalar.activation(out=st[("rstd1", q)][:, i0:i1], in_=st[("var1", q)][:, i0:i1], func=ACT.Abs_reciprocal_sqrt, bias=eps_t[:])
+
+        def v_shift(q, i0, i1):
+            t0 = QUAD * q
+            nc.vector.scalar_tensor_tensor(
+                out=st[("s1", q)][:, i0:i1], in0=st[("nm1", q)][:, i0:i1], scalar=16.0, in1=agam1[:, t0 + i0 : t0 + i1], op0=ALU.mult, op1=ALU.mult
+            )
+
+        def s_scale(q, i0, i1):
+            for i in range(i0, i1):
+                t = QUAD * q + i
+                nc.scalar.activation(
+                    out=st[("sh1", q)][:, i : i + 1], in_=st[("rstd1", q)][:, i : i + 1], func=ACT.Identity,
+                    scale=st[("s1", q)][:, i : i + 1], bias=gb1[:, 32 + t : 33 + t],
+                )
+                nc.scalar.activation(out=st[("var1", q)][:, i : i + 1], in_=st[("rstd1", q)][:, i : i + 1], func=ACT.Copy, scale=agam1[:, t : t + 1])
+
+        def s_relu(q, i0, i1):
+            for i in range(i0, i1):
+                nc.scalar.activation(
+                    out=st[("z", q)][:, i, :], in_=st[("zmax", q)][:, i, :], func=ACT.Relu,
+                    bias=st[("sh1", q)][:, i : i + 1], scale=st[("var1", q)][:, i : i + 1],
+                )
+
+        def pe_tr(q, i0, i1, b):
+            if i0 == 0:
+                st[("tr_ps", q)] = bank(b, [P, QUAD, P], F32, "tr_ps")
+            for i in range(i0, i1):
+                nc.tensor.transpose(st[("tr_ps", q)][:, i, :], st[("z", q)][:, i, :], ident_f[:])
+
+        def copy_out(q, i0, i1, on_vector=True):
             cols = slice((QUAD * q + i0) * P, (QUAD * q + i1) * P)
+            src = st[("tr_ps", q)][:, i0:i1, :].rearrange("v i n -> v (i n)")
             if on_vector:
-                nc.vector.tensor_copy(out=o_sb[:, cols], in_=st[("tr_ps", q)][:, i0:i1, :].rearrange("v i n -> v (i n)"))
+                nc.vector.tensor_copy(out=o_sb[:, cols], in_=src)
             else:
-                nc.scalar.copy(out=o_sb[:, cols], in_=st[("tr_ps", q)][:, i0:i1, :].rearrange("v i n -> v (i n)"))
+                nc.scalar.copy(out=o_sb[:, cols], in_=src)
+
+        def store(q, i0, i1):
+            cols = slice((QUAD * q + i0) * P, (QUAD * q + i1) * P)
             nc.sync.dma_start(out=out[:, cols], in_=o_sb[:, cols])
 
-        def finish(q):
-            if 0 <= q:
-                pe_tr(q, 0, QUAD)
-                s_out(q, 0, QUAD)
+        open_tiles(0, 0, (2, 3, 4, 5))
+        open_tiles(1, 0, (6, 7))
+        p_passes(0, 0, 2, (0,))
+        p_passes(0, 2, 4, (0,))
+        p_passes(0, 0, 4, (1,))
+        p_passes(1, 0, 2, (0, 1))
+        p_passes(0, 0, 4, (2,))
+        p_passes(1, 0, 2, (2,))
+        p_passes(0, 0, 4, (3,))
+        p_passes(1, 0, 2, (3,))
+        a_passes(0, 1)
+        a_passes(1, 0)
+        s_yacopy(0)
+        v_add(0, 0, 4)
+        open_tiles(1, 2, (2, 3))
+        p_passes(1, 2, 4, (0, 1, 2, 3))
+        s_yacopy(1)
+        v_max(0, 0, 2)
+        v_nm(0, 0, 4)
+        s_var(0, 0, 4)
+        v_max(0, 2, 4)
+        v_shift(0, 0, 4)
+        s_rstd(0, 0, 4)
+        s_scale(0, 0, 4)
+        s_relu(0, 0, 4)
+        a_passes(2, 1)
+        a_passes(3, 0)
 
-        for t in range(4):
-            l0_stat(0, t)
-        l0_aggr(0)
-        for g in range(1, G0):
-            l0_stat(g, 0)
-            l0_stat(g, 1)
-            l0_stat(g, 2)
-            l0_small(g - 1, 0)
-            l0_stat(g, 3)
-            l0_small(g - 1, 1)
-            l0_aggr(g)
-            l0_small(g - 1, 2)
-            l0_act(g - 1)
-            if g - 1 in REGROUP_ON_G:
-                l0_regroup(g - 1)
-        if 0 not in REGROUP_ON_G:
-            l0_regroup(0)
-        l0_small(G0 - 1, 0)
-        l0_quant_p(0)
-        l0_small(G0 - 1, 1)
-        if 1 not in REGROUP_ON_G:
-            l0_regroup(1)
-        l0_small(G0 - 1, 2)
-        l0_act(G0 - 1)
-        l0_quant_p(1)
-        l0_regroup(2)
-        l0_max(0)
-        l0_quant_p(2)
-        l0_max(1)
-        l0_quant_a(0)
-        l0_quant_a(1)
-        l0_max(2)
-        l0_regroup(G0 - 1)
-        l0_quant_a(2)
-        l0_quant_p(G0 - 1)
-        l0_max(3)
-        l0_quant_a(3)
+        def quad_vs(q, outs):
+            for x in outs:
+                copy_out(x, 0, 4)
+                store(x, 0, 4)
+            v_add(q, 0, 4)
+            v_max(q, 0, 2)
+            v_nm(q, 0, 4)
+            s_var(q, 0, 4)
+            v_max(q, 2, 4)
+            v_shift(q, 0, 4)
+            s_rstd(q, 0, 4)
+            s_scale(q, 0, 4)
+            s_relu(q, 0, 4)
 
-        early = [bank(2 + i, [P, NM, NV], F32, "ye_ps") for i in range(4)]
-        pair_10 = bank(6, [P, 2, NM, NV], F32, "yp_ps")
-        st[("yp_ps", 1, 0)] = pair_10
-
-        def early_passes(i, js):
-            acc = early[i][:] if i < 4 else pair_10[:, i - 4]
-            for j in js:
-                mx_pass(acc.rearrange("p m v -> p (m v)"), j, i * P, j == 0, j == G0 - 1)
-
-        early_passes(0, (0,))
-        early_passes(1, (0,))
-        early_passes(0, (1,))
-        early_passes(1, (1,))
-        early_passes(2, (0, 1))
-        early_passes(3, (0, 1))
-        for i in range(4):
-            early_passes(i, (2,))
-        early_passes(4, (0, 1, 2))
-        for i in range(5):
-            early_passes(i, (3,))
-
-        first_quad = {}
-        for lo, width, top in LOADS:
-            if not top:
-                first_quad[lo // (QUAD * P)] = (lo + width) // (QUAD * P)
-
-        def add_stats(q, half):
-            v_add(q, 2 * half, 2 * half + 2, st[("yp_ps", q, half)][:])
-            v_stats(q, 2 * half, 2 * half + 2)
-
-        LAST = NQ - 1
-        for q in range(LAST):
-            if q in first_quad and q < LAST:
-                for q2 in range(q, first_quad[q]):
-                    mx_ya(q2)
-                    s_yacopy(q2)
-                    if q2 == 0:
-                        early_passes(5, (0, 1, 2, 3))
-            if q >= 1:
-                if q - 1 >= S_CHAIN_FROM:
-                    s_chain(q - 1, 0, QUAD)
-                else:
-                    s_rstd(q - 1, 0, QUAD)
-                    small(nc.gpsimd, q - 1, 0, QUAD)
-                s_act(q - 1, 0, QUAD)
-            if q == 0:
-                for i in range(4):
-                    v_add(0, i, i + 1, early[i][:].unsqueeze(1))
-                v_stats(0, 0, 4)
-                if S_CHAIN_FROM == 0:
-                    v_negmean(0, 0, QUAD)
-            else:
-                if q >= 2:
-                    mx_yp(q, 0, 2 + 2 * (q % 2))
-                add_stats(q, 0)
-                mx_yp(q, 1, 7 if q == 1 else 3 + 2 * (q % 2))
-                finish(q - TR_LAG)
-                add_stats(q, 1)
-                if q >= S_CHAIN_FROM:
-                    v_negmean(q, 0, QUAD)
-                if q < LAST - 1:
-                    v_max(q - 1, 0, QUAD)
-
-        q = LAST
-        accs = [bank(b, [P, NM, NV], F32, "yl_ps") for b in (4, 5, 2, 3)]
-        for i in range(QUAD):
-            for j in range(G0):
-                mx_pass(accs[i][:].rearrange("p m v -> p (m v)"), j, (QUAD * q + i) * P, j == 0, j == G0 - 1)
-        pe_tr(q - 3, 0, QUAD)
-        s_chain(q - 1, 0, QUAD)
-        s_act(q - 1, 0, QUAD)
-        for i in (0, 1):
-            v_add(q, i, i + 1, accs[i][:].unsqueeze(1))
-        v_stats(q, 0, 2)
-        v_negmean(q, 0, 2)
-        v_max(q - 2, 0, QUAD)
-        pe_tr(q - 2, 0, QUAD)
-        s_chain(q, 0, 2)
-        s_act(q, 0, 2)
-        for i in (2, 3):
-            v_add(q, i, i + 1, accs[i][:].unsqueeze(1))
-        v_stats(q, 2, 4)
-        v_negmean(q, 2, 4)
-        s_out(q - 3, 0, QUAD)
-        s_chain(q, 2, 4)
-        s_act(q, 2, 4)
-        v_max(q - 1, 0, QUAD)
-        pe_tr(q - 1, 0, QUAD)
-        s_out(q - 2, 0, QUAD, True)
+        quad_vs(1, ())
+        s_yacopy(2)
+        s_yacopy(3)
+        pe_tr(0, 0, 4, 7)
+        open_tiles(2, 0, (2, 3, 4, 5))
+        p_passes(2, 0, 4, (0, 1, 2, 3))
+        quad_vs(2, (0,))
+        pe_tr(1, 0, 4, 7)
+        open_tiles(3, 0, (6, 2, 3, 4))
+        p_passes(3, 0, 4, (0, 1, 2, 3))
+        quad_vs(3, (1,))
+        a_passes(4, 1)
+        a_passes(5, 0)
+        s_yacopy(4)
+        s_yacopy(5)
+        pe_tr(2, 0, 4, 7)
+        open_tiles(4, 0, (2, 3, 4, 5))
+        p_passes(4, 0, 4, (0, 1, 2, 3))
+        quad_vs(4, (2,))
+        pe_tr(3, 0, 4, 7)
+        open_tiles(5, 0, (6, 2, 3, 4))
+        p_passes(5, 0, 4, (0, 1, 2, 3))
+        quad_vs(5, (3,))
+        a_passes(6, 1)
+        s_yacopy(6)
+        pe_tr(4, 0, 4, 7)
+        open_tiles(6, 0, (2, 3, 4, 5))
+        p_passes(6, 0, 4, (0, 1, 2, 3))
+        a_passes(7, 0)
+        quad_vs(6, (4,))
+        s_yacopy(7, True)
+        open_tiles(7, 0, (6, 7, 1, 2))
+        p_passes(7, 0, 4, (0, 1, 2, 3))
+        pe_tr(5, 0, 4, 3)
+        pe_tr(6, 0, 4, 0)
+        q = 7
+        v_add(q, 0, 2)
+        v_nm(q, 0, 2)
+        s_var(q, 0, 2)
+        v_add(q, 2, 3)
+        v_shift(q, 0, 2)
+        v_add(q, 3, 4)
+        v_nm(q, 2, 4)
+        s_rstd(q, 0, 2)
+        s_var(q, 2, 4)
         v_max(q, 0, 2)
-        pe_tr(q, 0, 2)
+        v_shift(q, 2, 4)
         v_max(q, 2, 4)
-        pe_tr(q, 2, 4)
-        s_out(q - 1, 0, QUAD, True)
-        s_out(q, 0, 2)
-        s_out(q, 2, 4)
+        s_scale(q, 0, 2)
+        s_relu(q, 0, 2)
+        s_rstd(q, 2, 4)
+        s_scale(q, 2, 4)
+        s_relu(q, 2, 4)
+        copy_out(5, 0, 4)
+        store(5, 0, 4)
+        copy_out(6, 0, 4)
+        store(6, 0, 4)
+        pe_tr(q, 0, 2, 4)
+        copy_out(q, 0, 2)
+        store(q, 0, 2)
+        pe_tr(q, 2, 4, 4)
+        copy_out(q, 2, 4, False)
+        store(q, 2, 4)

@@ -23,7 +23,7 @@ EPS = 1e-3
 QUAD = 4
 NQ = C1 // (QUAD * P)
 
-REGROUP_ON_G = (0, 1)
+REGROUP_ON_G = ()
 LOADS = ((0, 1024, True), (0, 1024, False), (1024, 1024, False), (1024, 1024, True), (2048, 1024, False), (2048, 1024, True), (3072, 512, False), (3072, 512, True), (3584, 512, False), (3584, 512, True))
 TR_LAG = 3
 L0_ORDER = (0, 1, 4, 2, 5, 3, 6, 7)
@@ -127,7 +127,11 @@ def tile_vfe_w_kernel(tc, voxel_feats, W0, gamma0, beta0, W1_words, W1_scales, g
                 nc.tensor.transpose(wT_ps[:, t, :], w0_sb[:, g, t, :], ident_bf[:])
             if g == G0 - 1:
                 nc.tensor.transpose(wT_ps[:, 4, :], gb[:], ident_bf[:])
-            nc.scalar.copy(out=w0T[:, g], in_=wT_ps[:, 0:4, :])
+            if g == 0:
+                nc.vector.tensor_copy(out=w0T[:, g, 0:2], in_=wT_ps[:, 0:2, :])
+                nc.scalar.copy(out=w0T[:, g, 2:4], in_=wT_ps[:, 2:4, :])
+            else:
+                nc.scalar.copy(out=w0T[:, g], in_=wT_ps[:, 0:4, :])
             if g == G0 - 1:
                 nc.scalar.copy(out=gb1[:], in_=wT_ps[:, 4, 0:64])
                 nc.scalar.activation(out=sgn1[:], in_=wT_ps[:, 4, 0:32], func=ACT.Sign)
@@ -196,12 +200,11 @@ def tile_vfe_w_kernel(tc, voxel_feats, W0, gamma0, beta0, W1_words, W1_scales, g
                 in_=agr[:, g].rearrange("p r t -> p (r t)"),
             )
 
-        def l0_act2(g, t0):
-            for t in (t0, t0 + 1):
-                nc.scalar.activation(
-                    out=p_bf[:, g, t, :], in_=y0[(g, t // 2)][:, t % 2, :], func=ACT.Relu,
-                    bias=sh0[:, g, t : t + 1], scale=s0[:, g, t : t + 1],
-                )
+        def l0_act1(g, t):
+            nc.scalar.activation(
+                out=p_bf[:, g, t, :], in_=y0[(g, t // 2)][:, t % 2, :], func=ACT.Relu,
+                bias=sh0[:, g, t : t + 1], scale=s0[:, g, t : t + 1],
+            )
 
         def l0_ag(g):
             for t in range(4):
@@ -210,40 +213,60 @@ def tile_vfe_w_kernel(tc, voxel_feats, W0, gamma0, beta0, W1_words, W1_scales, g
         def l0_rstd(g):
             nc.scalar.activation(out=rstd0[:, g, :], in_=mv0[:, g, :, 1], func=ACT.Abs_reciprocal_sqrt, bias=eps_t[:])
 
-        for t in range(4):
-            l0_stat(0, t)
+        nm0 = keep.tile([P, G0, 4], F32)
+
+        def l0_rstd2(g):
+            nc.scalar.activation(out=rstd0[:, g : g + 2, :], in_=mv0[:, g : g + 2, :, 1], func=ACT.Abs_reciprocal_sqrt, bias=eps_t[:])
+
+        def l0_nm2(g):
+            pair = slice(g, g + 2)
+            nc.vector.tensor_tensor(out=nm0[:, pair, :], in0=mv0[:, pair, :, 0], in1=g0_sb[:, pair, :], op=ALU.mult)
+
+        def l0_small2(g):
+            pair = slice(g, g + 2)
+            nc.vector.tensor_tensor(out=ms0[:, pair, :], in0=nm0[:, pair, :], in1=rstd0[:, pair, :], op=ALU.mult)
+            nc.vector.tensor_tensor(out=s0[:, pair, :], in0=rstd0[:, pair, :], in1=g0_sb[:, pair, :], op=ALU.mult)
+            nc.vector.tensor_tensor(out=sh0[:, pair, :], in0=b0_sb[:, pair, :], in1=ms0[:, pair, :], op=ALU.subtract)
+
+        for g in (0, 1):
+            for t in range(4):
+                l0_stat(g, t)
         l0_ag(0)
-        l0_rstd(0)
-        for g in range(1, G0):
-            l0_stat(g, 0)
-            l0_stat(g, 1)
-            l0_small(g - 1, 0)
-            l0_stat(g, 2)
-            l0_small(g - 1, 1)
-            l0_stat(g, 3)
-            l0_small(g - 1, 2)
-            l0_ag(g)
-            l0_act2(g - 1, 0)
-            l0_rstd(g)
-            l0_act2(g - 1, 2)
-            if g - 1 in REGROUP_ON_G:
-                l0_regroup(g - 1)
+        l0_ag(1)
+        l0_rstd2(0)
+        l0_stat(2, 0)
+        l0_nm2(0)
+        l0_stat(2, 1)
+        l0_small2(0)
+        l0_act(0)
+        l0_act1(1, 0)
+        l0_stat(2, 2)
+        l0_stat(2, 3)
+        for t in range(4):
+            l0_stat(3, t)
+        l0_ag(2)
+        l0_ag(3)
+        l0_rstd2(2)
+        for t in range(1, 4):
+            l0_act1(1, t)
+        l0_regroup(0)
+        l0_nm2(2)
+        l0_small2(2)
         l0_quant_p(0)
-        l0_small(G0 - 1, 0)
         l0_max(0)
-        l0_small(G0 - 1, 1)
+        l0_act(2)
+        l0_act(3)
+        l0_regroup(1)
         l0_quant_a(0)
-        l0_small(G0 - 1, 2)
-        l0_act(G0 - 1)
         l0_quant_p(1)
-        l0_regroup(2)
         l0_max(1)
+        l0_regroup(2)
+        l0_quant_a(1)
         l0_quant_p(2)
         l0_max(2)
-        l0_quant_a(1)
-        l0_regroup(G0 - 1)
+        l0_regroup(3)
         l0_quant_a(2)
-        l0_quant_p(G0 - 1)
+        l0_quant_p(3)
         l0_max(3)
         l0_quant_a(3)
 

@@ -299,6 +299,10 @@ def tile_vfe_w_kernel(tc, voxel_feats, W0, gamma0, beta0, W1_words, W1_scales, g
                 for i in range(i0, i1):
                     mx_pass(st[("acc", q, i)][:].rearrange("p m v -> p (m v)"), j, (QUAD * q + i) * P, j == 0, j == G0 - 1)
 
+        def p_tiles(q, i0, i1):
+            for i in range(i0, i1):
+                p_passes(q, i, i + 1, (0, 1, 2, 3))
+
         def a_passes(q, b):
             ya_ps = bank(b, [P, QUAD, NV], F32, "ya_ps")
             st[("ya_ps", q)] = ya_ps
@@ -309,6 +313,8 @@ def tile_vfe_w_kernel(tc, voxel_feats, W0, gamma0, beta0, W1_words, W1_scales, g
         def s_yacopy(q, on_vector=False):
             st[("ya", q)] = work.tile([P, QUAD, NV], F32, name="ya_sb")
             st[("y", q)] = work.tile([P, QUAD, NM, NV], F32, name="y")
+            st[("st1", q)] = work.tile([P, QUAD, 6], F32, name="st1")
+            st[("mv1", q)] = work.tile([P, QUAD, 2], F32, name="mv1")
             for n in ("sum1", "nm1", "var1", "rstd1", "s1", "sh1"):
                 st[(n, q)] = work.tile([P, QUAD], F32, name=n)
             st[("zmax", q)] = work.tile([P, QUAD, NV], F32, name="zmax")
@@ -328,6 +334,32 @@ def tile_vfe_w_kernel(tc, voxel_feats, W0, gamma0, beta0, W1_words, W1_scales, g
                     in1=st[("ya", q)][:, i : i + 1, :].to_broadcast([P, NM, NV]),
                     op0=ALU.mult, op1=ALU.add, accum_out=st[("sum1", q)][:, i : i + 1],
                 )
+
+        def v_add_plain(q, i0, i1):
+            for i in range(i0, i1):
+                t = QUAD * q + i
+                nc.vector.scalar_tensor_tensor(
+                    out=st[("y", q)][:, i], in0=st[("acc", q, i)][:], scalar=sgn1[:, t : t + 1],
+                    in1=st[("ya", q)][:, i : i + 1, :].to_broadcast([P, NM, NV]),
+                    op0=ALU.mult, op1=ALU.add,
+                )
+
+        def v_bn(q, i0, i1):
+            for i in range(i0, i1):
+                nc.vector.bn_stats(out=st[("st1", q)][:, i, :], in_=st[("y", q)][:, i].rearrange("p m v -> p (m v)"))
+
+        def v_ag(q, i0, i1):
+            for i in range(i0, i1):
+                nc.vector.bn_aggr(out=st[("mv1", q)][:, i, :], in_=st[("st1", q)][:, i, :])
+
+        def s_rstd_bn(q, i0, i1):
+            nc.scalar.activation(out=st[("rstd1", q)][:, i0:i1], in_=st[("mv1", q)][:, i0:i1, 1], func=ACT.Abs_reciprocal_sqrt, bias=eps_t[:])
+
+        def v_shift_bn(q, i0, i1):
+            t0 = QUAD * q
+            nc.vector.scalar_tensor_tensor(
+                out=st[("s1", q)][:, i0:i1], in0=st[("mv1", q)][:, i0:i1, 0], scalar=-1.0, in1=agam1[:, t0 + i0 : t0 + i1], op0=ALU.mult, op1=ALU.mult
+            )
 
         def v_nm(q, i0, i1):
             nc.vector.tensor_scalar(out=st[("nm1", q)][:, i0:i1], in0=st[("sum1", q)][:, i0:i1], scalar1=-1.0 / (16 * ROWS), scalar2=None, op0=ALU.mult)
@@ -432,58 +464,63 @@ def tile_vfe_w_kernel(tc, voxel_feats, W0, gamma0, beta0, W1_words, W1_scales, g
         quad_vs(1, ())
         s_yacopy(2)
         s_yacopy(3)
-        pe_tr(0, 0, 4, 7)
         open_tiles(2, 0, (2, 3, 4, 5))
         p_passes(2, 0, 4, (0, 1, 2, 3))
-        quad_vs(2, (0,))
-        pe_tr(1, 0, 4, 7)
+        quad_vs(2, ())
         open_tiles(3, 0, (6, 2, 3, 4))
-        p_passes(3, 0, 4, (0, 1, 2, 3))
-        quad_vs(3, (1,))
+        p_tiles(3, 0, 4)
+        pe_tr(0, 0, 4, 7)
+        pe_tr(1, 0, 4, 5)
+        quad_vs(3, (0, 1))
         a_passes(4, 1)
         a_passes(5, 0)
-        s_yacopy(4)
-        s_yacopy(5)
+        s_yacopy(4, True)
+        s_yacopy(5, True)
         pe_tr(2, 0, 4, 7)
         open_tiles(4, 0, (2, 3, 4, 5))
         p_passes(4, 0, 4, (0, 1, 2, 3))
         quad_vs(4, (2,))
-        pe_tr(3, 0, 4, 7)
         open_tiles(5, 0, (6, 2, 3, 4))
-        p_passes(5, 0, 4, (0, 1, 2, 3))
-        quad_vs(5, (3,))
+        p_tiles(5, 0, 4)
         a_passes(6, 1)
-        s_yacopy(6)
-        pe_tr(4, 0, 4, 7)
-        open_tiles(6, 0, (2, 3, 4, 5))
+        quad_vs(5, ())
+        s_yacopy(6, True)
+        open_tiles(6, 0, (5, 2, 3, 4))
         p_passes(6, 0, 4, (0, 1, 2, 3))
+        pe_tr(3, 0, 4, 7)
+        pe_tr(4, 0, 4, 1)
+        quad_vs(6, ())
+        copy_out(3, 0, 4)
+        store(3, 0, 4)
         a_passes(7, 0)
-        quad_vs(6, (4,))
         s_yacopy(7, True)
-        open_tiles(7, 0, (6, 7, 1, 2))
+        copy_out(4, 0, 4)
+        store(4, 0, 4)
+        open_tiles(7, 0, (6, 5, 2, 3))
         p_passes(7, 0, 4, (0, 1, 2, 3))
-        pe_tr(5, 0, 4, 3)
-        pe_tr(6, 0, 4, 0)
+        pe_tr(5, 0, 4, 7)
+        pe_tr(6, 0, 4, 1)
         q = 7
-        v_add(q, 0, 2)
-        v_nm(q, 0, 2)
-        s_var(q, 0, 2)
-        v_add(q, 2, 3)
-        v_shift(q, 0, 2)
-        v_add(q, 3, 4)
-        v_nm(q, 2, 4)
-        s_rstd(q, 0, 2)
-        s_var(q, 2, 4)
-        v_max(q, 0, 2)
-        v_shift(q, 2, 4)
-        v_max(q, 2, 4)
-        s_scale(q, 0, 2)
-        s_relu(q, 0, 2)
-        s_rstd(q, 2, 4)
-        s_scale(q, 2, 4)
-        s_relu(q, 2, 4)
-        copy_out(5, 0, 4)
+        copy_out(5, 0, 4, False)
         store(5, 0, 4)
+        v_add(q, 0, 2)
+        v_nm(q, 0, 1)
+        v_add_plain(q, 2, 3)
+        v_nm(q, 1, 2)
+        v_add_plain(q, 3, 4)
+        s_var(q, 0, 2)
+        v_bn(q, 2, 4)
+        v_shift(q, 0, 2)
+        v_ag(q, 2, 4)
+        v_max(q, 0, 2)
+        v_shift_bn(q, 2, 4)
+        v_max(q, 2, 4)
+        s_rstd(q, 0, 2)
+        s_rstd_bn(q, 2, 4)
+        s_scale(q, 0, 2)
+        s_scale(q, 2, 4)
+        s_relu(q, 0, 2)
+        s_relu(q, 2, 4)
         copy_out(6, 0, 4)
         store(6, 0, 4)
         pe_tr(q, 0, 2, 4)

@@ -52,6 +52,8 @@ def tile_vfe_w_kernel(tc, voxel_feats, W0, gamma0, beta0, W1_words, W1_scales, g
         nc.vector.tensor_scalar(out=eps_t[:], in0=zero_t[:], scalar1=EPS, scalar2=None, op0=ALU.add)
         gb = keep.tile([P, P], BF16)
         nc.vector.memset(gb[:], 0.0)
+        gb0 = keep.tile([P, 512], BF16)
+        nc.vector.memset(gb0[:], 0.0)
         planes = keep.tile([P, 2, C1], U8, align_bytes=64)
         nc.vector.memset(planes[:].bitcast(I32), 0)
         ident_bf = keep.tile([P, P], BF16)
@@ -65,6 +67,8 @@ def tile_vfe_w_kernel(tc, voxel_feats, W0, gamma0, beta0, W1_words, W1_scales, g
         ident_f = keep.tile([P, P], F32)
         make_identity(nc, ident_f[:])
 
+        warm = keep.tile([P, 1], F32)
+        nc.scalar.activation(out=warm[:], in_=eps_t[:], func=ACT.Abs_reciprocal_sqrt)
         vox_sb = keep.tile([P, NM, 128], BF16)
         nc.sync.dma_start(out=vox_sb[:], in_=voxel_feats)
         w0_sb = keep.tile([P, G0, 4, 128], BF16)
@@ -73,15 +77,12 @@ def tile_vfe_w_kernel(tc, voxel_feats, W0, gamma0, beta0, W1_words, W1_scales, g
             nc.sync.dma_start(out=w0_sb[:, g], in_=w0_view[:, g])
         nc.scalar.dma_start(out=gb[0:32, :], in_=gamma1.rearrange("(t p) -> t p", p=P))
         nc.scalar.dma_start(out=gb[32:64, :], in_=beta1.rearrange("(t p) -> t p", p=P))
-        g0_sb = keep.tile([P, G0, 4], BF16)
-        nc.scalar.dma_start(out=g0_sb[:], in_=gamma0.rearrange("(g p t) -> p g t", g=G0, p=P, t=4))
-        b0_sb = keep.tile([P, G0, 4], BF16)
-        nc.scalar.dma_start(out=b0_sb[:], in_=beta0.rearrange("(g p t) -> p g t", g=G0, p=P, t=4))
-        warm = keep.tile([P, 1], F32)
-        nc.scalar.activation(out=warm[:], in_=eps_t[:], func=ACT.Abs_reciprocal_sqrt)
         words = {}
         for lo, width, top in LOADS:
             for j in range(G0):
+                if lo == 0 and top and j == 1:
+                    nc.scalar.dma_start(out=gb0[0:4, :], in_=gamma0.rearrange("(g x) -> g x", g=G0))
+                    nc.scalar.dma_start(out=gb0[4:8, :], in_=beta0.rearrange("(g x) -> g x", g=G0))
                 g = j if top else G0 + j
                 wt = keep.tile([P, width], I32, name="w_%d_%d" % (lo, g), align_bytes=64)
                 nc.sync.dma_start(
@@ -144,7 +145,20 @@ def tile_vfe_w_kernel(tc, voxel_feats, W0, gamma0, beta0, W1_words, W1_scales, g
                 for u in range(2):
                     nc.tensor.matmul(out=yt[:, u, :], lhsT=w0T[:, g, 2 * half + u, :], rhs=xT[:], start=True, stop=True)
 
+        gb0T = keep.tile([P, 2, G0, 4], BF16)
+        g0_sb = gb0T[:, 0]
+        b0_sb = gb0T[:, 1]
+
+        def gb0_transposes():
+            gT_ps = bank(1, [P, 4, P], BF16, "gT_ps")
+            rows = gb0[:].rearrange("r (p t) -> r t p", t=4)
+            for t in range(4):
+                nc.tensor.transpose(gT_ps[:, t, :], rows[:, t, :], ident_bf[:])
+            nc.scalar.copy(out=gb0T[:].rearrange("p s g t -> p (s g) t"), in_=gT_ps[:, :, 0:8].rearrange("p t r -> p r t"))
+
         for step in L0_ORDER:
+            if step == 7:
+                gb0_transposes()
             if step < G0:
                 w0_transposes(step)
             else:
@@ -253,9 +267,9 @@ def tile_vfe_w_kernel(tc, voxel_feats, W0, gamma0, beta0, W1_words, W1_scales, g
         l0_nm2(2)
         l0_small2(2)
         l0_quant_p(0)
-        l0_max(0)
         l0_act(2)
         l0_act(3)
+        l0_max(0)
         l0_regroup(1)
         l0_quant_a(0)
         l0_quant_p(1)
@@ -263,11 +277,11 @@ def tile_vfe_w_kernel(tc, voxel_feats, W0, gamma0, beta0, W1_words, W1_scales, g
         l0_regroup(2)
         l0_quant_a(1)
         l0_quant_p(2)
-        l0_max(2)
         l0_regroup(3)
-        l0_quant_a(2)
+        l0_max(2)
         l0_quant_p(3)
         l0_max(3)
+        l0_quant_a(2)
         l0_quant_a(3)
 
         o_sb = keep.tile([P, C1], F32)
@@ -462,8 +476,8 @@ def tile_vfe_w_kernel(tc, voxel_feats, W0, gamma0, beta0, W1_words, W1_scales, g
             s_relu(q, 0, 4)
 
         quad_vs(1, ())
-        s_yacopy(2)
-        s_yacopy(3)
+        s_yacopy(2, True)
+        s_yacopy(3, True)
         open_tiles(2, 0, (2, 3, 4, 5))
         p_passes(2, 0, 4, (0, 1, 2, 3))
         quad_vs(2, ())

@@ -24,7 +24,7 @@ QUAD = 4
 NQ = C1 // (QUAD * P)
 
 REGROUP_ON_G = ()
-LOADS = ((0, 1024, True), (0, 1024, False), (1024, 1024, False), (1024, 1024, True), (2048, 1024, False), (2048, 1024, True), (3072, 512, False), (3072, 512, True), (3584, 512, False), (3584, 512, True))
+LOADS = ((0, 1024, True), (0, 1024, False), (1024, 1024, False), (1024, 1024, True), (2048, 1024, False), (2048, 1024, True), (3072, 512, False), (3072, 512, True), (3584, 512, False), (3584, 256, True), (3840, 256, True))
 TR_LAG = 3
 L0_ORDER = (0, 1, 4, 2, 5, 3, 6, 7)
 S_CHAIN_FROM = 0
@@ -415,6 +415,28 @@ def tile_vfe_w_kernel(tc, voxel_feats, W0, gamma0, beta0, W1_words, W1_scales, g
                     bias=st[("sh1", q)][:, i : i + 1], scale=st[("var1", q)][:, i : i + 1],
                 )
 
+        def v_scale(q, i0, i1):
+            t0 = QUAD * q
+            rstd1, s1, sh1, var1 = st[("rstd1", q)], st[("s1", q)], st[("sh1", q)], st[("var1", q)]
+            nc.vector.tensor_tensor(out=s1[:, i0:i1], in0=rstd1[:, i0:i1], in1=s1[:, i0:i1], op=ALU.mult)
+            nc.vector.tensor_tensor(out=var1[:, i0:i1], in0=rstd1[:, i0:i1], in1=agam1[:, t0 + i0 : t0 + i1], op=ALU.mult)
+            nc.vector.tensor_tensor(out=sh1[:, i0:i1], in0=s1[:, i0:i1], in1=gb1[:, 32 + t0 + i0 : 32 + t0 + i1], op=ALU.add)
+
+        def v_affine(q, i0, i1):
+            for i in range(i0, i1):
+                nc.vector.tensor_scalar(
+                    out=st[("z", q)][:, i, :], in0=st[("zmax", q)][:, i, :],
+                    scalar1=st[("var1", q)][:, i : i + 1], scalar2=st[("sh1", q)][:, i : i + 1], op0=ALU.mult, op1=ALU.add,
+                )
+
+        def relu_out(q, i0, i1, on_vector=True):
+            cols = slice((QUAD * q + i0) * P, (QUAD * q + i1) * P)
+            src = st[("tr_ps", q)][:, i0:i1, :].rearrange("v i n -> v (i n)")
+            if on_vector:
+                nc.vector.tensor_scalar(out=o_sb[:, cols], in0=src, scalar1=0.0, scalar2=None, op0=ALU.max)
+            else:
+                nc.scalar.activation(out=o_sb[:, cols], in_=src, func=ACT.Relu)
+
         def pe_tr(q, i0, i1, b):
             if i0 == 0:
                 st[("tr_ps", q)] = bank(b, [P, QUAD, P], F32, "tr_ps")
@@ -511,30 +533,35 @@ def tile_vfe_w_kernel(tc, voxel_feats, W0, gamma0, beta0, W1_words, W1_scales, g
         copy_out(4, 0, 4)
         store(4, 0, 4)
         open_tiles(7, 0, (6, 5, 2, 3))
-        p_passes(7, 0, 4, (0, 1, 2, 3))
+        p_passes(7, 0, 2, (0, 1, 2, 3))
+        p_passes(7, 2, 3, (0, 1, 2))
+        p_passes(7, 3, 4, (0, 1))
+        p_passes(7, 2, 3, (3,))
+        p_passes(7, 3, 4, (2, 3))
         pe_tr(5, 0, 4, 7)
         pe_tr(6, 0, 4, 1)
         q = 7
-        copy_out(5, 0, 4, False)
-        store(5, 0, 4)
         v_add(q, 0, 2)
         v_nm(q, 0, 1)
         v_add_plain(q, 2, 3)
         v_nm(q, 1, 2)
         v_add_plain(q, 3, 4)
         s_var(q, 0, 2)
-        v_bn(q, 2, 4)
+        copy_out(5, 0, 4, False)
+        store(5, 0, 4)
         v_shift(q, 0, 2)
-        v_ag(q, 2, 4)
+        v_bn(q, 2, 4)
         v_max(q, 0, 2)
+        v_ag(q, 2, 4)
+        v_max(q, 2, 3)
         v_shift_bn(q, 2, 4)
-        v_max(q, 2, 4)
+        v_max(q, 3, 4)
         s_rstd(q, 0, 2)
-        s_rstd_bn(q, 2, 4)
         s_scale(q, 0, 2)
+        s_rstd_bn(q, 2, 4)
+        s_relu(q, 0, 1)
         s_scale(q, 2, 4)
-        s_relu(q, 0, 2)
-        s_relu(q, 2, 4)
+        s_relu(q, 1, 4)
         copy_out(6, 0, 4)
         store(6, 0, 4)
         pe_tr(q, 0, 2, 4)

@@ -306,12 +306,43 @@ def tile_vfe_w_kernel(tc, voxel_feats, W0, gamma0, beta0, W1_words, W1_scales, g
 
         def open_tiles(q, i0, banks):
             for k, b in enumerate(banks):
-                st[("acc", q, i0 + k)] = bank(b, [P, NM, NV], F32, "yp_ps")
+                st[("acc", q, i0 + k)] = bank(b, [P, NM, NV], F32, "yp_ps")[:]
 
         def p_passes(q, i0, i1, js):
             for j in js:
                 for i in range(i0, i1):
-                    mx_pass(st[("acc", q, i)][:].rearrange("p m v -> p (m v)"), j, (QUAD * q + i) * P, j == 0, j == G0 - 1)
+                    mx_pass(st[("acc", q, i)].rearrange("p m v -> p (m v)"), j, (QUAD * q + i) * P, j == 0, j == G0 - 1)
+
+        def open_closed_pairs(q, banks):
+            for h, b in enumerate(banks):
+                pair = bank(b, [P, 2, NM, NV], F32, "yp_ps")
+                st[("acc", q, 2 * h)] = pair[:, 0]
+                st[("acc", q, 2 * h + 1)] = pair[:, 1]
+
+        def open_pair(q, i0, b):
+            pair = bank(b, [P, 2, NM, NV], F32, "yp_ps")
+            for k in range(2):
+                st[("acc", q, i0 + k)] = pair[:, k]
+                st[("first", q, i0 + k)] = k == 0
+
+        def open_a(q, b):
+            st[("ya_ps", q)] = bank(b, [P, QUAD, NV], F32, "ya_ps")
+
+        def a_group(q, js):
+            for j in js:
+                for i in range(QUAD):
+                    mx_pass(
+                        st[("ya_ps", q)][:, i, :], G0 + j, (QUAD * q + i) * P,
+                        j == 0 and i == 0, j == G0 - 1 and i == QUAD - 1,
+                    )
+
+        def pair_passes(q, i0, js):
+            for j in js:
+                for k in range(2):
+                    mx_pass(
+                        st[("acc", q, i0 + k)].rearrange("p m v -> p (m v)"), j, (QUAD * q + i0 + k) * P,
+                        j == 0 and k == 0, j == G0 - 1 and k == 1,
+                    )
 
         def p_tiles(q, i0, i1):
             for i in range(i0, i1):
@@ -344,7 +375,7 @@ def tile_vfe_w_kernel(tc, voxel_feats, W0, gamma0, beta0, W1_words, W1_scales, g
             for i in range(i0, i1):
                 t = QUAD * q + i
                 nc.vector.scalar_tensor_tensor(
-                    out=st[("y", q)][:, i], in0=st[("acc", q, i)][:], scalar=sgn1[:, t : t + 1],
+                    out=st[("y", q)][:, i], in0=st[("acc", q, i)], scalar=sgn1[:, t : t + 1],
                     in1=st[("ya", q)][:, i : i + 1, :].to_broadcast([P, NM, NV]),
                     op0=ALU.mult, op1=ALU.add, accum_out=st[("sum1", q)][:, i : i + 1],
                 )
@@ -353,7 +384,7 @@ def tile_vfe_w_kernel(tc, voxel_feats, W0, gamma0, beta0, W1_words, W1_scales, g
             for i in range(i0, i1):
                 t = QUAD * q + i
                 nc.vector.scalar_tensor_tensor(
-                    out=st[("y", q)][:, i], in0=st[("acc", q, i)][:], scalar=sgn1[:, t : t + 1],
+                    out=st[("y", q)][:, i], in0=st[("acc", q, i)], scalar=sgn1[:, t : t + 1],
                     in1=st[("ya", q)][:, i : i + 1, :].to_broadcast([P, NM, NV]),
                     op0=ALU.mult, op1=ALU.add,
                 )
@@ -442,6 +473,15 @@ def tile_vfe_w_kernel(tc, voxel_feats, W0, gamma0, beta0, W1_words, W1_scales, g
                 st[("tr_ps", q)] = bank(b, [P, QUAD, P], F32, "tr_ps")
             for i in range(i0, i1):
                 nc.tensor.transpose(st[("tr_ps", q)][:, i, :], st[("z", q)][:, i, :], ident_f[:])
+
+        def pe_tr2(q, i0, i1, b):
+            st[("tr2_ps", q)] = bank(b, [P, QUAD, P], F32, "tr_ps")
+            for i in range(i0, i1):
+                nc.tensor.transpose(st[("tr2_ps", q)][:, i, :], st[("z", q)][:, i, :], ident_f[:])
+
+        def copy_out2(q, i0, i1, on_vector):
+            cols = slice((QUAD * q + i0) * P, (QUAD * q + i1) * P)
+            nc.scalar.copy(out=o_sb[:, cols], in_=st[("tr2_ps", q)][:, i0:i1, :].rearrange("v i n -> v (i n)"))
 
         def copy_out(q, i0, i1, on_vector=True):
             cols = slice((QUAD * q + i0) * P, (QUAD * q + i1) * P)
@@ -567,6 +607,6 @@ def tile_vfe_w_kernel(tc, voxel_feats, W0, gamma0, beta0, W1_words, W1_scales, g
         pe_tr(q, 0, 2, 4)
         copy_out(q, 0, 2)
         store(q, 0, 2)
-        pe_tr(q, 2, 4, 4)
-        copy_out(q, 2, 4, False)
+        pe_tr2(q, 2, 4, 0)
+        copy_out2(q, 2, 4, False)
         store(q, 2, 4)

@@ -228,13 +228,20 @@ def tile_vfe_w_kernel(tc, voxel_feats, W0, gamma0, beta0, W1_words, W1_scales, g
             nc.scalar.activation(out=rstd0[:, g, :], in_=mv0[:, g, :, 1], func=ACT.Abs_reciprocal_sqrt, bias=eps_t[:])
 
         nm0 = keep.tile([P, G0, 4], F32)
+        st0p = keep.tile([P, 2 * G0, 2, 3], F32)
+
+        def l0_stat2(g, h):
+            nc.vector.bn_stats(out=st0p[:, 2 * g + h].rearrange("p u s -> p (u s)"), in_=y0[(g, h)][:].rearrange("p u r -> p r u"))
 
         def l0_rstd2(g):
-            nc.scalar.activation(out=rstd0[:, g : g + 2, :], in_=mv0[:, g : g + 2, :, 1], func=ACT.Abs_reciprocal_sqrt, bias=eps_t[:])
+            nc.scalar.activation(
+                out=rstd0[:, g : g + 2, :].rearrange("p g (h u) -> p (g h) u", u=2), in_=st0p[:, 2 * g : 2 * g + 4, :, 2],
+                func=ACT.Abs_reciprocal_sqrt, scale=1.0 / ROWS, bias=eps_t[:],
+            )
 
         def l0_nm2(g):
             pair = slice(g, g + 2)
-            nc.vector.tensor_tensor(out=nm0[:, pair, :], in0=mv0[:, pair, :, 0], in1=g0_sb[:, pair, :], op=ALU.mult)
+            nc.vector.tensor_tensor(out=nm0[:, pair, :].rearrange("p g (h u) -> p (g h) u", u=2), in0=st0p[:, 2 * g : 2 * g + 4, :, 1], in1=g0_sb[:, pair, :].rearrange("p g (h u) -> p (g h) u", u=2), op=ALU.mult)
 
         def l0_small2(g):
             pair = slice(g, g + 2)
@@ -243,28 +250,22 @@ def tile_vfe_w_kernel(tc, voxel_feats, W0, gamma0, beta0, W1_words, W1_scales, g
             nc.vector.tensor_tensor(out=sh0[:, pair, :], in0=b0_sb[:, pair, :], in1=ms0[:, pair, :], op=ALU.subtract)
 
         for g in (0, 1):
-            for t in range(4):
-                l0_stat(g, t)
-        l0_ag(0)
-        l0_ag(1)
+            for h in (0, 1):
+                l0_stat2(g, h)
         l0_rstd2(0)
-        l0_stat(2, 0)
+        l0_stat2(2, 0)
         l0_nm2(0)
-        l0_stat(2, 1)
         l0_small2(0)
         l0_act(0)
         l0_act1(1, 0)
-        l0_stat(2, 2)
-        l0_stat(2, 3)
-        for t in range(4):
-            l0_stat(3, t)
-        l0_ag(2)
-        l0_ag(3)
+        l0_stat2(2, 1)
+        l0_stat2(3, 0)
+        l0_stat2(3, 1)
         l0_rstd2(2)
         for t in range(1, 4):
             l0_act1(1, t)
-        l0_regroup(0)
         l0_nm2(2)
+        l0_regroup(0)
         l0_small2(2)
         l0_quant_p(0)
         l0_act(2)
@@ -360,6 +361,7 @@ def tile_vfe_w_kernel(tc, voxel_feats, W0, gamma0, beta0, W1_words, W1_scales, g
             st[("y", q)] = work.tile([P, QUAD, NM, NV], F32, name="y")
             st[("st1", q)] = work.tile([P, QUAD, 6], F32, name="st1")
             st[("mv1", q)] = work.tile([P, QUAD, 2], F32, name="mv1")
+            st[("bn2", q)] = work.tile([P, 2, 3], F32, name="bn2")
             for n in ("sum1", "nm1", "var1", "rstd1", "s1", "sh1"):
                 st[(n, q)] = work.tile([P, QUAD], F32, name=n)
             st[("zmax", q)] = work.tile([P, QUAD, NV], F32, name="zmax")
@@ -392,6 +394,23 @@ def tile_vfe_w_kernel(tc, voxel_feats, W0, gamma0, beta0, W1_words, W1_scales, g
         def v_bn(q, i0, i1):
             for i in range(i0, i1):
                 nc.vector.bn_stats(out=st[("st1", q)][:, i, :], in_=st[("y", q)][:, i].rearrange("p m v -> p (m v)"))
+
+        def v_bn2(q):
+            nc.vector.bn_stats(
+                out=st[("bn2", q)][:].rearrange("p u s -> p (u s)"),
+                in_=st[("y", q)][:, 2:4].rearrange("p u m v -> p (m v) u"),
+            )
+
+        def s_rstd_bn2(q):
+            nc.scalar.activation(
+                out=st[("rstd1", q)][:, 2:4], in_=st[("bn2", q)][:, :, 2], func=ACT.Abs_reciprocal_sqrt, scale=1.0 / ROWS, bias=eps_t[:]
+            )
+
+        def v_shift_bn2(q):
+            t0 = QUAD * q
+            nc.vector.scalar_tensor_tensor(
+                out=st[("s1", q)][:, 2:4], in0=st[("bn2", q)][:, :, 1], scalar=-1.0, in1=agam1[:, t0 + 2 : t0 + 4], op0=ALU.mult, op1=ALU.mult
+            )
 
         def v_ag(q, i0, i1):
             for i in range(i0, i1):
@@ -590,15 +609,14 @@ def tile_vfe_w_kernel(tc, voxel_feats, W0, gamma0, beta0, W1_words, W1_scales, g
         copy_out(5, 0, 4, False)
         store(5, 0, 4)
         v_shift(q, 0, 2)
-        v_bn(q, 2, 4)
         v_max(q, 0, 2)
-        v_ag(q, 2, 4)
+        v_bn2(q)
         v_max(q, 2, 3)
-        v_shift_bn(q, 2, 4)
+        v_shift_bn2(q)
         v_max(q, 3, 4)
         s_rstd(q, 0, 2)
         s_scale(q, 0, 2)
-        s_rstd_bn(q, 2, 4)
+        s_rstd_bn2(q)
         s_relu(q, 0, 1)
         s_scale(q, 2, 4)
         s_relu(q, 1, 4)

@@ -314,37 +314,6 @@ def tile_vfe_w_kernel(tc, voxel_feats, W0, gamma0, beta0, W1_words, W1_scales, g
                 for i in range(i0, i1):
                     mx_pass(st[("acc", q, i)].rearrange("p m v -> p (m v)"), j, (QUAD * q + i) * P, j == 0, j == G0 - 1)
 
-        def open_closed_pairs(q, banks):
-            for h, b in enumerate(banks):
-                pair = bank(b, [P, 2, NM, NV], F32, "yp_ps")
-                st[("acc", q, 2 * h)] = pair[:, 0]
-                st[("acc", q, 2 * h + 1)] = pair[:, 1]
-
-        def open_pair(q, i0, b):
-            pair = bank(b, [P, 2, NM, NV], F32, "yp_ps")
-            for k in range(2):
-                st[("acc", q, i0 + k)] = pair[:, k]
-                st[("first", q, i0 + k)] = k == 0
-
-        def open_a(q, b):
-            st[("ya_ps", q)] = bank(b, [P, QUAD, NV], F32, "ya_ps")
-
-        def a_group(q, js):
-            for j in js:
-                for i in range(QUAD):
-                    mx_pass(
-                        st[("ya_ps", q)][:, i, :], G0 + j, (QUAD * q + i) * P,
-                        j == 0 and i == 0, j == G0 - 1 and i == QUAD - 1,
-                    )
-
-        def pair_passes(q, i0, js):
-            for j in js:
-                for k in range(2):
-                    mx_pass(
-                        st[("acc", q, i0 + k)].rearrange("p m v -> p (m v)"), j, (QUAD * q + i0 + k) * P,
-                        j == 0 and k == 0, j == G0 - 1 and k == 1,
-                    )
-
         def p_tiles(q, i0, i1):
             for i in range(i0, i1):
                 p_passes(q, i, i + 1, (0, 1, 2, 3))
@@ -359,10 +328,8 @@ def tile_vfe_w_kernel(tc, voxel_feats, W0, gamma0, beta0, W1_words, W1_scales, g
         def s_yacopy(q, on_vector=False):
             st[("ya", q)] = work.tile([P, QUAD, NV], F32, name="ya_sb")
             st[("y", q)] = work.tile([P, QUAD, NM, NV], F32, name="y")
-            st[("st1", q)] = work.tile([P, QUAD, 6], F32, name="st1")
-            st[("mv1", q)] = work.tile([P, QUAD, 2], F32, name="mv1")
             st[("bn2", q)] = work.tile([P, 2, 3], F32, name="bn2")
-            for n in ("sum1", "nm1", "var1", "rstd1", "s1", "sh1"):
+            for n in ("sum1", "nm1", "m2", "rstd1"):
                 st[(n, q)] = work.tile([P, QUAD], F32, name=n)
             st[("zmax", q)] = work.tile([P, QUAD, NV], F32, name="zmax")
             st[("z", q)] = work.tile([P, QUAD, NV], F32, name="z")
@@ -373,119 +340,69 @@ def tile_vfe_w_kernel(tc, voxel_feats, W0, gamma0, beta0, W1_words, W1_scales, g
                 else:
                     nc.scalar.activation(out=st[("ya", q)][:, i, :], in_=st[("ya_ps", q)][:, i, :], func=ACT.Copy, scale=sgn1[:, t : t + 1])
 
-        def v_add(q, i0, i1):
+        def v_add(q, i0, i1, with_sum=True):
             for i in range(i0, i1):
                 t = QUAD * q + i
                 nc.vector.scalar_tensor_tensor(
                     out=st[("y", q)][:, i], in0=st[("acc", q, i)], scalar=sgn1[:, t : t + 1],
                     in1=st[("ya", q)][:, i : i + 1, :].to_broadcast([P, NM, NV]),
-                    op0=ALU.mult, op1=ALU.add, accum_out=st[("sum1", q)][:, i : i + 1],
+                    op0=ALU.mult, op1=ALU.add, accum_out=st[("sum1", q)][:, i : i + 1] if with_sum else None,
                 )
 
-        def v_add_plain(q, i0, i1):
-            for i in range(i0, i1):
-                t = QUAD * q + i
-                nc.vector.scalar_tensor_tensor(
-                    out=st[("y", q)][:, i], in0=st[("acc", q, i)], scalar=sgn1[:, t : t + 1],
-                    in1=st[("ya", q)][:, i : i + 1, :].to_broadcast([P, NM, NV]),
-                    op0=ALU.mult, op1=ALU.add,
-                )
-
-        def v_bn(q, i0, i1):
-            for i in range(i0, i1):
-                nc.vector.bn_stats(out=st[("st1", q)][:, i, :], in_=st[("y", q)][:, i].rearrange("p m v -> p (m v)"))
-
-        def v_bn2(q):
-            nc.vector.bn_stats(
-                out=st[("bn2", q)][:].rearrange("p u s -> p (u s)"),
-                in_=st[("y", q)][:, 2:4].rearrange("p u m v -> p (m v) u"),
-            )
-
-        def s_rstd_bn2(q):
-            nc.scalar.activation(
-                out=st[("rstd1", q)][:, 2:4], in_=st[("bn2", q)][:, :, 2], func=ACT.Abs_reciprocal_sqrt, scale=1.0 / ROWS, bias=eps_t[:]
-            )
-
-        def v_shift_bn2(q):
-            t0 = QUAD * q
-            nc.vector.scalar_tensor_tensor(
-                out=st[("s1", q)][:, 2:4], in0=st[("bn2", q)][:, :, 1], scalar=-1.0, in1=agam1[:, t0 + 2 : t0 + 4], op0=ALU.mult, op1=ALU.mult
-            )
-
-        def v_ag(q, i0, i1):
-            for i in range(i0, i1):
-                nc.vector.bn_aggr(out=st[("mv1", q)][:, i, :], in_=st[("st1", q)][:, i, :])
-
-        def s_rstd_bn(q, i0, i1):
-            nc.scalar.activation(out=st[("rstd1", q)][:, i0:i1], in_=st[("mv1", q)][:, i0:i1, 1], func=ACT.Abs_reciprocal_sqrt, bias=eps_t[:])
-
-        def v_shift_bn(q, i0, i1):
-            t0 = QUAD * q
-            nc.vector.scalar_tensor_tensor(
-                out=st[("s1", q)][:, i0:i1], in0=st[("mv1", q)][:, i0:i1, 0], scalar=-1.0, in1=agam1[:, t0 + i0 : t0 + i1], op0=ALU.mult, op1=ALU.mult
-            )
-
-        def v_nm(q, i0, i1):
-            nc.vector.tensor_scalar(out=st[("nm1", q)][:, i0:i1], in0=st[("sum1", q)][:, i0:i1], scalar1=-1.0 / (16 * ROWS), scalar2=None, op0=ALU.mult)
+        def v_negmean(q, i0, i1):
+            nc.vector.tensor_scalar(out=st[("nm1", q)][:, i0:i1], in0=st[("sum1", q)][:, i0:i1], scalar1=-1.0 / ROWS, scalar2=None, op0=ALU.mult)
 
         def v_max(q, i0, i1):
             y = st[("y", q)]
             nc.vector.tensor_tensor(out=st[("zmax", q)][:, i0:i1], in0=y[:, i0:i1, 0, :], in1=y[:, i0:i1, 1, :], op=ALU.max)
 
-        def s_var(q, i0, i1):
+        def v_center(q, i0, i1):
+            for i in range(i0, i1):
+                t = QUAD * q + i
+                nc.vector.tensor_scalar(
+                    out=st[("zmax", q)][:, i, :], in0=st[("zmax", q)][:, i, :],
+                    scalar1=st[("nm1", q)][:, i : i + 1], scalar2=agam1[:, t : t + 1], op0=ALU.add, op1=ALU.mult,
+                )
+
+        def s_squares(q, i0, i1):
             for i in range(i0, i1):
                 junk = work.tile([P, ROWS], BF16, name="junk")
                 nc.scalar.activation(
                     out=junk[:], in_=st[("y", q)][:, i].rearrange("p m v -> p (m v)"), func=ACT.Square,
-                    scale=1.0 / 16, bias=st[("nm1", q)][:, i : i + 1], accum_out=st[("var1", q)][:, i : i + 1],
+                    bias=st[("nm1", q)][:, i : i + 1], accum_out=st[("m2", q)][:, i : i + 1],
                 )
 
         def s_rstd(q, i0, i1):
-            nc.scalar.activation(out=st[("rstd1", q)][:, i0:i1], in_=st[("var1", q)][:, i0:i1], func=ACT.Abs_reciprocal_sqrt, bias=eps_t[:])
-
-        def v_shift(q, i0, i1):
-            t0 = QUAD * q
-            nc.vector.scalar_tensor_tensor(
-                out=st[("s1", q)][:, i0:i1], in0=st[("nm1", q)][:, i0:i1], scalar=16.0, in1=agam1[:, t0 + i0 : t0 + i1], op0=ALU.mult, op1=ALU.mult
+            nc.scalar.activation(
+                out=st[("rstd1", q)][:, i0:i1], in_=st[("m2", q)][:, i0:i1], func=ACT.Abs_reciprocal_sqrt, scale=1.0 / ROWS, bias=eps_t[:]
             )
 
-        def s_scale(q, i0, i1):
-            for i in range(i0, i1):
-                t = QUAD * q + i
-                nc.scalar.activation(
-                    out=st[("sh1", q)][:, i : i + 1], in_=st[("rstd1", q)][:, i : i + 1], func=ACT.Identity,
-                    scale=st[("s1", q)][:, i : i + 1], bias=gb1[:, 32 + t : 33 + t],
+        def v_stats_pair(q):
+            nc.vector.bn_stats(
+                out=st[("bn2", q)][:].rearrange("p u s -> p (u s)"),
+                in_=st[("y", q)][:, 2:4].rearrange("p u m v -> p (m v) u"),
+            )
+
+        def s_rstd_pair(q):
+            nc.scalar.activation(
+                out=st[("rstd1", q)][:, 2:4], in_=st[("bn2", q)][:, :, 2], func=ACT.Abs_reciprocal_sqrt, scale=1.0 / ROWS, bias=eps_t[:]
+            )
+
+        def v_center_pair(q):
+            for u in range(2):
+                t = QUAD * q + 2 + u
+                nc.vector.tensor_scalar(
+                    out=st[("zmax", q)][:, 2 + u, :], in0=st[("zmax", q)][:, 2 + u, :],
+                    scalar1=st[("bn2", q)][:, u, 1:2], scalar2=agam1[:, t : t + 1], op0=ALU.subtract, op1=ALU.mult,
                 )
-                nc.scalar.activation(out=st[("var1", q)][:, i : i + 1], in_=st[("rstd1", q)][:, i : i + 1], func=ACT.Copy, scale=agam1[:, t : t + 1])
 
         def s_relu(q, i0, i1):
             for i in range(i0, i1):
+                t = QUAD * q + i
                 nc.scalar.activation(
                     out=st[("z", q)][:, i, :], in_=st[("zmax", q)][:, i, :], func=ACT.Relu,
-                    bias=st[("sh1", q)][:, i : i + 1], scale=st[("var1", q)][:, i : i + 1],
+                    scale=st[("rstd1", q)][:, i : i + 1], bias=gb1[:, 32 + t : 33 + t],
                 )
-
-        def v_scale(q, i0, i1):
-            t0 = QUAD * q
-            rstd1, s1, sh1, var1 = st[("rstd1", q)], st[("s1", q)], st[("sh1", q)], st[("var1", q)]
-            nc.vector.tensor_tensor(out=s1[:, i0:i1], in0=rstd1[:, i0:i1], in1=s1[:, i0:i1], op=ALU.mult)
-            nc.vector.tensor_tensor(out=var1[:, i0:i1], in0=rstd1[:, i0:i1], in1=agam1[:, t0 + i0 : t0 + i1], op=ALU.mult)
-            nc.vector.tensor_tensor(out=sh1[:, i0:i1], in0=s1[:, i0:i1], in1=gb1[:, 32 + t0 + i0 : 32 + t0 + i1], op=ALU.add)
-
-        def v_affine(q, i0, i1):
-            for i in range(i0, i1):
-                nc.vector.tensor_scalar(
-                    out=st[("z", q)][:, i, :], in0=st[("zmax", q)][:, i, :],
-                    scalar1=st[("var1", q)][:, i : i + 1], scalar2=st[("sh1", q)][:, i : i + 1], op0=ALU.mult, op1=ALU.add,
-                )
-
-        def relu_out(q, i0, i1, on_vector=True):
-            cols = slice((QUAD * q + i0) * P, (QUAD * q + i1) * P)
-            src = st[("tr_ps", q)][:, i0:i1, :].rearrange("v i n -> v (i n)")
-            if on_vector:
-                nc.vector.tensor_scalar(out=o_sb[:, cols], in0=src, scalar1=0.0, scalar2=None, op0=ALU.max)
-            else:
-                nc.scalar.activation(out=o_sb[:, cols], in_=src, func=ACT.Relu)
 
         def pe_tr(q, i0, i1, b):
             if i0 == 0:
@@ -532,28 +449,26 @@ def tile_vfe_w_kernel(tc, voxel_feats, W0, gamma0, beta0, W1_words, W1_scales, g
         p_passes(1, 2, 4, (0, 1, 2, 3))
         s_yacopy(1)
         v_max(0, 0, 2)
-        v_nm(0, 0, 4)
-        s_var(0, 0, 4)
+        v_negmean(0, 0, 4)
+        s_squares(0, 0, 4)
         v_max(0, 2, 4)
-        v_shift(0, 0, 4)
+        v_center(0, 0, 4)
         s_rstd(0, 0, 4)
-        s_scale(0, 0, 4)
         s_relu(0, 0, 4)
         a_passes(2, 1)
         a_passes(3, 0)
 
         def quad_vs(q, outs):
             for x in outs:
-                copy_out(x, 0, 4)
+                copy_out(x, 0, 4, False)
                 store(x, 0, 4)
             v_add(q, 0, 4)
             v_max(q, 0, 2)
-            v_nm(q, 0, 4)
-            s_var(q, 0, 4)
+            v_negmean(q, 0, 4)
+            s_squares(q, 0, 4)
             v_max(q, 2, 4)
-            v_shift(q, 0, 4)
+            v_center(q, 0, 4)
             s_rstd(q, 0, 4)
-            s_scale(q, 0, 4)
             s_relu(q, 0, 4)
 
         quad_vs(1, ())
@@ -584,13 +499,9 @@ def tile_vfe_w_kernel(tc, voxel_feats, W0, gamma0, beta0, W1_words, W1_scales, g
         p_passes(6, 0, 4, (0, 1, 2, 3))
         pe_tr(3, 0, 4, 7)
         pe_tr(4, 0, 4, 1)
-        quad_vs(6, ())
-        copy_out(3, 0, 4)
-        store(3, 0, 4)
+        quad_vs(6, (3, 4))
         a_passes(7, 0)
         s_yacopy(7, True)
-        copy_out(4, 0, 4)
-        store(4, 0, 4)
         open_tiles(7, 0, (6, 5, 2, 3))
         p_passes(7, 0, 2, (0, 1, 2, 3))
         p_passes(7, 2, 3, (0, 1, 2))
@@ -601,25 +512,21 @@ def tile_vfe_w_kernel(tc, voxel_feats, W0, gamma0, beta0, W1_words, W1_scales, g
         pe_tr(6, 0, 4, 1)
         q = 7
         v_add(q, 0, 2)
-        v_nm(q, 0, 1)
-        v_add_plain(q, 2, 3)
-        v_nm(q, 1, 2)
-        v_add_plain(q, 3, 4)
-        s_var(q, 0, 2)
+        v_negmean(q, 0, 1)
+        v_max(q, 0, 2)
+        v_negmean(q, 1, 2)
+        s_squares(q, 0, 2)
+        v_add(q, 2, 4, False)
+        v_center(q, 0, 2)
+        v_max(q, 2, 4)
+        v_stats_pair(q)
         copy_out(5, 0, 4, False)
         store(5, 0, 4)
-        v_shift(q, 0, 2)
-        v_max(q, 0, 2)
-        v_bn2(q)
-        v_max(q, 2, 3)
-        v_shift_bn2(q)
-        v_max(q, 3, 4)
         s_rstd(q, 0, 2)
-        s_scale(q, 0, 2)
-        s_rstd_bn2(q)
-        s_relu(q, 0, 1)
-        s_scale(q, 2, 4)
-        s_relu(q, 1, 4)
+        s_relu(q, 0, 2)
+        s_rstd_pair(q)
+        v_center_pair(q)
+        s_relu(q, 2, 4)
         copy_out(6, 0, 4)
         store(6, 0, 4)
         pe_tr(q, 0, 2, 4)

@@ -44,8 +44,9 @@ def tile_vfe_w_kernel(tc, voxel_feats, W0, gamma0, beta0, W1_words, W1_scales, g
         def bank(b, shape, dtype, name):
             return psum.tile(shape, dtype, name=name, tag="b%d" % b)
 
-        warm_bf = keep.tile([P, 512], BF16)
-        nc.vector.memset(warm_bf[:], 0.0)
+        planes = keep.tile([P, 2, C1], U8, align_bytes=64)
+        for h in range(2):
+            nc.vector.memset(planes[:, h].bitcast(I32), 0)
         zero_t = keep.tile([P, 1], F32)
         nc.vector.memset(zero_t[:], 0.0)
         eps_t = keep.tile([P, 1], F32)
@@ -54,8 +55,6 @@ def tile_vfe_w_kernel(tc, voxel_feats, W0, gamma0, beta0, W1_words, W1_scales, g
         nc.vector.memset(gb[:], 0.0)
         gb0 = keep.tile([P, 512], BF16)
         nc.vector.memset(gb0[:], 0.0)
-        planes = keep.tile([P, 2, C1], U8, align_bytes=64)
-        nc.vector.memset(planes[:].bitcast(I32), 0)
         ident_bf = keep.tile([P, P], BF16)
         make_identity(nc, ident_bf[:])
         for h in range(2):
@@ -111,9 +110,6 @@ def tile_vfe_w_kernel(tc, voxel_feats, W0, gamma0, beta0, W1_words, W1_scales, g
         a_codes = keep.tile([P, G0, NV], U32, align_bytes=64)
         a_scales = keep.tile([P, G0, NV], U8, align_bytes=64)
 
-        warm_ps = bank(7, [P, 512], F32, "warm_ps")
-        for n in range(3):
-            nc.tensor.matmul(out=warm_ps[:], lhsT=warm_bf[:, 0:P], rhs=warm_bf[:], start=True, stop=True)
         xT_ps = bank(0, [P, NM, NV], BF16, "xT_ps")
         for m in range(NM):
             nc.tensor.transpose(xT_ps[:, m, :], vox_sb[:, m, :], ident_bf[:])

@@ -423,9 +423,9 @@ def tile_vfe_w_kernel(tc, voxel_feats, W0, gamma0, beta0, W1_words, W1_scales, g
             else:
                 nc.scalar.copy(out=o_sb[:, cols], in_=src)
 
-        def store(q, i0, i1):
-            cols = slice((QUAD * q + i0) * P, (QUAD * q + i1) * P)
-            nc.sync.dma_start(out=out[:, cols], in_=o_sb[:, cols])
+        def store(t0, t1, eng):
+            cols = slice(t0 * P, t1 * P)
+            eng.dma_start(out=out[:, cols], in_=o_sb[:, cols])
 
         open_tiles(0, 0, (2, 3, 4, 5))
         open_tiles(1, 0, (6, 7))
@@ -457,7 +457,6 @@ def tile_vfe_w_kernel(tc, voxel_feats, W0, gamma0, beta0, W1_words, W1_scales, g
         def quad_vs(q, outs):
             for x in outs:
                 copy_out(x, 0, 4, False)
-                store(x, 0, 4)
             v_add(q, 0, 4)
             v_max(q, 0, 2)
             v_negmean(q, 0, 4)
@@ -495,7 +494,9 @@ def tile_vfe_w_kernel(tc, voxel_feats, W0, gamma0, beta0, W1_words, W1_scales, g
         p_passes(6, 0, 4, (0, 1, 2, 3))
         pe_tr(3, 0, 4, 7)
         pe_tr(4, 0, 4, 1)
+        store(0, 12, nc.sync)
         quad_vs(6, (3, 4))
+        store(12, 20, nc.sync)
         a_passes(7, 0)
         s_yacopy(7, True)
         open_tiles(7, 0, (6, 5, 2, 3))
@@ -517,17 +518,17 @@ def tile_vfe_w_kernel(tc, voxel_feats, W0, gamma0, beta0, W1_words, W1_scales, g
         v_max(q, 2, 4)
         v_stats_pair(q)
         copy_out(5, 0, 4, False)
-        store(5, 0, 4)
+        store(20, 24, nc.sync)
         s_rstd(q, 0, 2)
         s_relu(q, 0, 2)
         s_rstd_pair(q)
         v_center_pair(q)
         s_relu(q, 2, 4)
         copy_out(6, 0, 4)
-        store(6, 0, 4)
+        store(24, 28, nc.sync)
         pe_tr(q, 0, 2, 4)
         copy_out(q, 0, 2)
-        store(q, 0, 2)
+        store(28, 30, nc.sync)
         pe_tr2(q, 2, 4, 0)
         copy_out2(q, 2, 4, False)
-        store(q, 2, 4)
+        store(30, 32, nc.scalar)

@@ -13,24 +13,33 @@ ACT = mybir.ActivationFunctionType
 ALU = mybir.AluOpType
 
 P = 128
-NV = 128
-NM = 2
-ROWS = NV * NM
+VOXELS = 128
+POINTS = 2
+ROWS = VOXELS * POINTS
 C0 = 2048
 C1 = 4096
-G0 = C0 // 512
-EPS = 1e-3
+CODES = 4
+GROUPS = C0 // (P * CODES)
 QUAD = 4
-NQ = C1 // (QUAD * P)
+QUADS = C1 // (QUAD * P)
+EPS = 1e-3
 
-REGROUP_ON_G = ()
-LOADS = ((0, 1024, True), (0, 1024, False), (1024, 1024, False), (1024, 1024, True), (2048, 1024, False), (2048, 1024, True), (3072, 512, False), (3072, 512, True), (3584, 512, False), (3584, 256, True), (3840, 256, True))
-TR_LAG = 3
-L0_ORDER = (0, 1, 4, 2, 5, 3, 6, 7)
-S_CHAIN_FROM = 0
+LOADS = (
+    (0, 1024, True),
+    (0, 1024, False),
+    (1024, 1024, False),
+    (1024, 1024, True),
+    (2048, 1024, False),
+    (2048, 1024, True),
+    (3072, 512, False),
+    (3072, 512, True),
+    (3584, 512, False),
+    (3584, 256, True),
+    (3840, 256, True),
+)
 WORK_BUFS = 4
 
-FLOPS = 2 * ROWS * 128 * C0 + 2 * ROWS * 2 * C0 * C1
+FLOPS = 2 * ROWS * P * C0 + 2 * ROWS * 2 * C0 * C1
 
 
 def tile_vfe_w_kernel(tc, voxel_feats, W0, gamma0, beta0, W1_words, W1_scales, gamma1, beta1, out):
@@ -44,491 +53,462 @@ def tile_vfe_w_kernel(tc, voxel_feats, W0, gamma0, beta0, W1_words, W1_scales, g
         def bank(b, shape, dtype, name):
             return psum.tile(shape, dtype, name=name, tag="b%d" % b)
 
-        planes = keep.tile([P, 2, C1], U8, align_bytes=64)
+        scale_rows = keep.tile([P, 2, C1], U8, align_bytes=64)
         for h in range(2):
-            nc.vector.memset(planes[:, h].bitcast(I32), 0)
-        zero_t = keep.tile([P, 1], F32)
-        nc.vector.memset(zero_t[:], 0.0)
-        eps_t = keep.tile([P, 1], F32)
-        nc.vector.tensor_scalar(out=eps_t[:], in0=zero_t[:], scalar1=EPS, scalar2=None, op0=ALU.add)
-        gb = keep.tile([P, P], BF16)
-        nc.vector.memset(gb[:], 0.0)
-        gb0 = keep.tile([P, 512], BF16)
-        nc.vector.memset(gb0[:], 0.0)
+            nc.vector.memset(scale_rows[:, h].bitcast(I32), 0)
+        zero = keep.tile([P, 1], F32)
+        nc.vector.memset(zero[:], 0.0)
+        eps = keep.tile([P, 1], F32)
+        nc.vector.tensor_scalar(out=eps[:], in0=zero[:], scalar1=EPS, scalar2=None, op0=ALU.add)
+        affine1_rows = keep.tile([P, P], BF16)
+        nc.vector.memset(affine1_rows[:], 0.0)
+        affine0_rows = keep.tile([P, P * CODES], BF16)
+        nc.vector.memset(affine0_rows[:], 0.0)
         ident_bf = keep.tile([P, P], BF16)
         make_identity(nc, ident_bf[:])
         for h in range(2):
             for quadrant in range(4):
                 nc.gpsimd.dma_start(
-                    out=planes[32 * quadrant : 32 * quadrant + 16, h, :].bitcast(F32),
+                    out=scale_rows[32 * quadrant : 32 * quadrant + 16, h, :].bitcast(F32),
                     in_=W1_scales[4 * h : 4 * h + 4, 4 * quadrant : 4 * quadrant + 4, :].bitcast(F32),
                 )
         ident_f = keep.tile([P, P], F32)
         make_identity(nc, ident_f[:])
 
-        warm = keep.tile([P, 1], F32)
-        nc.scalar.activation(out=warm[:], in_=eps_t[:], func=ACT.Abs_reciprocal_sqrt)
-        vox_sb = keep.tile([P, NM, 128], BF16)
-        nc.sync.dma_start(out=vox_sb[:], in_=voxel_feats)
-        w0_sb = keep.tile([P, G0, 4, 128], BF16)
-        w0_view = W0.rearrange("(g p t) c -> p g t c", g=G0, p=P, t=4)
-        for g in range(G0):
-            nc.sync.dma_start(out=w0_sb[:, g], in_=w0_view[:, g])
-        nc.scalar.dma_start(out=gb[0:32, :], in_=gamma1.rearrange("(t p) -> t p", p=P))
-        nc.scalar.dma_start(out=gb[32:64, :], in_=beta1.rearrange("(t p) -> t p", p=P))
-        words = {}
-        for lo, width, top in LOADS:
-            for j in range(G0):
-                if lo == 0 and top and j == 1:
-                    nc.scalar.dma_start(out=gb0[0:4, :], in_=gamma0.rearrange("(g x) -> g x", g=G0))
-                    nc.scalar.dma_start(out=gb0[4:8, :], in_=beta0.rearrange("(g x) -> g x", g=G0))
-                g = j if top else G0 + j
-                wt = keep.tile([P, width], I32, name="w_%d_%d" % (lo, g), align_bytes=64)
+        table_load = keep.tile([P, 1], F32)
+        nc.scalar.activation(out=table_load[:], in_=eps[:], func=ACT.Abs_reciprocal_sqrt)
+        vox = keep.tile([P, POINTS, 128], BF16, align_bytes=256)
+        nc.sync.dma_start(out=vox[:], in_=voxel_feats)
+        w0 = keep.tile([P, GROUPS, CODES, 128], BF16, align_bytes=256)
+        w0_rows = W0.rearrange("(g p t) c -> p g t c", g=GROUPS, p=P, t=CODES)
+        for g in range(GROUPS):
+            nc.sync.dma_start(out=w0[:, g], in_=w0_rows[:, g])
+        nc.scalar.dma_start(out=affine1_rows[0:32, :], in_=gamma1.rearrange("(t p) -> t p", p=P))
+        nc.scalar.dma_start(out=affine1_rows[32:64, :], in_=beta1.rearrange("(t p) -> t p", p=P))
+        words = keep.tile([P, 2 * GROUPS * C1], I32, align_bytes=256)
+        word_columns = {}
+        column = 0
+        for lo, width, meets_p in LOADS:
+            for j in range(GROUPS):
+                if lo == 0 and meets_p and j == 1:
+                    nc.scalar.dma_start(out=affine0_rows[0:4, :], in_=gamma0.rearrange("(g x) -> g x", g=GROUPS))
+                    nc.scalar.dma_start(out=affine0_rows[4:8, :], in_=beta0.rearrange("(g x) -> g x", g=GROUPS))
+                half = 0 if meets_p else 1
                 nc.sync.dma_start(
-                    out=wt[:],
-                    in_=W1_words[g].rearrange("p n t -> p (n t)")[:, 4 * lo : 4 * (lo + width)].bitcast(I32),
+                    out=words[:, column : column + width],
+                    in_=W1_words[GROUPS * half + j].rearrange("p n t -> p (n t)")[:, CODES * lo : CODES * (lo + width)].bitcast(I32),
                 )
-                for c in range(0, width, P):
-                    words[(g, lo + c)] = (wt, c)
+                for n in range(0, width, P):
+                    word_columns[(half, j, lo + n)] = column + n
+                column += width
 
         xT = keep.tile([P, ROWS], BF16)
-        w0T = keep.tile([P, G0, 4, P], BF16)
-        gb1 = keep.tile([P, 64], F32)
-        sgn1 = keep.tile([P, 32], F32)
-        agam1 = keep.tile([P, 32], F32)
-        st0 = keep.tile([P, G0, 4, 6], F32)
-        mv0 = keep.tile([P, G0, 4, 2], F32)
-        rstd0 = keep.tile([P, G0, 4], F32)
-        s0 = keep.tile([P, G0, 4], F32)
-        ms0 = keep.tile([P, G0, 4], F32)
-        sh0 = keep.tile([P, G0, 4], F32)
-        p_bf = keep.tile([P, G0, 4, ROWS], BF16)
-        grp = keep.tile([P, G0, ROWS, 4], BF16, align_bytes=64)
-        agr = keep.tile([P, G0, NV, 4], BF16, align_bytes=64)
-        p_codes = keep.tile([P, G0, ROWS], U32, align_bytes=64)
-        p_scales = keep.tile([P, G0, ROWS], U8, align_bytes=64)
-        a_codes = keep.tile([P, G0, NV], U32, align_bytes=64)
-        a_scales = keep.tile([P, G0, NV], U8, align_bytes=64)
+        w0T = keep.tile([P, GROUPS, CODES, P], BF16)
+        affine1 = keep.tile([P, 64], F32)
+        gamma1_sign = keep.tile([P, 32], F32)
+        gamma1_abs = keep.tile([P, 32], F32)
+        rstd0 = keep.tile([P, GROUPS, CODES], F32)
+        scale0 = keep.tile([P, GROUPS, CODES], F32)
+        mean_scale0 = keep.tile([P, GROUPS, CODES], F32)
+        shift0 = keep.tile([P, GROUPS, CODES], F32)
+        p_bf = keep.tile([P, GROUPS, CODES, ROWS], BF16)
+        p_packed = keep.tile([P, GROUPS, ROWS, CODES], BF16, align_bytes=64)
+        a_packed = keep.tile([P, GROUPS, VOXELS, CODES], BF16, align_bytes=64)
+        p_codes = keep.tile([P, GROUPS, ROWS], U32, align_bytes=64)
+        p_scales = keep.tile([P, GROUPS, ROWS], U8, align_bytes=64)
+        a_codes = keep.tile([P, GROUPS, VOXELS], U32, align_bytes=64)
+        a_scales = keep.tile([P, GROUPS, VOXELS], U8, align_bytes=64)
 
-        xT_ps = bank(0, [P, NM, NV], BF16, "xT_ps")
-        for m in range(NM):
-            nc.tensor.transpose(xT_ps[:, m, :], vox_sb[:, m, :], ident_bf[:])
+        xT_ps = bank(0, [P, POINTS, VOXELS], BF16, "xT_ps")
+        for m in range(POINTS):
+            nc.tensor.transpose(xT_ps[:, m, :], vox[:, m, :], ident_bf[:])
         nc.vector.tensor_copy(out=xT[:], in_=xT_ps[:].rearrange("c m v -> c (m v)"))
 
-        y0_bank = ((2, 3), (4, 5), (6, 7), (1, 0))
+        y0_banks = ((2, 3), (4, 5), (6, 7), (1, 0))
         y0 = {}
-        def w0_transposes(g):
-            blocks = 5 if g == G0 - 1 else 4
-            wT_ps = bank(4 + g, [P, blocks, P], BF16, "wT_ps")
-            for t in range(4):
-                nc.tensor.transpose(wT_ps[:, t, :], w0_sb[:, g, t, :], ident_bf[:])
-            if g == G0 - 1:
-                nc.tensor.transpose(wT_ps[:, 4, :], gb[:], ident_bf[:])
+
+        def turn_w0(g):
+            last = g == GROUPS - 1
+            wT_ps = bank(4 + g, [P, CODES + 1 if last else CODES, P], BF16, "wT_ps")
+            for t in range(CODES):
+                nc.tensor.transpose(wT_ps[:, t, :], w0[:, g, t, :], ident_bf[:])
+            if last:
+                nc.tensor.transpose(wT_ps[:, CODES, :], affine1_rows[:], ident_bf[:])
             if g == 0:
                 nc.vector.tensor_copy(out=w0T[:, g, 0:2], in_=wT_ps[:, 0:2, :])
                 nc.scalar.copy(out=w0T[:, g, 2:4], in_=wT_ps[:, 2:4, :])
             else:
-                nc.scalar.copy(out=w0T[:, g], in_=wT_ps[:, 0:4, :])
-            if g == G0 - 1:
-                nc.scalar.copy(out=gb1[:], in_=wT_ps[:, 4, 0:64])
-                nc.scalar.activation(out=sgn1[:], in_=wT_ps[:, 4, 0:32], func=ACT.Sign)
-                nc.scalar.activation(out=agam1[:], in_=wT_ps[:, 4, 0:32], func=ACT.Abs)
+                nc.scalar.copy(out=w0T[:, g], in_=wT_ps[:, 0:CODES, :])
+            if last:
+                nc.scalar.copy(out=affine1[:], in_=wT_ps[:, CODES, 0:64])
+                nc.scalar.activation(out=gamma1_sign[:], in_=wT_ps[:, CODES, 0:32], func=ACT.Sign)
+                nc.scalar.activation(out=gamma1_abs[:], in_=wT_ps[:, CODES, 0:32], func=ACT.Abs)
 
-        def l0_matmuls(g):
-            for half in range(2):
-                yt = bank(y0_bank[g][half], [P, 2, ROWS], F32, "y0")
-                y0[(g, half)] = yt
+        def multiply0(g):
+            for pair in range(2):
+                y0[(g, pair)] = bank(y0_banks[g][pair], [P, 2, ROWS], F32, "y0")
                 for u in range(2):
-                    nc.tensor.matmul(out=yt[:, u, :], lhsT=w0T[:, g, 2 * half + u, :], rhs=xT[:], start=True, stop=True)
+                    nc.tensor.matmul(
+                        out=y0[(g, pair)][:, u, :], lhsT=w0T[:, g, 2 * pair + u, :], rhs=xT[:], start=True, stop=True
+                    )
 
-        gb0T = keep.tile([P, 2, G0, 4], BF16)
-        g0_sb = gb0T[:, 0]
-        b0_sb = gb0T[:, 1]
+        affine0 = keep.tile([P, 2, GROUPS, CODES], BF16)
+        gamma0_t = affine0[:, 0]
+        beta0_t = affine0[:, 1]
 
-        def gb0_transposes():
-            gT_ps = bank(1, [P, 4, P], BF16, "gT_ps")
-            rows = gb0[:].rearrange("r (p t) -> r t p", t=4)
-            for t in range(4):
-                nc.tensor.transpose(gT_ps[:, t, :], rows[:, t, :], ident_bf[:])
-            nc.scalar.copy(out=gb0T[:].rearrange("p s g t -> p (s g) t"), in_=gT_ps[:, :, 0:8].rearrange("p t r -> p r t"))
-
-        for step in L0_ORDER:
-            if step == 7:
-                gb0_transposes()
-            if step < G0:
-                w0_transposes(step)
-            else:
-                l0_matmuls(step - G0)
-
-        def l0_stat(g, t):
-            nc.vector.bn_stats(out=st0[:, g, t, :], in_=y0[(g, t // 2)][:, t % 2, :])
-
-        def l0_aggr(g):
-            for t in range(4):
-                nc.vector.bn_aggr(out=mv0[:, g, t, :], in_=st0[:, g, t, :])
-            nc.scalar.activation(out=rstd0[:, g, :], in_=mv0[:, g, :, 1], func=ACT.Abs_reciprocal_sqrt, bias=eps_t[:])
-
-        def l0_small(g, step):
-            if step == 0:
-                nc.vector.tensor_tensor(out=s0[:, g, :], in0=rstd0[:, g, :], in1=g0_sb[:, g, :], op=ALU.mult)
-            elif step == 1:
-                nc.vector.tensor_tensor(out=ms0[:, g, :], in0=mv0[:, g, :, 0], in1=s0[:, g, :], op=ALU.mult)
-            else:
-                nc.vector.tensor_tensor(out=sh0[:, g, :], in0=b0_sb[:, g, :], in1=ms0[:, g, :], op=ALU.subtract)
-
-        def l0_act(g):
-            for t in range(4):
-                nc.scalar.activation(
-                    out=p_bf[:, g, t, :], in_=y0[(g, t // 2)][:, t % 2, :], func=ACT.Relu,
-                    bias=sh0[:, g, t : t + 1], scale=s0[:, g, t : t + 1],
-                )
-
-        def l0_regroup(g):
-            if g in REGROUP_ON_G:
-                nc.gpsimd.tensor_scalar(
-                    out=grp[:, g], in0=p_bf[:, g].rearrange("p t r -> p r t"),
-                    scalar1=1.0, scalar2=0.0, op0=ALU.mult, op1=ALU.add,
-                )
-            else:
-                nc.vector.tensor_copy(
-                    out=grp[:, g].rearrange("p (c i) t -> p c t i", i=4),
-                    in_=p_bf[:, g].rearrange("p t (c i) -> p c t i", i=4),
-                )
-
-        def l0_quant_p(g):
-            nc.vector.quantize_mx(
-                out=p_codes[:, g, :].bitcast(FP8X4), scales=p_scales[:, g, :],
-                in_=grp[:, g].rearrange("p r t -> p (r t)"),
+        def turn_affine0():
+            ps = bank(1, [P, CODES, P], BF16, "affine0_ps")
+            rows = affine0_rows[:].rearrange("r (p t) -> r t p", t=CODES)
+            for t in range(CODES):
+                nc.tensor.transpose(ps[:, t, :], rows[:, t, :], ident_bf[:])
+            nc.scalar.copy(
+                out=affine0[:].rearrange("p s g t -> p (s g) t"), in_=ps[:, :, 0 : 2 * GROUPS].rearrange("p t r -> p r t")
             )
 
-        def l0_max(g):
-            nc.vector.tensor_tensor(out=agr[:, g], in0=grp[:, g, 0:NV, :], in1=grp[:, g, NV:ROWS, :], op=ALU.max)
+        turn_w0(0)
+        turn_w0(1)
+        multiply0(0)
+        turn_w0(2)
+        multiply0(1)
+        turn_w0(3)
+        multiply0(2)
+        turn_affine0()
+        multiply0(3)
 
-        def l0_quant_a(g):
-            nc.vector.quantize_mx(
-                out=a_codes[:, g, :].bitcast(FP8X4), scales=a_scales[:, g, :],
-                in_=agr[:, g].rearrange("p r t -> p (r t)"),
-            )
-
-        def l0_act1(g, t):
+        def relu0(g, t):
             nc.scalar.activation(
                 out=p_bf[:, g, t, :], in_=y0[(g, t // 2)][:, t % 2, :], func=ACT.Relu,
-                bias=sh0[:, g, t : t + 1], scale=s0[:, g, t : t + 1],
+                bias=shift0[:, g, t : t + 1], scale=scale0[:, g, t : t + 1],
             )
 
-        def l0_ag(g):
-            for t in range(4):
-                nc.vector.bn_aggr(out=mv0[:, g, t, :], in_=st0[:, g, t, :])
+        def pack_p(g):
+            nc.vector.tensor_copy(
+                out=p_packed[:, g].rearrange("p (c i) t -> p c t i", i=4),
+                in_=p_bf[:, g].rearrange("p t (c i) -> p c t i", i=4),
+            )
 
-        def l0_rstd(g):
-            nc.scalar.activation(out=rstd0[:, g, :], in_=mv0[:, g, :, 1], func=ACT.Abs_reciprocal_sqrt, bias=eps_t[:])
+        def quantise_p(g):
+            nc.vector.quantize_mx(
+                out=p_codes[:, g, :].bitcast(FP8X4), scales=p_scales[:, g, :], in_=p_packed[:, g].rearrange("p r t -> p (r t)")
+            )
 
-        nm0 = keep.tile([P, G0, 4], F32)
-        st0p = keep.tile([P, 2 * G0, 2, 3], F32)
+        def max_points(g):
+            nc.vector.tensor_tensor(
+                out=a_packed[:, g], in0=p_packed[:, g, 0:VOXELS, :], in1=p_packed[:, g, VOXELS:ROWS, :], op=ALU.max
+            )
 
-        def l0_stat2(g, h):
-            nc.vector.bn_stats(out=st0p[:, 2 * g + h].rearrange("p u s -> p (u s)"), in_=y0[(g, h)][:].rearrange("p u r -> p r u"))
+        def quantise_a(g):
+            nc.vector.quantize_mx(
+                out=a_codes[:, g, :].bitcast(FP8X4), scales=a_scales[:, g, :], in_=a_packed[:, g].rearrange("p r t -> p (r t)")
+            )
 
-        def l0_rstd2(g):
+        neg_shift0 = keep.tile([P, GROUPS, CODES], F32)
+        stats0 = keep.tile([P, 2 * GROUPS, 2, 3], F32)
+
+        def stats_of(g, pair):
+            nc.vector.bn_stats(
+                out=stats0[:, 2 * g + pair].rearrange("p u s -> p (u s)"), in_=y0[(g, pair)][:].rearrange("p u r -> p r u")
+            )
+
+        def rstd_of(g):
             nc.scalar.activation(
-                out=rstd0[:, g : g + 2, :].rearrange("p g (h u) -> p (g h) u", u=2), in_=st0p[:, 2 * g : 2 * g + 4, :, 2],
-                func=ACT.Abs_reciprocal_sqrt, scale=1.0 / ROWS, bias=eps_t[:],
+                out=rstd0[:, g : g + 2, :].rearrange("p g (h u) -> p (g h) u", u=2), in_=stats0[:, 2 * g : 2 * g + 4, :, 2],
+                func=ACT.Abs_reciprocal_sqrt, scale=1.0 / ROWS, bias=eps[:],
             )
 
-        def l0_nm2(g):
-            pair = slice(g, g + 2)
-            nc.vector.tensor_tensor(out=nm0[:, pair, :].rearrange("p g (h u) -> p (g h) u", u=2), in0=st0p[:, 2 * g : 2 * g + 4, :, 1], in1=g0_sb[:, pair, :].rearrange("p g (h u) -> p (g h) u", u=2), op=ALU.mult)
+        def mean_gamma(g):
+            both = slice(g, g + 2)
+            nc.vector.tensor_tensor(
+                out=neg_shift0[:, both, :].rearrange("p g (h u) -> p (g h) u", u=2), in0=stats0[:, 2 * g : 2 * g + 4, :, 1],
+                in1=gamma0_t[:, both, :].rearrange("p g (h u) -> p (g h) u", u=2), op=ALU.mult,
+            )
 
-        def l0_small2(g):
-            pair = slice(g, g + 2)
-            nc.vector.tensor_tensor(out=ms0[:, pair, :], in0=nm0[:, pair, :], in1=rstd0[:, pair, :], op=ALU.mult)
-            nc.vector.tensor_tensor(out=s0[:, pair, :], in0=rstd0[:, pair, :], in1=g0_sb[:, pair, :], op=ALU.mult)
-            nc.vector.tensor_tensor(out=sh0[:, pair, :], in0=b0_sb[:, pair, :], in1=ms0[:, pair, :], op=ALU.subtract)
+        def scale_and_shift(g):
+            both = slice(g, g + 2)
+            nc.vector.tensor_tensor(out=mean_scale0[:, both, :], in0=neg_shift0[:, both, :], in1=rstd0[:, both, :], op=ALU.mult)
+            nc.vector.tensor_tensor(out=scale0[:, both, :], in0=rstd0[:, both, :], in1=gamma0_t[:, both, :], op=ALU.mult)
+            nc.vector.tensor_tensor(out=shift0[:, both, :], in0=beta0_t[:, both, :], in1=mean_scale0[:, both, :], op=ALU.subtract)
 
         for g in (0, 1):
-            for h in (0, 1):
-                l0_stat2(g, h)
-        l0_rstd2(0)
-        l0_stat2(2, 0)
-        l0_nm2(0)
-        l0_small2(0)
-        l0_act(0)
-        l0_act1(1, 0)
-        l0_stat2(2, 1)
-        l0_stat2(3, 0)
-        l0_stat2(3, 1)
-        l0_rstd2(2)
-        for t in range(1, 4):
-            l0_act1(1, t)
-        l0_nm2(2)
-        l0_regroup(0)
-        l0_small2(2)
-        l0_quant_p(0)
-        l0_act(2)
-        l0_act(3)
-        l0_max(0)
-        l0_regroup(1)
-        l0_quant_a(0)
-        l0_quant_p(1)
-        l0_max(1)
-        l0_regroup(2)
-        l0_quant_a(1)
-        l0_quant_p(2)
-        l0_regroup(3)
-        l0_max(2)
-        l0_quant_p(3)
-        l0_max(3)
-        l0_quant_a(2)
-        l0_quant_a(3)
+            for pair in range(2):
+                stats_of(g, pair)
+        rstd_of(0)
+        stats_of(2, 0)
+        mean_gamma(0)
+        scale_and_shift(0)
+        for t in range(CODES):
+            relu0(0, t)
+        relu0(1, 0)
+        stats_of(2, 1)
+        stats_of(3, 0)
+        stats_of(3, 1)
+        rstd_of(2)
+        for t in range(1, CODES):
+            relu0(1, t)
+        mean_gamma(2)
+        pack_p(0)
+        scale_and_shift(2)
+        quantise_p(0)
+        for g in (2, 3):
+            for t in range(CODES):
+                relu0(g, t)
+        max_points(0)
+        for g in (1, 2):
+            pack_p(g)
+            quantise_a(g - 1)
+            quantise_p(g)
+            if g == 1:
+                max_points(g)
+        pack_p(3)
+        max_points(2)
+        quantise_p(3)
+        max_points(3)
+        quantise_a(2)
+        quantise_a(3)
 
-        o_sb = keep.tile([P, C1], F32)
+        out_sb = keep.tile([P, C1], F32)
         st = {}
 
-        def mx_pass(acc, g, n0, first, last):
-            j = g % G0
-            top = g < G0
-            wt, c = words[(g, n0)]
-            if top:
-                rhs, rhs_scale = p_codes[:, j, :], p_scales[:, j, :]
-            else:
-                rhs, rhs_scale = a_codes[:, j, :], a_scales[:, j, :]
+        def pass_mx(acc, half, j, n0, first, last):
+            column = word_columns[(half, j, n0)]
+            codes, scales = (p_codes, p_scales) if half == 0 else (a_codes, a_scales)
             nc.tensor.matmul_mx(
                 out=acc,
-                lhsT=wt[:, c : c + P].bitcast(FP8X4),
-                lhsT_scale=planes[4 * j : P, 0 if top else 1, n0 : n0 + P],
-                rhs=rhs.bitcast(FP8X4),
-                rhs_scale=rhs_scale,
+                lhsT=words[:, column : column + P].bitcast(FP8X4),
+                lhsT_scale=scale_rows[4 * j : P, half, n0 : n0 + P],
+                rhs=codes[:, j, :].bitcast(FP8X4),
+                rhs_scale=scales[:, j, :],
                 start=first, stop=last,
             )
 
-        def open_tiles(q, i0, banks):
-            for k, b in enumerate(banks):
-                st[("acc", q, i0 + k)] = bank(b, [P, NM, NV], F32, "yp_ps")[:]
+        def open_sums(q, i0, banks):
+            for i, b in enumerate(banks):
+                st[("sum_p", q, i0 + i)] = bank(b, [P, POINTS, VOXELS], F32, "sum_p")[:]
 
-        def p_passes(q, i0, i1, js):
-            for j in js:
+        def passes_p(q, i0, i1, groups):
+            for j in groups:
                 for i in range(i0, i1):
-                    mx_pass(st[("acc", q, i)].rearrange("p m v -> p (m v)"), j, (QUAD * q + i) * P, j == 0, j == G0 - 1)
+                    acc = st[("sum_p", q, i)].rearrange("p m v -> p (m v)")
+                    pass_mx(acc, 0, j, (QUAD * q + i) * P, j == 0, j == GROUPS - 1)
 
-        def p_tiles(q, i0, i1):
-            for i in range(i0, i1):
-                p_passes(q, i, i + 1, (0, 1, 2, 3))
-
-        def a_passes(q, b):
-            ya_ps = bank(b, [P, QUAD, NV], F32, "ya_ps")
-            st[("ya_ps", q)] = ya_ps
+        def passes_p_by_tile(q):
             for i in range(QUAD):
-                for j in range(G0):
-                    mx_pass(ya_ps[:, i, :], G0 + j, (QUAD * q + i) * P, j == 0, j == G0 - 1)
+                passes_p(q, i, i + 1, range(GROUPS))
 
-        def s_yacopy(q, on_vector=False):
-            st[("ya", q)] = work.tile([P, QUAD, NV], F32, name="ya_sb")
-            st[("y", q)] = work.tile([P, QUAD, NM, NV], F32, name="y")
-            st[("bn2", q)] = work.tile([P, 2, 3], F32, name="bn2")
-            for n in ("sum1", "nm1", "m2", "rstd1"):
-                st[(n, q)] = work.tile([P, QUAD], F32, name=n)
-            st[("zmax", q)] = work.tile([P, QUAD, NV], F32, name="zmax")
-            st[("z", q)] = work.tile([P, QUAD, NV], F32, name="z")
+        def passes_a(q, b):
+            sum_a = bank(b, [P, QUAD, VOXELS], F32, "sum_a")
+            st[("sum_a", q)] = sum_a
+            for i in range(QUAD):
+                for j in range(GROUPS):
+                    pass_mx(sum_a[:, i, :], 1, j, (QUAD * q + i) * P, j == 0, j == GROUPS - 1)
+
+        def take_a(q, on_vector):
+            st[("a", q)] = work.tile([P, QUAD, VOXELS], F32, name="a")
+            st[("y", q)] = work.tile([P, QUAD, POINTS, VOXELS], F32, name="y")
+            st[("pair_stats", q)] = work.tile([P, 2, 3], F32, name="pair_stats")
+            for name in ("sum", "neg_mean", "squares", "rstd"):
+                st[(name, q)] = work.tile([P, QUAD], F32, name=name)
+            st[("w", q)] = work.tile([P, QUAD, VOXELS], F32, name="w")
+            st[("z", q)] = work.tile([P, QUAD, VOXELS], F32, name="z")
             for i in range(QUAD):
                 t = QUAD * q + i
+                dst, src, sign = st[("a", q)][:, i, :], st[("sum_a", q)][:, i, :], gamma1_sign[:, t : t + 1]
                 if on_vector:
-                    nc.vector.tensor_scalar(out=st[("ya", q)][:, i, :], in0=st[("ya_ps", q)][:, i, :], scalar1=sgn1[:, t : t + 1], scalar2=None, op0=ALU.mult)
+                    nc.vector.tensor_scalar(out=dst, in0=src, scalar1=sign, scalar2=None, op0=ALU.mult)
                 else:
-                    nc.scalar.activation(out=st[("ya", q)][:, i, :], in_=st[("ya_ps", q)][:, i, :], func=ACT.Copy, scale=sgn1[:, t : t + 1])
+                    nc.scalar.activation(out=dst, in_=src, func=ACT.Copy, scale=sign)
 
-        def v_add(q, i0, i1, with_sum=True):
+        def add(q, i0, i1, with_sum=True):
             for i in range(i0, i1):
                 t = QUAD * q + i
                 nc.vector.scalar_tensor_tensor(
-                    out=st[("y", q)][:, i], in0=st[("acc", q, i)], scalar=sgn1[:, t : t + 1],
-                    in1=st[("ya", q)][:, i : i + 1, :].to_broadcast([P, NM, NV]),
-                    op0=ALU.mult, op1=ALU.add, accum_out=st[("sum1", q)][:, i : i + 1] if with_sum else None,
+                    out=st[("y", q)][:, i], in0=st[("sum_p", q, i)], scalar=gamma1_sign[:, t : t + 1],
+                    in1=st[("a", q)][:, i : i + 1, :].to_broadcast([P, POINTS, VOXELS]),
+                    op0=ALU.mult, op1=ALU.add, accum_out=st[("sum", q)][:, i : i + 1] if with_sum else None,
                 )
 
-        def v_negmean(q, i0, i1):
-            nc.vector.tensor_scalar(out=st[("nm1", q)][:, i0:i1], in0=st[("sum1", q)][:, i0:i1], scalar1=-1.0 / ROWS, scalar2=None, op0=ALU.mult)
+        def neg_mean(q, i0, i1):
+            nc.vector.tensor_scalar(
+                out=st[("neg_mean", q)][:, i0:i1], in0=st[("sum", q)][:, i0:i1], scalar1=-1.0 / ROWS, scalar2=None, op0=ALU.mult
+            )
 
-        def v_max(q, i0, i1):
+        def max_rows(q, i0, i1):
             y = st[("y", q)]
-            nc.vector.tensor_tensor(out=st[("zmax", q)][:, i0:i1], in0=y[:, i0:i1, 0, :], in1=y[:, i0:i1, 1, :], op=ALU.max)
+            nc.vector.tensor_tensor(out=st[("w", q)][:, i0:i1], in0=y[:, i0:i1, 0, :], in1=y[:, i0:i1, 1, :], op=ALU.max)
 
-        def v_center(q, i0, i1):
+        def centre(q, i0, i1):
             for i in range(i0, i1):
                 t = QUAD * q + i
                 nc.vector.tensor_scalar(
-                    out=st[("zmax", q)][:, i, :], in0=st[("zmax", q)][:, i, :],
-                    scalar1=st[("nm1", q)][:, i : i + 1], scalar2=agam1[:, t : t + 1], op0=ALU.add, op1=ALU.mult,
+                    out=st[("w", q)][:, i, :], in0=st[("w", q)][:, i, :],
+                    scalar1=st[("neg_mean", q)][:, i : i + 1], scalar2=gamma1_abs[:, t : t + 1], op0=ALU.add, op1=ALU.mult,
                 )
 
-        def s_squares(q, i0, i1):
+        def squares(q, i0, i1):
             for i in range(i0, i1):
-                junk = work.tile([P, ROWS], BF16, name="junk")
+                unused = work.tile([P, ROWS], BF16, name="unused")
                 nc.scalar.activation(
-                    out=junk[:], in_=st[("y", q)][:, i].rearrange("p m v -> p (m v)"), func=ACT.Square,
-                    bias=st[("nm1", q)][:, i : i + 1], accum_out=st[("m2", q)][:, i : i + 1],
+                    out=unused[:], in_=st[("y", q)][:, i].rearrange("p m v -> p (m v)"), func=ACT.Square,
+                    bias=st[("neg_mean", q)][:, i : i + 1], accum_out=st[("squares", q)][:, i : i + 1],
                 )
 
-        def s_rstd(q, i0, i1):
+        def rstd(q, i0, i1):
             nc.scalar.activation(
-                out=st[("rstd1", q)][:, i0:i1], in_=st[("m2", q)][:, i0:i1], func=ACT.Abs_reciprocal_sqrt, scale=1.0 / ROWS, bias=eps_t[:]
+                out=st[("rstd", q)][:, i0:i1], in_=st[("squares", q)][:, i0:i1],
+                func=ACT.Abs_reciprocal_sqrt, scale=1.0 / ROWS, bias=eps[:],
             )
 
-        def v_stats_pair(q):
+        def pair_stats(q):
             nc.vector.bn_stats(
-                out=st[("bn2", q)][:].rearrange("p u s -> p (u s)"),
+                out=st[("pair_stats", q)][:].rearrange("p u s -> p (u s)"),
                 in_=st[("y", q)][:, 2:4].rearrange("p u m v -> p (m v) u"),
             )
 
-        def s_rstd_pair(q):
+        def pair_rstd(q):
             nc.scalar.activation(
-                out=st[("rstd1", q)][:, 2:4], in_=st[("bn2", q)][:, :, 2], func=ACT.Abs_reciprocal_sqrt, scale=1.0 / ROWS, bias=eps_t[:]
+                out=st[("rstd", q)][:, 2:4], in_=st[("pair_stats", q)][:, :, 2],
+                func=ACT.Abs_reciprocal_sqrt, scale=1.0 / ROWS, bias=eps[:],
             )
 
-        def v_center_pair(q):
+        def pair_centre(q):
             for u in range(2):
                 t = QUAD * q + 2 + u
                 nc.vector.tensor_scalar(
-                    out=st[("zmax", q)][:, 2 + u, :], in0=st[("zmax", q)][:, 2 + u, :],
-                    scalar1=st[("bn2", q)][:, u, 1:2], scalar2=agam1[:, t : t + 1], op0=ALU.subtract, op1=ALU.mult,
+                    out=st[("w", q)][:, 2 + u, :], in0=st[("w", q)][:, 2 + u, :],
+                    scalar1=st[("pair_stats", q)][:, u, 1:2], scalar2=gamma1_abs[:, t : t + 1], op0=ALU.subtract, op1=ALU.mult,
                 )
 
-        def s_relu(q, i0, i1):
+        def relu1(q, i0, i1):
             for i in range(i0, i1):
                 t = QUAD * q + i
                 nc.scalar.activation(
-                    out=st[("z", q)][:, i, :], in_=st[("zmax", q)][:, i, :], func=ACT.Relu,
-                    scale=st[("rstd1", q)][:, i : i + 1], bias=gb1[:, 32 + t : 33 + t],
+                    out=st[("z", q)][:, i, :], in_=st[("w", q)][:, i, :], func=ACT.Relu,
+                    scale=st[("rstd", q)][:, i : i + 1], bias=affine1[:, 32 + t : 33 + t],
                 )
 
-        def pe_tr(q, i0, i1, b):
-            if i0 == 0:
-                st[("tr_ps", q)] = bank(b, [P, QUAD, P], F32, "tr_ps")
+        def turn(q, i0, i1, b):
+            z_ps = bank(b, [P, QUAD, P], F32, "z_ps")
             for i in range(i0, i1):
-                nc.tensor.transpose(st[("tr_ps", q)][:, i, :], st[("z", q)][:, i, :], ident_f[:])
+                nc.tensor.transpose(z_ps[:, i, :], st[("z", q)][:, i, :], ident_f[:])
+            return z_ps
 
-        def pe_tr2(q, i0, i1, b):
-            st[("tr2_ps", q)] = bank(b, [P, QUAD, P], F32, "tr_ps")
-            for i in range(i0, i1):
-                nc.tensor.transpose(st[("tr2_ps", q)][:, i, :], st[("z", q)][:, i, :], ident_f[:])
-
-        def copy_out2(q, i0, i1, on_vector):
-            cols = slice((QUAD * q + i0) * P, (QUAD * q + i1) * P)
-            nc.scalar.copy(out=o_sb[:, cols], in_=st[("tr2_ps", q)][:, i0:i1, :].rearrange("v i n -> v (i n)"))
-
-        def copy_out(q, i0, i1, on_vector=True):
-            cols = slice((QUAD * q + i0) * P, (QUAD * q + i1) * P)
-            src = st[("tr_ps", q)][:, i0:i1, :].rearrange("v i n -> v (i n)")
+        def take_out(z_ps, q, i0, i1, on_vector):
+            dst = out_sb[:, (QUAD * q + i0) * P : (QUAD * q + i1) * P]
+            src = z_ps[:, i0:i1, :].rearrange("v i n -> v (i n)")
             if on_vector:
-                nc.vector.tensor_copy(out=o_sb[:, cols], in_=src)
+                nc.vector.tensor_copy(out=dst, in_=src)
             else:
-                nc.scalar.copy(out=o_sb[:, cols], in_=src)
+                nc.scalar.copy(out=dst, in_=src)
 
-        def store(t0, t1, eng):
-            cols = slice(t0 * P, t1 * P)
-            eng.dma_start(out=out[:, cols], in_=o_sb[:, cols])
+        def store(engine, t0, t1):
+            engine.dma_start(out=out[:, t0 * P : t1 * P], in_=out_sb[:, t0 * P : t1 * P])
 
-        open_tiles(0, 0, (2, 3, 4, 5))
-        open_tiles(1, 0, (6, 7))
-        p_passes(0, 0, 2, (0,))
-        p_passes(0, 2, 4, (0,))
-        p_passes(0, 0, 4, (1,))
-        p_passes(1, 0, 2, (0, 1))
-        p_passes(0, 0, 4, (2,))
-        p_passes(1, 0, 2, (2,))
-        p_passes(0, 0, 4, (3,))
-        p_passes(1, 0, 2, (3,))
-        a_passes(0, 1)
-        a_passes(1, 0)
-        s_yacopy(0)
-        v_add(0, 0, 4)
-        open_tiles(1, 2, (2, 3))
-        p_passes(1, 2, 4, (0, 1, 2, 3))
-        s_yacopy(1)
-        v_max(0, 0, 2)
-        v_negmean(0, 0, 4)
-        s_squares(0, 0, 4)
-        v_max(0, 2, 4)
-        v_center(0, 0, 4)
-        s_rstd(0, 0, 4)
-        s_relu(0, 0, 4)
-        a_passes(2, 1)
-        a_passes(3, 0)
+        def norm_and_relu(q):
+            max_rows(q, 0, 2)
+            neg_mean(q, 0, QUAD)
+            squares(q, 0, QUAD)
+            max_rows(q, 2, QUAD)
+            centre(q, 0, QUAD)
+            rstd(q, 0, QUAD)
+            relu1(q, 0, QUAD)
 
-        def quad_vs(q, outs):
-            for x in outs:
-                copy_out(x, 0, 4, False)
-            v_add(q, 0, 4)
-            v_max(q, 0, 2)
-            v_negmean(q, 0, 4)
-            s_squares(q, 0, 4)
-            v_max(q, 2, 4)
-            v_center(q, 0, 4)
-            s_rstd(q, 0, 4)
-            s_relu(q, 0, 4)
+        open_sums(0, 0, (2, 3, 4, 5))
+        open_sums(1, 0, (6, 7))
+        passes_p(0, 0, 2, (0,))
+        passes_p(0, 2, 4, (0,))
+        passes_p(0, 0, 4, (1,))
+        passes_p(1, 0, 2, (0, 1))
+        for j in (2, 3):
+            passes_p(0, 0, 4, (j,))
+            passes_p(1, 0, 2, (j,))
+        passes_a(0, 1)
+        passes_a(1, 0)
+        take_a(0, False)
+        add(0, 0, QUAD)
+        open_sums(1, 2, (2, 3))
+        passes_p(1, 2, 4, range(GROUPS))
+        take_a(1, False)
+        norm_and_relu(0)
+        passes_a(2, 1)
+        passes_a(3, 0)
+        add(1, 0, QUAD)
+        norm_and_relu(1)
 
-        quad_vs(1, ())
-        s_yacopy(2, True)
-        s_yacopy(3, True)
-        open_tiles(2, 0, (2, 3, 4, 5))
-        p_passes(2, 0, 4, (0, 1, 2, 3))
-        quad_vs(2, ())
-        open_tiles(3, 0, (6, 2, 3, 4))
-        p_tiles(3, 0, 4)
-        pe_tr(0, 0, 4, 7)
-        pe_tr(1, 0, 4, 5)
-        quad_vs(3, (0, 1))
-        a_passes(4, 1)
-        a_passes(5, 0)
-        s_yacopy(4, True)
-        s_yacopy(5, True)
-        pe_tr(2, 0, 4, 7)
-        open_tiles(4, 0, (2, 3, 4, 5))
-        p_passes(4, 0, 4, (0, 1, 2, 3))
-        quad_vs(4, (2,))
-        open_tiles(5, 0, (6, 2, 3, 4))
-        p_tiles(5, 0, 4)
-        a_passes(6, 1)
-        quad_vs(5, ())
-        s_yacopy(6, True)
-        open_tiles(6, 0, (5, 2, 3, 4))
-        p_passes(6, 0, 4, (0, 1, 2, 3))
-        pe_tr(3, 0, 4, 7)
-        pe_tr(4, 0, 4, 1)
-        store(0, 12, nc.sync)
-        quad_vs(6, (3, 4))
-        store(12, 20, nc.sync)
-        a_passes(7, 0)
-        s_yacopy(7, True)
-        open_tiles(7, 0, (6, 5, 2, 3))
-        p_passes(7, 0, 2, (0, 1, 2, 3))
-        p_passes(7, 2, 3, (0, 1, 2))
-        p_passes(7, 3, 4, (0, 1))
-        p_passes(7, 2, 3, (3,))
-        p_passes(7, 3, 4, (2, 3))
-        pe_tr(5, 0, 4, 7)
-        pe_tr(6, 0, 4, 1)
-        q = 7
-        v_add(q, 0, 2)
-        v_negmean(q, 0, 1)
-        v_max(q, 0, 2)
-        v_negmean(q, 1, 2)
-        s_squares(q, 0, 2)
-        v_add(q, 2, 4, False)
-        v_center(q, 0, 2)
-        v_max(q, 2, 4)
-        v_stats_pair(q)
-        copy_out(5, 0, 4, False)
-        store(20, 24, nc.sync)
-        s_rstd(q, 0, 2)
-        s_relu(q, 0, 2)
-        s_rstd_pair(q)
-        v_center_pair(q)
-        s_relu(q, 2, 4)
-        copy_out(6, 0, 4)
-        store(24, 28, nc.sync)
-        pe_tr(q, 0, 2, 4)
-        copy_out(q, 0, 2)
-        store(28, 30, nc.sync)
-        pe_tr2(q, 2, 4, 0)
-        copy_out2(q, 2, 4, False)
-        store(30, 32, nc.scalar)
+        take_a(2, True)
+        take_a(3, True)
+        open_sums(2, 0, (2, 3, 4, 5))
+        passes_p(2, 0, 4, range(GROUPS))
+        add(2, 0, QUAD)
+        norm_and_relu(2)
+        open_sums(3, 0, (6, 2, 3, 4))
+        passes_p_by_tile(3)
+        turned0 = turn(0, 0, QUAD, 7)
+        turned1 = turn(1, 0, QUAD, 5)
+        take_out(turned0, 0, 0, QUAD, False)
+        take_out(turned1, 1, 0, QUAD, False)
+        add(3, 0, QUAD)
+        norm_and_relu(3)
+
+        passes_a(4, 1)
+        passes_a(5, 0)
+        take_a(4, True)
+        take_a(5, True)
+        turned2 = turn(2, 0, QUAD, 7)
+        open_sums(4, 0, (2, 3, 4, 5))
+        passes_p(4, 0, 4, range(GROUPS))
+        take_out(turned2, 2, 0, QUAD, False)
+        add(4, 0, QUAD)
+        norm_and_relu(4)
+        open_sums(5, 0, (6, 2, 3, 4))
+        passes_p_by_tile(5)
+        passes_a(6, 1)
+        add(5, 0, QUAD)
+        norm_and_relu(5)
+
+        take_a(6, True)
+        open_sums(6, 0, (5, 2, 3, 4))
+        passes_p(6, 0, 4, range(GROUPS))
+        turned3 = turn(3, 0, QUAD, 7)
+        turned4 = turn(4, 0, QUAD, 1)
+        store(nc.sync, 0, 3 * QUAD)
+        take_out(turned3, 3, 0, QUAD, False)
+        take_out(turned4, 4, 0, QUAD, False)
+        add(6, 0, QUAD)
+        norm_and_relu(6)
+        store(nc.sync, 3 * QUAD, 5 * QUAD)
+
+        q = QUADS - 1
+        passes_a(q, 0)
+        take_a(q, True)
+        open_sums(q, 0, (6, 5, 2, 3))
+        passes_p(q, 0, 2, range(GROUPS))
+        passes_p(q, 2, 3, (0, 1, 2))
+        passes_p(q, 3, 4, (0, 1))
+        passes_p(q, 2, 3, (3,))
+        passes_p(q, 3, 4, (2, 3))
+        turned5 = turn(5, 0, QUAD, 7)
+        turned6 = turn(6, 0, QUAD, 1)
+        add(q, 0, 2)
+        neg_mean(q, 0, 1)
+        max_rows(q, 0, 2)
+        neg_mean(q, 1, 2)
+        squares(q, 0, 2)
+        add(q, 2, 4, with_sum=False)
+        centre(q, 0, 2)
+        max_rows(q, 2, 4)
+        pair_stats(q)
+        take_out(turned5, 5, 0, QUAD, False)
+        store(nc.sync, 5 * QUAD, 6 * QUAD)
+        rstd(q, 0, 2)
+        relu1(q, 0, 2)
+        pair_rstd(q)
+        pair_centre(q)
+        relu1(q, 2, 4)
+        take_out(turned6, 6, 0, QUAD, True)
+        store(nc.sync, 6 * QUAD, 7 * QUAD)
+        first_pair = turn(q, 0, 2, 4)
+        take_out(first_pair, q, 0, 2, True)
+        store(nc.sync, 7 * QUAD, 7 * QUAD + 2)
+        last_pair = turn(q, 2, 4, 0)
+        take_out(last_pair, q, 2, 4, False)
+        store(nc.scalar, 7 * QUAD + 2, 8 * QUAD)

from contextlib import ExitStack

import concourse.mybir as mybir
from concourse.masks import make_identity

F32 = mybir.dt.float32
BF16 = mybir.dt.bfloat16
I32 = mybir.dt.int32
U32 = mybir.dt.uint32
U8 = mybir.dt.uint8
FP8X4 = mybir.dt.float8_e4m3fn_x4
ACT = mybir.ActivationFunctionType
ALU = mybir.AluOpType

P = 128
VOXELS = 128
POINTS = 2
ROWS = VOXELS * POINTS
C0 = 2048
C1 = 4096
CODES = 4
GROUPS = C0 // (P * CODES)
QUAD = 4
QUADS = C1 // (QUAD * P)
EPS = 1e-3

LOADS = (
    (0, 1024, True),
    (0, 1024, False),
    (1024, 1024, False),
    (1024, 1024, True),
    (2048, 1024, False),
    (2048, 1024, True),
    (3072, 512, False),
    (3072, 512, True),
    (3584, 512, False),
    (3584, 256, True),
    (3840, 256, True),
)
WORK_BUFS = 4

FLOPS = 2 * ROWS * P * C0 + 2 * ROWS * 2 * C0 * C1


def tile_vfe_w_kernel(tc, voxel_feats, W0, gamma0, beta0, W1_words, W1_scales, gamma1, beta1, out):
    nc = tc.nc
    with ExitStack() as ctx:
        ctx.enter_context(tc.manual_schedule())
        keep = ctx.enter_context(tc.tile_pool(name="keep", bufs=1))
        work = ctx.enter_context(tc.tile_pool(name="work", bufs=WORK_BUFS))
        psum = ctx.enter_context(tc.psum_pool(name="psum", bufs=1))

        def bank(b, shape, dtype, name):
            return psum.tile(shape, dtype, name=name, tag="b%d" % b)

        scale_rows = keep.tile([P, 2, C1], U8, align_bytes=64)
        for h in range(2):
            nc.vector.memset(scale_rows[:, h].bitcast(I32), 0)
        zero = keep.tile([P, 1], F32)
        nc.vector.memset(zero[:], 0.0)
        eps = keep.tile([P, 1], F32)
        nc.vector.tensor_scalar(out=eps[:], in0=zero[:], scalar1=EPS, scalar2=None, op0=ALU.add)
        affine1_rows = keep.tile([P, P], BF16)
        nc.vector.memset(affine1_rows[:], 0.0)
        affine0_rows = keep.tile([P, P * CODES], BF16)
        nc.vector.memset(affine0_rows[:], 0.0)
        ident_bf = keep.tile([P, P], BF16)
        make_identity(nc, ident_bf[:])
        for h in range(2):
            for quadrant in range(4):
                nc.gpsimd.dma_start(
                    out=scale_rows[32 * quadrant : 32 * quadrant + 16, h, :].bitcast(F32),
                    in_=W1_scales[4 * h : 4 * h + 4, 4 * quadrant : 4 * quadrant + 4, :].bitcast(F32),
                )
        ident_f = keep.tile([P, P], F32)
        make_identity(nc, ident_f[:])

        table_load = keep.tile([P, 1], F32)
        nc.scalar.activation(out=table_load[:], in_=eps[:], func=ACT.Abs_reciprocal_sqrt)
        vox = keep.tile([P, POINTS, 128], BF16, align_bytes=256)
        nc.sync.dma_start(out=vox[:], in_=voxel_feats)
        w0 = keep.tile([P, GROUPS, CODES, 128], BF16, align_bytes=256)
        w0_rows = W0.rearrange("(g p t) c -> p g t c", g=GROUPS, p=P, t=CODES)
        for g in range(GROUPS):
            nc.sync.dma_start(out=w0[:, g], in_=w0_rows[:, g])
        nc.scalar.dma_start(out=affine1_rows[0:32, :], in_=gamma1.rearrange("(t p) -> t p", p=P))
        nc.scalar.dma_start(out=affine1_rows[32:64, :], in_=beta1.rearrange("(t p) -> t p", p=P))
        words = keep.tile([P, 2 * GROUPS * C1], I32, align_bytes=256)
        word_columns = {}
        column = 0
        for lo, width, meets_p in LOADS:
            for j in range(GROUPS):
                if lo == 0 and meets_p and j == 1:
                    nc.scalar.dma_start(out=affine0_rows[0:4, :], in_=gamma0.rearrange("(g x) -> g x", g=GROUPS))
                    nc.scalar.dma_start(out=affine0_rows[4:8, :], in_=beta0.rearrange("(g x) -> g x", g=GROUPS))
                half = 0 if meets_p else 1
                nc.sync.dma_start(
                    out=words[:, column : column + width],
                    in_=W1_words[GROUPS * half + j].rearrange("p n t -> p (n t)")[:, CODES * lo : CODES * (lo + width)].bitcast(I32),
                )
                for n in range(0, width, P):
                    word_columns[(half, j, lo + n)] = column + n
                column += width

        xT = keep.tile([P, ROWS], BF16)
        w0T = keep.tile([P, GROUPS, CODES, P], BF16)
        affine1 = keep.tile([P, 64], F32)
        gamma1_sign = keep.tile([P, 32], F32)
        gamma1_abs = keep.tile([P, 32], F32)
        rstd0 = keep.tile([P, GROUPS, CODES], F32)
        scale0 = keep.tile([P, GROUPS, CODES], F32)
        mean_scale0 = keep.tile([P, GROUPS, CODES], F32)
        shift0 = keep.tile([P, GROUPS, CODES], F32)
        p_bf = keep.tile([P, GROUPS, CODES, ROWS], BF16)
        p_packed = keep.tile([P, GROUPS, ROWS, CODES], BF16, align_bytes=64)
        a_packed = keep.tile([P, GROUPS, VOXELS, CODES], BF16, align_bytes=64)
        p_codes = keep.tile([P, GROUPS, ROWS], U32, align_bytes=64)
        p_scales = keep.tile([P, GROUPS, ROWS], U8, align_bytes=64)
        a_codes = keep.tile([P, GROUPS, VOXELS], U32, align_bytes=64)
        a_scales = keep.tile([P, GROUPS, VOXELS], U8, align_bytes=64)

        xT_ps = bank(0, [P, POINTS, VOXELS], BF16, "xT_ps")
        for m in range(POINTS):
            nc.tensor.transpose(xT_ps[:, m, :], vox[:, m, :], ident_bf[:])
        nc.vector.tensor_copy(out=xT[:], in_=xT_ps[:].rearrange("c m v -> c (m v)"))

        y0_banks = ((2, 3), (4, 5), (6, 7), (1, 0))
        y0 = {}

        def turn_w0(g):
            last = g == GROUPS - 1
            wT_ps = bank(4 + g, [P, CODES + 1 if last else CODES, P], BF16, "wT_ps")
            for t in range(CODES):
                nc.tensor.transpose(wT_ps[:, t, :], w0[:, g, t, :], ident_bf[:])
            if last:
                nc.tensor.transpose(wT_ps[:, CODES, :], affine1_rows[:], ident_bf[:])
            if g == 0:
                nc.vector.tensor_copy(out=w0T[:, g, 0:2], in_=wT_ps[:, 0:2, :])
                nc.scalar.copy(out=w0T[:, g, 2:4], in_=wT_ps[:, 2:4, :])
            else:
                nc.scalar.copy(out=w0T[:, g], in_=wT_ps[:, 0:CODES, :])
            if last:
                nc.scalar.copy(out=affine1[:], in_=wT_ps[:, CODES, 0:64])
                nc.scalar.activation(out=gamma1_sign[:], in_=wT_ps[:, CODES, 0:32], func=ACT.Sign)
                nc.scalar.activation(out=gamma1_abs[:], in_=wT_ps[:, CODES, 0:32], func=ACT.Abs)

        def multiply0(g):
            for pair in range(2):
                y0[(g, pair)] = bank(y0_banks[g][pair], [P, 2, ROWS], F32, "y0")
                for u in range(2):
                    nc.tensor.matmul(
                        out=y0[(g, pair)][:, u, :], lhsT=w0T[:, g, 2 * pair + u, :], rhs=xT[:], start=True, stop=True
                    )

        affine0 = keep.tile([P, 2, GROUPS, CODES], BF16)
        gamma0_t = affine0[:, 0]
        beta0_t = affine0[:, 1]

        def turn_affine0():
            ps = bank(1, [P, CODES, P], BF16, "affine0_ps")
            rows = affine0_rows[:].rearrange("r (p t) -> r t p", t=CODES)
            for t in range(CODES):
                nc.tensor.transpose(ps[:, t, :], rows[:, t, :], ident_bf[:])
            nc.scalar.copy(
                out=affine0[:].rearrange("p s g t -> p (s g) t"), in_=ps[:, :, 0 : 2 * GROUPS].rearrange("p t r -> p r t")
            )

        turn_w0(0)
        turn_w0(1)
        multiply0(0)
        turn_w0(2)
        multiply0(1)
        turn_w0(3)
        multiply0(2)
        turn_affine0()
        multiply0(3)

        def relu0(g, t):
            nc.scalar.activation(
                out=p_bf[:, g, t, :], in_=y0[(g, t // 2)][:, t % 2, :], func=ACT.Relu,
                bias=shift0[:, g, t : t + 1], scale=scale0[:, g, t : t + 1],
            )

        def pack_p(g):
            nc.vector.tensor_copy(
                out=p_packed[:, g].rearrange("p (c i) t -> p c t i", i=4),
                in_=p_bf[:, g].rearrange("p t (c i) -> p c t i", i=4),
            )

        def quantise_p(g):
            nc.vector.quantize_mx(
                out=p_codes[:, g, :].bitcast(FP8X4), scales=p_scales[:, g, :], in_=p_packed[:, g].rearrange("p r t -> p (r t)")
            )

        def max_points(g):
            nc.vector.tensor_tensor(
                out=a_packed[:, g], in0=p_packed[:, g, 0:VOXELS, :], in1=p_packed[:, g, VOXELS:ROWS, :], op=ALU.max
            )

        def quantise_a(g):
            nc.vector.quantize_mx(
                out=a_codes[:, g, :].bitcast(FP8X4), scales=a_scales[:, g, :], in_=a_packed[:, g].rearrange("p r t -> p (r t)")
            )

        neg_shift0 = keep.tile([P, GROUPS, CODES], F32)
        stats0 = keep.tile([P, 2 * GROUPS, 2, 3], F32)

        def stats_of(g, pair):
            nc.vector.bn_stats(
                out=stats0[:, 2 * g + pair].rearrange("p u s -> p (u s)"), in_=y0[(g, pair)][:].rearrange("p u r -> p r u")
            )

        def rstd_of(g):
            nc.scalar.activation(
                out=rstd0[:, g : g + 2, :].rearrange("p g (h u) -> p (g h) u", u=2), in_=stats0[:, 2 * g : 2 * g + 4, :, 2],
                func=ACT.Abs_reciprocal_sqrt, scale=1.0 / ROWS, bias=eps[:],
            )

        def mean_gamma(g):
            both = slice(g, g + 2)
            nc.vector.tensor_tensor(
                out=neg_shift0[:, both, :].rearrange("p g (h u) -> p (g h) u", u=2), in0=stats0[:, 2 * g : 2 * g + 4, :, 1],
                in1=gamma0_t[:, both, :].rearrange("p g (h u) -> p (g h) u", u=2), op=ALU.mult,
            )

        def scale_and_shift(g):
            both = slice(g, g + 2)
            nc.vector.tensor_tensor(out=mean_scale0[:, both, :], in0=neg_shift0[:, both, :], in1=rstd0[:, both, :], op=ALU.mult)
            nc.vector.tensor_tensor(out=scale0[:, both, :], in0=rstd0[:, both, :], in1=gamma0_t[:, both, :], op=ALU.mult)
            nc.vector.tensor_tensor(out=shift0[:, both, :], in0=beta0_t[:, both, :], in1=mean_scale0[:, both, :], op=ALU.subtract)

        for g in (0, 1):
            for pair in range(2):
                stats_of(g, pair)
        rstd_of(0)
        stats_of(2, 0)
        mean_gamma(0)
        scale_and_shift(0)
        for t in range(CODES):
            relu0(0, t)
        relu0(1, 0)
        stats_of(2, 1)
        stats_of(3, 0)
        stats_of(3, 1)
        rstd_of(2)
        for t in range(1, CODES):
            relu0(1, t)
        mean_gamma(2)
        pack_p(0)
        scale_and_shift(2)
        quantise_p(0)
        for g in (2, 3):
            for t in range(CODES):
                relu0(g, t)
        max_points(0)
        for g in (1, 2):
            pack_p(g)
            quantise_a(g - 1)
            quantise_p(g)
            if g == 1:
                max_points(g)
        pack_p(3)
        max_points(2)
        quantise_p(3)
        max_points(3)
        quantise_a(2)
        quantise_a(3)

        out_sb = keep.tile([P, C1], F32)
        st = {}

        def pass_mx(acc, half, j, n0, first, last):
            column = word_columns[(half, j, n0)]
            codes, scales = (p_codes, p_scales) if half == 0 else (a_codes, a_scales)
            nc.tensor.matmul_mx(
                out=acc,
                lhsT=words[:, column : column + P].bitcast(FP8X4),
                lhsT_scale=scale_rows[4 * j : P, half, n0 : n0 + P],
                rhs=codes[:, j, :].bitcast(FP8X4),
                rhs_scale=scales[:, j, :],
                start=first, stop=last,
            )

        def open_sums(q, i0, banks):
            for i, b in enumerate(banks):
                st[("sum_p", q, i0 + i)] = bank(b, [P, POINTS, VOXELS], F32, "sum_p")[:]

        def passes_p(q, i0, i1, groups):
            for j in groups:
                for i in range(i0, i1):
                    acc = st[("sum_p", q, i)].rearrange("p m v -> p (m v)")
                    pass_mx(acc, 0, j, (QUAD * q + i) * P, j == 0, j == GROUPS - 1)

        def passes_p_by_tile(q):
            for i in range(QUAD):
                passes_p(q, i, i + 1, range(GROUPS))

        def passes_a(q, b):
            sum_a = bank(b, [P, QUAD, VOXELS], F32, "sum_a")
            st[("sum_a", q)] = sum_a
            for i in range(QUAD):
                for j in range(GROUPS):
                    pass_mx(sum_a[:, i, :], 1, j, (QUAD * q + i) * P, j == 0, j == GROUPS - 1)

        def take_a(q, on_vector):
            st[("a", q)] = work.tile([P, QUAD, VOXELS], F32, name="a")
            st[("y", q)] = work.tile([P, QUAD, POINTS, VOXELS], F32, name="y")
            st[("pair_stats", q)] = work.tile([P, 2, 3], F32, name="pair_stats")
            for name in ("sum", "neg_mean", "squares", "rstd"):
                st[(name, q)] = work.tile([P, QUAD], F32, name=name)
            st[("w", q)] = work.tile([P, QUAD, VOXELS], F32, name="w")
            st[("z", q)] = work.tile([P, QUAD, VOXELS], F32, name="z")
            for i in range(QUAD):
                t = QUAD * q + i
                dst, src, sign = st[("a", q)][:, i, :], st[("sum_a", q)][:, i, :], gamma1_sign[:, t : t + 1]
                if on_vector:
                    nc.vector.tensor_scalar(out=dst, in0=src, scalar1=sign, scalar2=None, op0=ALU.mult)
                else:
                    nc.scalar.activation(out=dst, in_=src, func=ACT.Copy, scale=sign)

        def add(q, i0, i1, with_sum=True):
            for i in range(i0, i1):
                t = QUAD * q + i
                nc.vector.scalar_tensor_tensor(
                    out=st[("y", q)][:, i], in0=st[("sum_p", q, i)], scalar=gamma1_sign[:, t : t + 1],
                    in1=st[("a", q)][:, i : i + 1, :].to_broadcast([P, POINTS, VOXELS]),
                    op0=ALU.mult, op1=ALU.add, accum_out=st[("sum", q)][:, i : i + 1] if with_sum else None,
                )

        def neg_mean(q, i0, i1):
            nc.vector.tensor_scalar(
                out=st[("neg_mean", q)][:, i0:i1], in0=st[("sum", q)][:, i0:i1], scalar1=-1.0 / ROWS, scalar2=None, op0=ALU.mult
            )

        def max_rows(q, i0, i1):
            y = st[("y", q)]
            nc.vector.tensor_tensor(out=st[("w", q)][:, i0:i1], in0=y[:, i0:i1, 0, :], in1=y[:, i0:i1, 1, :], op=ALU.max)

        def centre(q, i0, i1):
            for i in range(i0, i1):
                t = QUAD * q + i
                nc.vector.tensor_scalar(
                    out=st[("w", q)][:, i, :], in0=st[("w", q)][:, i, :],
                    scalar1=st[("neg_mean", q)][:, i : i + 1], scalar2=gamma1_abs[:, t : t + 1], op0=ALU.add, op1=ALU.mult,
                )

        def squares(q, i0, i1):
            for i in range(i0, i1):
                unused = work.tile([P, ROWS], BF16, name="unused")
                nc.scalar.activation(
                    out=unused[:], in_=st[("y", q)][:, i].rearrange("p m v -> p (m v)"), func=ACT.Square,
                    bias=st[("neg_mean", q)][:, i : i + 1], accum_out=st[("squares", q)][:, i : i + 1],
                )

        def rstd(q, i0, i1):
            nc.scalar.activation(
                out=st[("rstd", q)][:, i0:i1], in_=st[("squares", q)][:, i0:i1],
                func=ACT.Abs_reciprocal_sqrt, scale=1.0 / ROWS, bias=eps[:],
            )

        def pair_stats(q):
            nc.vector.bn_stats(
                out=st[("pair_stats", q)][:].rearrange("p u s -> p (u s)"),
                in_=st[("y", q)][:, 2:4].rearrange("p u m v -> p (m v) u"),
            )

        def pair_rstd(q):
            nc.scalar.activation(
                out=st[("rstd", q)][:, 2:4], in_=st[("pair_stats", q)][:, :, 2],
                func=ACT.Abs_reciprocal_sqrt, scale=1.0 / ROWS, bias=eps[:],
            )

        def pair_centre(q):
            for u in range(2):
                t = QUAD * q + 2 + u
                nc.vector.tensor_scalar(
                    out=st[("w", q)][:, 2 + u, :], in0=st[("w", q)][:, 2 + u, :],
                    scalar1=st[("pair_stats", q)][:, u, 1:2], scalar2=gamma1_abs[:, t : t + 1], op0=ALU.subtract, op1=ALU.mult,
                )

        def relu1(q, i0, i1):
            for i in range(i0, i1):
                t = QUAD * q + i
                nc.scalar.activation(
                    out=st[("z", q)][:, i, :], in_=st[("w", q)][:, i, :], func=ACT.Relu,
                    scale=st[("rstd", q)][:, i : i + 1], bias=affine1[:, 32 + t : 33 + t],
                )

        def turn(q, i0, i1, b):
            z_ps = bank(b, [P, QUAD, P], F32, "z_ps")
            for i in range(i0, i1):
                nc.tensor.transpose(z_ps[:, i, :], st[("z", q)][:, i, :], ident_f[:])
            return z_ps

        def take_out(z_ps, q, i0, i1, on_vector):
            dst = out_sb[:, (QUAD * q + i0) * P : (QUAD * q + i1) * P]
            src = z_ps[:, i0:i1, :].rearrange("v i n -> v (i n)")
            if on_vector:
                nc.vector.tensor_copy(out=dst, in_=src)
            else:
                nc.scalar.copy(out=dst, in_=src)

        def store(engine, t0, t1):
            engine.dma_start(out=out[:, t0 * P : t1 * P], in_=out_sb[:, t0 * P : t1 * P])

        def norm_and_relu(q):
            max_rows(q, 0, 2)
            neg_mean(q, 0, QUAD)
            squares(q, 0, QUAD)
            max_rows(q, 2, QUAD)
            centre(q, 0, QUAD)
            rstd(q, 0, QUAD)
            relu1(q, 0, QUAD)

        open_sums(0, 0, (2, 3, 4, 5))
        open_sums(1, 0, (6, 7))
        passes_p(0, 0, 2, (0,))
        passes_p(0, 2, 4, (0,))
        passes_p(0, 0, 4, (1,))
        passes_p(1, 0, 2, (0, 1))
        for j in (2, 3):
            passes_p(0, 0, 4, (j,))
            passes_p(1, 0, 2, (j,))
        passes_a(0, 1)
        passes_a(1, 0)
        take_a(0, False)
        add(0, 0, QUAD)
        open_sums(1, 2, (2, 3))
        passes_p(1, 2, 4, range(GROUPS))
        take_a(1, False)
        norm_and_relu(0)
        passes_a(2, 1)
        passes_a(3, 0)
        add(1, 0, QUAD)
        norm_and_relu(1)

        take_a(2, True)
        take_a(3, True)
        open_sums(2, 0, (2, 3, 4, 5))
        passes_p(2, 0, 4, range(GROUPS))
        add(2, 0, QUAD)
        norm_and_relu(2)
        open_sums(3, 0, (6, 2, 3, 4))
        passes_p_by_tile(3)
        turned0 = turn(0, 0, QUAD, 7)
        turned1 = turn(1, 0, QUAD, 5)
        take_out(turned0, 0, 0, QUAD, False)
        take_out(turned1, 1, 0, QUAD, False)
        add(3, 0, QUAD)
        norm_and_relu(3)

        passes_a(4, 1)
        passes_a(5, 0)
        take_a(4, True)
        take_a(5, True)
        turned2 = turn(2, 0, QUAD, 7)
        open_sums(4, 0, (2, 3, 4, 5))
        passes_p(4, 0, 4, range(GROUPS))
        take_out(turned2, 2, 0, QUAD, False)
        add(4, 0, QUAD)
        norm_and_relu(4)
        open_sums(5, 0, (6, 2, 3, 4))
        passes_p_by_tile(5)
        passes_a(6, 1)
        add(5, 0, QUAD)
        norm_and_relu(5)

        take_a(6, True)
        open_sums(6, 0, (5, 2, 3, 4))
        passes_p(6, 0, 4, range(GROUPS))
        turned3 = turn(3, 0, QUAD, 7)
        turned4 = turn(4, 0, QUAD, 1)
        store(nc.sync, 0, 3 * QUAD)
        take_out(turned3, 3, 0, QUAD, False)
        take_out(turned4, 4, 0, QUAD, False)
        add(6, 0, QUAD)
        norm_and_relu(6)
        store(nc.sync, 3 * QUAD, 5 * QUAD)

        q = QUADS - 1
        passes_a(q, 0)
        take_a(q, True)
        open_sums(q, 0, (6, 5, 2, 3))
        passes_p(q, 0, 2, range(GROUPS))
        passes_p(q, 2, 3, (0, 1, 2))
        passes_p(q, 3, 4, (0, 1))
        passes_p(q, 2, 3, (3,))
        passes_p(q, 3, 4, (2, 3))
        turned5 = turn(5, 0, QUAD, 7)
        turned6 = turn(6, 0, QUAD, 1)
        add(q, 0, 2)
        neg_mean(q, 0, 1)
        max_rows(q, 0, 2)
        neg_mean(q, 1, 2)
        squares(q, 0, 2)
        add(q, 2, 4, with_sum=False)
        centre(q, 0, 2)
        max_rows(q, 2, 4)
        pair_stats(q)
        take_out(turned5, 5, 0, QUAD, False)
        store(nc.sync, 5 * QUAD, 6 * QUAD)
        rstd(q, 0, 2)
        relu1(q, 0, 2)
        pair_rstd(q)
        pair_centre(q)
        relu1(q, 2, 4)
        take_out(turned6, 6, 0, QUAD, True)
        store(nc.sync, 6 * QUAD, 7 * QUAD)
        first_pair = turn(q, 0, 2, 4)
        take_out(first_pair, q, 0, 2, True)
        store(nc.sync, 7 * QUAD, 7 * QUAD + 2)
        last_pair = turn(q, 2, 4, 0)
        take_out(last_pair, q, 2, 4, False)
        store(nc.scalar, 7 * QUAD + 2, 8 * QUAD)
